import numpy as np
import ml_dtypes


def mxq(x, axis, fmt="e4m3"):
    dtype, down = {"e4m3": (ml_dtypes.float8_e4m3fn, 7), "e5m2": (ml_dtypes.float8_e5m2, 14)}[fmt]
    v = np.moveaxis(np.asarray(x, np.float32).astype(ml_dtypes.bfloat16).astype(np.float64), axis, -1)
    blocks = v.reshape(v.shape[:-1] + (-1, 32))
    amax = np.abs(blocks).max(-1, keepdims=True)
    byte = np.maximum(np.where(amax > 0, np.frexp(amax)[1] - 1 + 127, 0) - down, 1)
    scale = np.exp2(byte - 127.0)
    codes = (blocks / scale).astype(np.float32).astype(dtype).astype(np.float64)
    return np.moveaxis((codes * scale).reshape(v.shape), -1, axis)


WIDE = False


def mx_kscale(k):
    if not WIDE:
        return np.ones(k)
    levels = np.array([10, -10, 5, -5, 0])
    a = np.random.permutation(np.resize(levels, k // 512 * 4)).reshape(k // 512, 4)
    idx = np.arange(k)
    return np.exp2(a[idx // 512, idx % 128 // 32])


BF16 = ml_dtypes.bfloat16


def bf(x):
    return np.asarray(x, np.float32).astype(BF16)


def f64(x):
    return np.asarray(x).astype(np.float64)


E2M1 = np.array([0.0, 0.5, 1.0, 1.5, 2.0, 3.0, 4.0, 6.0, -0.0, -0.5, -1.0, -1.5, -2.0, -3.0, -4.0, -6.0])


def pack_weight(w, fmt):
    k, n = w.shape
    w = f64(bf(w)).reshape(k // 32, 32, n)
    amax = np.abs(w).max(1)
    if fmt == "e4m3":
        byte = np.frexp(amax)[1] - 1 + 127 - 7
    else:
        mant, ex = np.frexp(amax / 6.0)
        byte = np.where(mant > 0.5, ex, ex - 1) + 127
    byte = np.clip(np.where(amax > 0, byte, 1), 1, 254)
    scaled = (w * np.exp2(127.0 - byte)[:, None, :]).reshape(k, n).astype(np.float32)
    by_word = np.ascontiguousarray(scaled.reshape(k // 512, 128, 4, n).transpose(0, 1, 3, 2))
    if fmt == "e4m3":
        words = by_word.astype(ml_dtypes.float8_e4m3fn).view(np.uint8)
    else:
        c = by_word.astype(ml_dtypes.float4_e2m1fn).view(np.uint8) & 0xF
        words = c[..., 0::2] | (c[..., 1::2] << 4)
    return np.ascontiguousarray(words), np.ascontiguousarray(byte.astype(np.uint8).reshape(k // 512, 16, n))


def unpack_weight(words, scales, fmt):
    g, p, n, _ = words.shape
    if fmt == "e4m3":
        vals = np.ascontiguousarray(words).view(ml_dtypes.float8_e4m3fn).astype(np.float64)
    else:
        nib = np.empty((g, p, n, 4), np.uint8)
        nib[..., 0::2] = words & 0xF
        nib[..., 1::2] = words >> 4
        vals = E2M1[nib]
    vals = vals * np.repeat(np.exp2(scales.astype(np.float64) - 127.0), 8, axis=1)[..., None]
    return vals.transpose(0, 1, 3, 2).reshape(g * 512, n)

def pack4(w):
    words, scales = pack_weight(w, "e2m1")
    return words.reshape(words.shape[0], 128, -1), scales


def unpack4(words, scales):
    return unpack_weight(words.reshape(words.shape[0], 128, -1, 2), scales, "e2m1")


B, N, D, H, HD, S, DO = 1, 1536, 1024, 16, 64, 11, 1024
E = H * HD
D4 = [0.4829629131445341, 0.8365163037378079, 0.2241438680420134, -0.1294095225512604]
T = len(D4)


def elu1(u):
    return np.where(u > 0.0, u, np.exp(np.minimum(u, 0.0)) - 1.0) + 1.0


def softplus(u):
    return np.log(1.0 + np.exp(u))


def shifted(t, o):
    if o == 0:
        return t
    return np.concatenate([np.zeros((B, H, o, HD)), t[:, :, :N - o, :]], axis=2)


def setup_inputs():
    s = mx_kscale(D)
    lg = np.random.standard_normal((B, H, N, S)) * 1.4
    g = np.exp(lg - lg.max(-1, keepdims=True))
    x = bf(np.random.standard_normal((B, N, D)) * s)
    w = np.random.standard_normal((3 * E, D)) * 0.6 / np.sqrt(D) / s
    words, scales = pack4(w.T)
    return {"x": x,
            "W_qkv_words": words,
            "W_qkv_scales": scales,
            "b_qkv": bf(np.random.standard_normal(3 * E) * 0.1),
            "gains": bf(g / g.sum(-1, keepdims=True)),
            "pos_bias": bf(np.random.standard_normal((S * T, H)) * 0.5),
            "identity_bypass": bf(-1.0 + 0.5 * np.random.standard_normal(H))}


def reference(x, W_qkv_words, W_qkv_scales, b_qkv, gains, pos_bias, identity_bypass):
    qkv = (mxq(f64(x), 2, "e4m3") @ unpack4(W_qkv_words, W_qkv_scales)) + f64(b_qkv)
    q, k, v = [t.reshape(B, N, H, HD).transpose(0, 2, 1, 3) for t in np.split(qkv, 3, axis=-1)]
    g, pb = f64(gains), f64(pos_bias)
    acc = np.zeros((B, H, N, HD))
    z = np.zeros((B, H, N, 1))
    tap = 0
    for j in range(S):
        d = 1 << j
        g_j = g[..., j][..., None]
        for tau, c in enumerate(D4):
            o = d * tau
            bias = pb[tap].reshape(1, H, 1, 1)
            tap += 1
            if o != 0 and o >= N:
                continue
            k_s, v_s = shifted(k, o), shifted(v, o)
            feat = elu1(np.sum(q * k_s, -1, keepdims=True) + bias)
            acc = acc + (g_j * c) * feat * v_s
            z = z + g_j * abs(c) * feat
    p = softplus(f64(identity_bypass)).reshape(1, H, 1, 1)
    local = elu1(np.sum(q * k, -1, keepdims=True))
    acc = acc + p * local * v
    z = z + p * local
    res = acc / (z + 1e-06)
    return res.transpose(0, 2, 1, 3).reshape(B, N, E)

@@ -1,0 +1,426 @@
+import concourse.mybir as mybir
+from concourse.masks import make_identity
+
+F32 = mybir.dt.float32
+BF16 = mybir.dt.bfloat16
+I32 = mybir.dt.int32
+U32 = mybir.dt.uint32
+U8 = mybir.dt.uint8
+FP8X4 = mybir.dt.float8_e4m3fn_x4
+FP4X4 = mybir.dt.float4_e2m1fn_x4
+ALU = mybir.AluOpType
+ACT = mybir.ActivationFunctionType
+AXIS = mybir.AxisListType
+
+P = 128
+TOKENS = 1536
+D_IN = 1024
+HEADS = 16
+HEAD_DIM = 64
+WIDTH = HEADS * HEAD_DIM
+SECTIONS = 3
+SCALES = 11
+TAUS = 4
+D4 = [0.4829629131445341, 0.8365163037378079, 0.2241438680420134, -0.1294095225512604]
+
+PACK = 4
+K_PASS = P * PACK
+PASSES = D_IN // K_PASS
+BLOCK = 512
+BLOCKS = TOKENS // BLOCK
+TILES = TOKENS // P
+TILES_PER_BLOCK = BLOCK // P
+
+LOW = P // HEADS
+HIGH = HEAD_DIM // LOW
+CHUNKS = SECTIONS * HIGH
+PAD = P
+
+OFFSETS = sorted(set(tau << j for j in range(SCALES) for tau in range(TAUS) if (tau << j) < TOKENS))
+SLOTS = len(OFFSETS)
+assert OFFSETS[0] == 0 and OFFSETS[1] == 1
+assert all(OFFSETS[2 * i] == 1 << i for i in range(1, 11))
+assert all(OFFSETS[2 * i + 1] == 3 << (i - 1) for i in range(1, 10))
+GROUP = 4
+GROUPS = (SLOTS + GROUP - 1) // GROUP
+
+ENTRY_RUNS = [(0, 11, 0, 0), (12, 10, 1, 1), (22, 10, 0, 2), (32, 1, 0, 1), (33, 9, 0, 3)]
+LOCAL = 11
+HERE = 12
+EVEN = 10
+ODD_FIRST = HERE + 2 * EVEN
+NEGATIVE_FIRST = ODD_FIRST + 1
+ENTRIES = ODD_FIRST + EVEN
+
+FLOPS = 2 * TOKENS * D_IN * SECTIONS * WIDTH + 4 * TOKENS * WIDTH * ENTRIES
+
+
+def slots_of(tile_index, group):
+    last_token = tile_index * P + P - 1
+    return [s for s in range(group * GROUP, min((group + 1) * GROUP, SLOTS)) if OFFSETS[s] <= last_token]
+
+
+def load_tables(tc, ident, b_qkv, pos_bias, identity_bypass, bias_col, tap_bias, bypass):
+    nc = tc.nc
+    with tc.tile_pool(name="setup", bufs=1) as setup, tc.psum_pool(name="setup_ps", bufs=1) as psum:
+        bias_rows = setup.tile([P, P], BF16, name="bias_rows")
+        nc.vector.memset(bias_rows[:], 0.0)
+        for section in range(SECTIONS):
+            nc.sync.dma_start(
+                out=bias_rows[section * HIGH : (section + 1) * HIGH, :].rearrange("a (h l) -> a h l", l=LOW),
+                in_=b_qkv[section * WIDTH : (section + 1) * WIDTH].rearrange(
+                    "(h a l) -> a h l", h=HEADS, a=HIGH, l=LOW
+                ),
+            )
+        bias_rows_f32 = setup.tile([P, P], F32, name="bias_rows_f32")
+        nc.vector.tensor_copy(out=bias_rows_f32[:], in_=bias_rows[:])
+        bias_ps = psum.tile([P, P], F32, name="bias_ps")
+        nc.tensor.transpose(out=bias_ps[:], in_=bias_rows_f32[:], identity=ident[:])
+        nc.vector.tensor_copy(out=bias_col[:], in_=bias_ps[:, 0:CHUNKS])
+
+        pos_raw = setup.tile([P, SCALES * TAUS * HEADS], BF16, name="pos_raw")
+        nc.sync.dma_start(out=pos_raw[:], in_=pos_bias.rearrange("r h -> (r h)").partition_broadcast(P))
+        pos_view = pos_raw[:].rearrange("p (j t h) -> p j t h", t=TAUS, h=HEADS)
+        nc.vector.memset(tap_bias[:, LOCAL, :], 0.0)
+        for first, count, j0, tau in ENTRY_RUNS:
+            nc.vector.tensor_copy(out=tap_bias[:, first : first + count, :], in_=pos_view[:, j0 : j0 + count, tau, :])
+
+        bypass_raw = setup.tile([P, HEADS], BF16, name="bypass_raw")
+        nc.sync.dma_start(out=bypass_raw[:], in_=identity_bypass.partition_broadcast(P))
+        bypass_f32 = setup.tile([P, HEADS], F32, name="bypass_f32")
+        nc.vector.tensor_copy(out=bypass_f32[:], in_=bypass_raw[:])
+        tail = setup.tile([P, HEADS], F32, name="tail")
+        nc.scalar.activation(out=tail[:], in_=bypass_f32[:], func=ACT.Abs)
+        nc.scalar.activation(out=tail[:], in_=tail[:], func=ACT.Exp, scale=-1.0)
+        nc.vector.tensor_scalar_add(out=tail[:], in0=tail[:], scalar1=1.0)
+        nc.scalar.activation(out=tail[:], in_=tail[:], func=ACT.Ln)
+        nc.vector.scalar_tensor_tensor(
+            out=bypass[:], in0=bypass_f32[:], scalar=0.0, in1=tail[:], op0=ALU.max, op1=ALU.add
+        )
+
+
+def project(tc, ident, x_rows, w_words, w_scales, bias_col, q_t, k_t, v_t):
+    nc = tc.nc
+    with (
+        tc.tile_pool(name="mx", bufs=1) as mx,
+        tc.tile_pool(name="stage", bufs=2) as stage,
+        tc.psum_pool(name="mx_ps", bufs=2) as psum,
+    ):
+        scales_raw = mx.tile([P, PASSES, SECTIONS * WIDTH], U8, name="scales_raw", align_bytes=64)
+        nc.vector.memset(scales_raw[:].bitcast(I32), 0)
+        for quadrant in range(4):
+            nc.sync.dma_start(
+                out=scales_raw[32 * quadrant : 32 * quadrant + 4, :, :].bitcast(I32),
+                in_=w_scales[:, 4 * quadrant : 4 * quadrant + 4, :].bitcast(I32).rearrange("g r n -> r g n"),
+            )
+        w_codes = mx.tile([P, PASSES, 2 * SECTIONS * WIDTH], U8, name="w_codes", align_bytes=64)
+        w_planes = mx.tile([P, PASSES, SECTIONS * WIDTH], U8, name="w_planes", align_bytes=64)
+
+        def sort_columns(sorted_bytes, given_bytes):
+            nc.vector.tensor_copy(
+                out=sorted_bytes.bitcast(I32).rearrange("p (a h w) -> p a h w", a=HIGH, h=HEADS),
+                in_=given_bytes.bitcast(I32).rearrange("p (h a w) -> p a h w", h=HEADS, a=HIGH),
+            )
+
+        x_codes = mx.tile([P, PASSES, TOKENS], U32, name="x_codes", align_bytes=64)
+        x_planes = mx.tile([P, PASSES, TOKENS], U8, name="x_planes", align_bytes=64)
+        words_per_pass = K_PASS // 2
+        for block in range(BLOCKS):
+            x_sb = stage.tile([P, TILES_PER_BLOCK, D_IN], BF16, name="x_sb")
+            nc.sync.dma_start(
+                out=x_sb[:],
+                in_=x_rows[block * BLOCK : (block + 1) * BLOCK, :].rearrange("(t p) k -> p t k", p=P),
+            )
+            if block == 0:
+                for g in range(PASSES):
+                    w_raw = stage.tile([P, 2 * SECTIONS * WIDTH], U8, name="w_raw", bufs=1)
+                    nc.sync.dma_start(out=w_raw[:].bitcast(I32), in_=w_words[g].bitcast(I32))
+                    for section in range(SECTIONS):
+                        code_bytes = slice(section * 2 * WIDTH, (section + 1) * 2 * WIDTH)
+                        scale_bytes = slice(section * WIDTH, (section + 1) * WIDTH)
+                        sort_columns(w_codes[:, g, code_bytes], w_raw[:, code_bytes])
+                        sort_columns(w_planes[:, g, scale_bytes], scales_raw[:, g, scale_bytes])
+            for g in range(PASSES):
+                grouped = stage.tile([P, BLOCK, PACK], BF16, name="grouped", align_bytes=64)
+                grouped_words = (
+                    grouped[:]
+                    .rearrange("p r t -> p (r t)")
+                    .bitcast(F32)
+                    .rearrange("p (s i r u) -> p s i r u", s=2, i=2, u=2)
+                )
+                for half in range(2):
+                    turned = psum.tile([P, 2, 2, P], F32, name="turned")
+                    for i in range(2):
+                        x_words = x_sb[:, 2 * half + i, :].bitcast(F32)
+                        for u in range(2):
+                            nc.tensor.transpose(
+                                out=turned[:, i, u, :],
+                                in_=x_words[:, words_per_pass * g + u : words_per_pass * (g + 1) : 2],
+                                identity=ident[:],
+                            )
+                    if half == 0:
+                        nc.vector.tensor_copy(
+                            out=grouped_words[:, half], in_=turned[:].rearrange("p i u r -> p i r u")
+                        )
+                    else:
+                        nc.scalar.copy(out=grouped_words[:, half], in_=turned[:].rearrange("p i u r -> p i r u"))
+                token_cols = slice(block * BLOCK, (block + 1) * BLOCK)
+                nc.vector.quantize_mx(
+                    out=x_codes[:, g, token_cols].bitcast(FP8X4),
+                    scales=x_planes[:, g, token_cols],
+                    in_=grouped[:].rearrange("p r t -> p (r t)"),
+                )
+
+        for block in range(BLOCKS):
+            token_cols = slice(block * BLOCK, (block + 1) * BLOCK)
+            padded_cols = slice(PAD + block * BLOCK, PAD + (block + 1) * BLOCK)
+            for chunk in range(CHUNKS):
+                product = psum.tile([P, BLOCK], F32, name="product", bufs=4)
+                for g in range(PASSES):
+                    nc.tensor.matmul_mx(
+                        out=product[:],
+                        lhsT=w_codes[:, g, chunk * 2 * P : (chunk + 1) * 2 * P].bitcast(FP4X4),
+                        lhsT_scale=w_planes[:, g, chunk * P : (chunk + 1) * P],
+                        rhs=x_codes[:, g, token_cols].bitcast(FP8X4),
+                        rhs_scale=x_planes[:, g, token_cols],
+                        start=(g == 0),
+                        stop=(g == PASSES - 1),
+                    )
+                a = chunk % HIGH
+                home = [q_t[:, a, token_cols], k_t[:, a, padded_cols], v_t[:, a, padded_cols]][chunk // HIGH]
+                if chunk % 2 == 0:
+                    nc.scalar.activation(
+                        out=home, in_=product[:], func=ACT.Identity, bias=bias_col[:, chunk : chunk + 1], scale=1.0
+                    )
+                else:
+                    nc.vector.tensor_scalar_add(out=home, in0=product[:], scalar1=bias_col[:, chunk : chunk + 1])
+
+
+def attend(tc, ident, q_t, k_t, v_t, gains, tap_bias, bypass, out_rows):
+    nc = tc.nc
+    with (
+        tc.tile_pool(name="work", bufs=3) as work,
+        tc.tile_pool(name="taps", bufs=2) as taps,
+        tc.psum_pool(name="att_ps", bufs=2) as psum,
+    ):
+        gain_of = {}
+        dots_of = {}
+        dots_ps_of = {}
+        score_of = {}
+        weight_of = {}
+        spread_ps_of = {}
+        sum_of = {}
+
+        def load_gains(t):
+            gains_raw = taps.tile([P, HEADS, SCALES], BF16, name="gains_raw")
+            nc.sync.dma_start(out=gains_raw[:], in_=gains[0, :, t * P : (t + 1) * P, :].rearrange("h n j -> n h j"))
+            by_scale = gains_raw[:].rearrange("p h j -> p j h")
+            gain = taps.tile([P, ENTRIES, HEADS], F32, name="gain")
+            for first, count, j0, tau in ENTRY_RUNS:
+                nc.scalar.mul(out=gain[:, first : first + count, :], in_=by_scale[:, j0 : j0 + count, :], mul=D4[tau])
+            nc.scalar.copy(out=gain[:, LOCAL, :], in_=bypass[:])
+            gain_of[t] = gain
+
+        def multiply_q_k(t, group):
+            slots = slots_of(t, group)
+            if not slots:
+                return
+            if group == 0:
+                dots = taps.tile([P, SLOTS, HEADS], F32, name="dots")
+                nc.vector.memset(dots[:], 0.0)
+                dots_of[t] = dots
+            dots_ps = psum.tile([P, GROUP, P], F32, name="dots_ps")
+            for i, slot in enumerate(slots):
+                first = PAD + t * P - OFFSETS[slot]
+                prod = work.tile([P, HIGH, P], F32, name="prod")
+                nc.vector.tensor_tensor(
+                    out=prod[:], in0=q_t[:, :, t * P : (t + 1) * P], in1=k_t[:, :, first : first + P], op=ALU.mult
+                )
+                for a in range(HIGH):
+                    nc.tensor.matmul(
+                        out=dots_ps[:, i, :],
+                        lhsT=prod[:, a, :],
+                        rhs=ident[:],
+                        is_transpose=True,
+                        start=(a == 0),
+                        stop=(a == HIGH - 1),
+                    )
+            dots_ps_of[(t, group)] = dots_ps
+
+        def finish_dots(t, group):
+            slots = slots_of(t, group)
+            if not slots:
+                return
+            nc.vector.tensor_reduce(
+                out=dots_of[t][:, slots[0] : slots[-1] + 1, :],
+                in_=dots_ps_of[(t, group)][:, 0 : len(slots), :].rearrange("p s (h l) -> p s h l", l=LOW),
+                axis=AXIS.X,
+                op=ALU.add,
+            )
+
+        def score_entries(t):
+            dots = dots_of[t]
+            u = taps.tile([P, ENTRIES, HEADS], F32, name="u")
+            nc.vector.tensor_tensor(
+                out=u[:, 0:HERE, :],
+                in0=dots[:, 0:1, :].to_broadcast([P, HERE, HEADS]),
+                in1=tap_bias[:, 0:HERE, :],
+                op=ALU.add,
+            )
+            nc.vector.tensor_tensor(
+                out=u[:, HERE:ODD_FIRST, :].rearrange("p (c e) h -> p c e h", c=2),
+                in0=dots[:, 2:SLOTS:2, :].unsqueeze(1).to_broadcast([P, 2, EVEN, HEADS]),
+                in1=tap_bias[:, HERE:ODD_FIRST, :].rearrange("p (c e) h -> p c e h", c=2),
+                op=ALU.add,
+            )
+            nc.vector.tensor_tensor(
+                out=u[:, ODD_FIRST:ENTRIES, :],
+                in0=dots[:, 1:SLOTS:2, :],
+                in1=tap_bias[:, ODD_FIRST:ENTRIES, :],
+                op=ALU.add,
+            )
+            decay = taps.tile([P, ENTRIES, HEADS], F32, name="decay")
+            nc.scalar.activation(out=decay[:], in_=u[:], func=ACT.Relu, scale=-1.0)
+            nc.scalar.activation(out=decay[:], in_=decay[:], func=ACT.Exp, scale=-1.0)
+            score_of[t] = (u, decay)
+
+        def weigh_entries(t):
+            u, decay = score_of[t]
+            feat = taps.tile([P, ENTRIES, HEADS], F32, name="feat")
+            nc.vector.scalar_tensor_tensor(
+                out=feat[:], in0=u[:], scalar=0.0, in1=decay[:], op0=ALU.max, op1=ALU.add
+            )
+            term = taps.tile([P, ENTRIES, HEADS], F32, name="term")
+            nc.vector.tensor_tensor(out=term[:], in0=feat[:], in1=gain_of[t][:], op=ALU.mult)
+
+            def sum_entries(name, first, last):
+                total = taps.tile([P, HEADS], F32, name=name)
+                nc.vector.tensor_reduce(
+                    out=total[:], in_=term[:, first:last, :].rearrange("p e h -> p h e"), axis=AXIS.X, op=ALU.add
+                )
+                return total
+
+            here = sum_entries("here", 0, HERE)
+            positive = sum_entries("positive", HERE, NEGATIVE_FIRST)
+            negative = sum_entries("negative", NEGATIVE_FIRST, ENTRIES)
+            z = taps.tile([P, HEADS], F32, name="z")
+            nc.vector.scalar_tensor_tensor(
+                out=z[:], in0=here[:], scalar=1e-6, in1=positive[:], op0=ALU.add, op1=ALU.add
+            )
+            nc.vector.tensor_tensor(out=z[:], in0=z[:], in1=negative[:], op=ALU.subtract)
+            inv_z = taps.tile([P, HEADS], F32, name="inv_z")
+            nc.vector.reciprocal(out=inv_z[:], in_=z[:])
+            inv_z_rows = inv_z[:].unsqueeze(1).to_broadcast([P, EVEN, HEADS])
+
+            weight = taps.tile([P, SLOTS, HEADS], F32, name="weight")
+            nc.vector.tensor_tensor(out=weight[:, 0, :], in0=here[:], in1=inv_z[:], op=ALU.mult)
+            both = taps.tile([P, EVEN, HEADS], F32, name="both")
+            nc.vector.tensor_tensor(
+                out=both[:], in0=term[:, HERE : HERE + EVEN, :], in1=term[:, HERE + EVEN : ODD_FIRST, :], op=ALU.add
+            )
+            nc.vector.tensor_tensor(out=weight[:, 2:SLOTS:2, :], in0=both[:], in1=inv_z_rows, op=ALU.mult)
+            nc.vector.tensor_tensor(
+                out=weight[:, 1:SLOTS:2, :], in0=term[:, ODD_FIRST:ENTRIES, :], in1=inv_z_rows, op=ALU.mult
+            )
+            weight_of[t] = weight
+
+        def spread_weights(t, group):
+            slots = slots_of(t, group)
+            if not slots:
+                return
+            count = len(slots)
+            repeated = work.tile([P, GROUP, P], F32, name="repeated", bufs=2)
+            nc.scalar.copy(
+                out=repeated[:, 0:count, :].rearrange("p s (h l) -> p s h l", l=LOW),
+                in_=weight_of[t][:, slots[0] : slots[-1] + 1, :].unsqueeze(3).to_broadcast([P, count, HEADS, LOW]),
+            )
+            spread_ps = psum.tile([P, GROUP, P], F32, name="spread_ps")
+            for i in range(count):
+                nc.tensor.transpose(out=spread_ps[:, i, :], in_=repeated[:, i, :], identity=ident[:])
+            spread_ps_of[(t, group)] = spread_ps
+
+        def multiply_w_v(t, group):
+            slots = slots_of(t, group)
+            if not slots:
+                return
+            if group == 0:
+                sum_of[t] = [
+                    psum.tile([P, BLOCK], F32, name="sum_lo", bufs=1),
+                    psum.tile([P, BLOCK], F32, name="sum_hi", bufs=1),
+                ]
+            last_slot = max(s for g in range(GROUPS) for s in slots_of(t, g))
+            per_bank = HIGH // 2
+            for i, slot in enumerate(slots):
+                first = PAD + t * P - OFFSETS[slot]
+                part = work.tile([P, HIGH, P], F32, name="part")
+                nc.vector.tensor_tensor(
+                    out=part[:],
+                    in0=v_t[:, :, first : first + P],
+                    in1=spread_ps_of[(t, group)][:, i, :].unsqueeze(1).to_broadcast([P, HIGH, P]),
+                    op=ALU.mult,
+                )
+                for a in range(HIGH):
+                    column = (a % per_bank) * P
+                    nc.tensor.matmul(
+                        out=sum_of[t][a // per_bank][:, column : column + P],
+                        lhsT=part[:, a, :],
+                        rhs=ident[:],
+                        is_transpose=True,
+                        start=(slot == 0 and a % per_bank == 0),
+                        stop=(slot == last_slot and a % per_bank == per_bank - 1),
+                    )
+
+        def store(t):
+            per_bank = HIGH // 2
+            result = work.tile([P, HEADS, HIGH, LOW], F32, name="result", bufs=2)
+            for bank in range(2):
+                nc.scalar.copy(
+                    out=result[:, :, bank * per_bank : (bank + 1) * per_bank, :],
+                    in_=sum_of[t][bank][:].rearrange("p (a h l) -> p h a l", a=per_bank, h=HEADS),
+                )
+            nc.sync.dma_start(out=out_rows[t * P : (t + 1) * P, :], in_=result[:].rearrange("p h a l -> p (h a l)"))
+
+        for step in range(TILES + 2):
+            dot_tile, weight_tile, out_tile = step, step - 1, step - 2
+            dotting = dot_tile < TILES
+            weighing = 0 <= weight_tile < TILES
+            summing = out_tile >= 0
+            if dotting:
+                load_gains(dot_tile)
+            if weighing:
+                score_entries(weight_tile)
+            if summing:
+                spread_weights(out_tile, 0)
+            for group in range(GROUPS):
+                if dotting:
+                    multiply_q_k(dot_tile, group)
+                if summing:
+                    multiply_w_v(out_tile, group)
+                    if group + 1 < GROUPS:
+                        spread_weights(out_tile, group + 1)
+                if dotting:
+                    finish_dots(dot_tile, group)
+                if weighing and group == 0:
+                    weigh_entries(weight_tile)
+            if summing:
+                store(out_tile)
+
+
+def tile_dwarfattention_pa_kernel(
+    tc, x, W_qkv_words, W_qkv_scales, b_qkv, gains, pos_bias, identity_bypass, out
+):
+    nc = tc.nc
+    with tc.tile_pool(name="keep", bufs=1) as keep:
+        ident = keep.tile([P, P], F32, name="ident")
+        make_identity(nc, ident[:])
+        bias_col = keep.tile([P, CHUNKS], F32, name="bias_col")
+        tap_bias = keep.tile([P, ENTRIES, HEADS], F32, name="tap_bias")
+        bypass = keep.tile([P, HEADS], F32, name="bypass")
+        q_t = keep.tile([P, HIGH, TOKENS], F32, name="q_t")
+        k_t = keep.tile([P, HIGH, PAD + TOKENS], F32, name="k_t")
+        v_t = keep.tile([P, HIGH, PAD + TOKENS], F32, name="v_t")
+        nc.vector.memset(k_t[:, :, 0:PAD], 0.0)
+        nc.vector.memset(v_t[:, :, 0:PAD], 0.0)
+        load_tables(tc, ident, b_qkv, pos_bias, identity_bypass, bias_col, tap_bias, bypass)
+        project(tc, ident, x.flatten_outer_dims(), W_qkv_words, W_qkv_scales, bias_col, q_t, k_t, v_t)
+        attend(tc, ident, q_t, k_t, v_t, gains, tap_bias, bypass, out.flatten_outer_dims())

@@ -33,7 +33,8 @@ TILES_PER_BLOCK = BLOCK // P
 
 LOW = P // HEADS
 HIGH = HEAD_DIM // LOW
-CHUNKS = SECTIONS * HIGH
+CHUNKS = 2 * HIGH
+PER_BANK = BLOCK // P
 PAD = P
 
 OFFSETS = sorted(set(tau << j for j in range(SCALES) for tau in range(TAUS) if (tau << j) < TOKENS))
@@ -43,6 +44,7 @@ assert all(OFFSETS[2 * i] == 1 << i for i in range(1, 11))
 assert all(OFFSETS[2 * i + 1] == 3 << (i - 1) for i in range(1, 10))
 GROUP = 4
 GROUPS = (SLOTS + GROUP - 1) // GROUP
+GPSIMD_SHARE = 3
 
 ENTRY_RUNS = [(0, 11, 0, 0), (12, 10, 1, 1), (22, 10, 0, 2), (32, 1, 0, 1), (33, 9, 0, 3)]
 LOCAL = 11
@@ -60,14 +62,14 @@ def slots_of(tile_index, group):
     return [s for s in range(group * GROUP, min((group + 1) * GROUP, SLOTS)) if OFFSETS[s] <= last_token]
 
 
-def load_tables(tc, ident, b_qkv, pos_bias, identity_bypass, bias_col, tap_bias, bypass):
+def load_tables(tc, ident, b_qkv, pos_bias, identity_bypass, bias_col, bias_row, tap_bias, bypass):
     nc = tc.nc
     with tc.tile_pool(name="setup", bufs=1) as setup, tc.psum_pool(name="setup_ps", bufs=1) as psum:
         bias_rows = setup.tile([P, P], BF16, name="bias_rows")
         nc.vector.memset(bias_rows[:], 0.0)
-        for section in range(SECTIONS):
+        for section in range(1, SECTIONS):
             nc.sync.dma_start(
-                out=bias_rows[section * HIGH : (section + 1) * HIGH, :].rearrange("a (h l) -> a h l", l=LOW),
+                out=bias_rows[(section - 1) * HIGH : section * HIGH, :].rearrange("a (h l) -> a h l", l=LOW),
                 in_=b_qkv[section * WIDTH : (section + 1) * WIDTH].rearrange(
                     "(h a l) -> a h l", h=HEADS, a=HIGH, l=LOW
                 ),
@@ -77,6 +79,13 @@ def load_tables(tc, ident, b_qkv, pos_bias, identity_bypass, bias_col, tap_bias,
         bias_ps = psum.tile([P, P], F32, name="bias_ps")
         nc.tensor.transpose(out=bias_ps[:], in_=bias_rows_f32[:], identity=ident[:])
         nc.vector.tensor_copy(out=bias_col[:], in_=bias_ps[:, 0:CHUNKS])
+
+        bias_q_raw = setup.tile([P, WIDTH], BF16, name="bias_q_raw")
+        nc.sync.dma_start(out=bias_q_raw[:], in_=b_qkv[0:WIDTH].partition_broadcast(P))
+        nc.vector.tensor_copy(
+            out=bias_row[:].rearrange("p (a h l) -> p a h l", a=HIGH, h=HEADS),
+            in_=bias_q_raw[:].rearrange("p (h a l) -> p a h l", h=HEADS, a=HIGH),
+        )
 
         pos_raw = setup.tile([P, SCALES * TAUS * HEADS], BF16, name="pos_raw")
         nc.sync.dma_start(out=pos_raw[:], in_=pos_bias.rearrange("r h -> (r h)").partition_broadcast(P))
@@ -99,7 +108,7 @@ def load_tables(tc, ident, b_qkv, pos_bias, identity_bypass, bias_col, tap_bias,
         )
 
 
-def project(tc, ident, x_rows, w_words, w_scales, bias_col, q_t, k_t, v_t):
+def project(tc, ident, x_rows, w_words, w_scales, bias_col, bias_row, q_tok, k_t, v_t):
     nc = tc.nc
     with (
         tc.tile_pool(name="mx", bufs=1) as mx,
@@ -172,37 +181,57 @@ def project(tc, ident, x_rows, w_words, w_scales, bias_col, q_t, k_t, v_t):
                 )
 
         for block in range(BLOCKS):
+            for t in range(block * TILES_PER_BLOCK, (block + 1) * TILES_PER_BLOCK):
+                for half in range(WIDTH // BLOCK):
+                    product = psum.tile([P, BLOCK], F32, name="product", bufs=4)
+                    for g in range(PASSES):
+                        nc.tensor.matmul_mx(
+                            out=product[:],
+                            lhsT=x_codes[:, g, t * P : (t + 1) * P].bitcast(FP8X4),
+                            lhsT_scale=x_planes[:, g, t * P : (t + 1) * P],
+                            rhs=w_codes[:, g, half * 2 * BLOCK : (half + 1) * 2 * BLOCK].bitcast(FP4X4),
+                            rhs_scale=w_planes[:, g, half * BLOCK : (half + 1) * BLOCK],
+                            start=(g == 0),
+                            stop=(g == PASSES - 1),
+                        )
+                    features = slice(half * BLOCK, (half + 1) * BLOCK)
+                    nc.vector.tensor_tensor(
+                        out=q_tok[:, t, features], in0=product[:], in1=bias_row[:, features], op=ALU.add
+                    )
             token_cols = slice(block * BLOCK, (block + 1) * BLOCK)
             padded_cols = slice(PAD + block * BLOCK, PAD + (block + 1) * BLOCK)
             for chunk in range(CHUNKS):
+                column = WIDTH + chunk * P
                 product = psum.tile([P, BLOCK], F32, name="product", bufs=4)
                 for g in range(PASSES):
                     nc.tensor.matmul_mx(
                         out=product[:],
-                        lhsT=w_codes[:, g, chunk * 2 * P : (chunk + 1) * 2 * P].bitcast(FP4X4),
-                        lhsT_scale=w_planes[:, g, chunk * P : (chunk + 1) * P],
+                        lhsT=w_codes[:, g, 2 * column : 2 * (column + P)].bitcast(FP4X4),
+                        lhsT_scale=w_planes[:, g, column : column + P],
                         rhs=x_codes[:, g, token_cols].bitcast(FP8X4),
                         rhs_scale=x_planes[:, g, token_cols],
                         start=(g == 0),
                         stop=(g == PASSES - 1),
                     )
-                a = chunk % HIGH
-                home = [q_t[:, a, token_cols], k_t[:, a, padded_cols], v_t[:, a, padded_cols]][chunk // HIGH]
-                if chunk % 2 == 0:
-                    nc.scalar.activation(
-                        out=home, in_=product[:], func=ACT.Identity, bias=bias_col[:, chunk : chunk + 1], scale=1.0
-                    )
-                else:
-                    nc.vector.tensor_scalar_add(out=home, in0=product[:], scalar1=bias_col[:, chunk : chunk + 1])
+                home = [k_t, v_t][chunk // HIGH]
+                nc.scalar.activation(
+                    out=home[:, chunk % HIGH, padded_cols],
+                    in_=product[:],
+                    func=ACT.Identity,
+                    bias=bias_col[:, chunk : chunk + 1],
+                    scale=1.0,
+                )
 
 
-def attend(tc, ident, q_t, k_t, v_t, gains, tap_bias, bypass, out_rows):
+def attend(tc, ident, q_tok, k_t, v_t, gains, tap_bias, bypass, out_rows):
     nc = tc.nc
     with (
         tc.tile_pool(name="work", bufs=3) as work,
         tc.tile_pool(name="taps", bufs=2) as taps,
         tc.psum_pool(name="att_ps", bufs=2) as psum,
     ):
+        q_ps_of = {}
+        q_sb_of = {}
         gain_of = {}
         dots_of = {}
         dots_ps_of = {}
@@ -210,6 +239,28 @@ def attend(tc, ident, q_t, k_t, v_t, gains, tap_bias, bypass, out_rows):
         weight_of = {}
         spread_ps_of = {}
         sum_of = {}
+
+        def turn_q(t):
+            q_ps_of[t] = [
+                psum.tile([P, PER_BANK, P], F32, name="q_lo", bufs=1),
+                psum.tile([P, PER_BANK, P], F32, name="q_hi", bufs=1),
+            ]
+            for a in range(HIGH):
+                nc.tensor.transpose(
+                    out=q_ps_of[t][a // PER_BANK][:, a % PER_BANK, :],
+                    in_=q_tok[:, t, a * P : (a + 1) * P],
+                    identity=ident[:],
+                )
+
+        def copy_q(t):
+            q_sb = work.tile([P, HIGH, P], F32, name="q_sb", bufs=2)
+            for bank in range(HIGH // PER_BANK):
+                staged = psum.tile([P, PER_BANK, P], F32, name="staged", tag="dots_ps")
+                for i in range(PER_BANK):
+                    a = bank * PER_BANK + i
+                    nc.tensor.transpose(out=staged[:, i, :], in_=q_tok[:, t, a * P : (a + 1) * P], identity=ident[:])
+                nc.scalar.copy(out=q_sb[:, bank * PER_BANK : (bank + 1) * PER_BANK, :], in_=staged[:])
+            q_sb_of[t] = q_sb
 
         def load_gains(t):
             gains_raw = taps.tile([P, HEADS, SCALES], BF16, name="gains_raw")
@@ -232,10 +283,21 @@ def attend(tc, ident, q_t, k_t, v_t, gains, tap_bias, bypass, out_rows):
             dots_ps = psum.tile([P, GROUP, P], F32, name="dots_ps")
             for i, slot in enumerate(slots):
                 first = PAD + t * P - OFFSETS[slot]
-                prod = work.tile([P, HIGH, P], F32, name="prod")
-                nc.vector.tensor_tensor(
-                    out=prod[:], in0=q_t[:, :, t * P : (t + 1) * P], in1=k_t[:, :, first : first + P], op=ALU.mult
-                )
+                if i < GPSIMD_SHARE:
+                    prod = work.tile([P, HIGH, P], F32, name="prod_gpsimd", bufs=4)
+                    nc.gpsimd.tensor_tensor(
+                        out=prod[:], in0=q_sb_of[t][:], in1=k_t[:, :, first : first + P], op=ALU.mult
+                    )
+                else:
+                    prod = work.tile([P, HIGH, P], F32, name="prod_vector", bufs=2)
+                    for bank in range(HIGH // PER_BANK):
+                        slices = slice(bank * PER_BANK, (bank + 1) * PER_BANK)
+                        nc.vector.tensor_tensor(
+                            out=prod[:, slices, :],
+                            in0=k_t[:, slices, first : first + P],
+                            in1=q_ps_of[t][bank][:],
+                            op=ALU.mult,
+                        )
                 for a in range(HIGH):
                     nc.tensor.matmul(
                         out=dots_ps[:, i, :],
@@ -260,7 +322,7 @@ def attend(tc, ident, q_t, k_t, v_t, gains, tap_bias, bypass, out_rows):
 
         def score_entries(t):
             dots = dots_of[t]
-            u = taps.tile([P, ENTRIES, HEADS], F32, name="u")
+            u = taps.tile([P, ENTRIES, HEADS], F32, name="u", bufs=1)
             nc.vector.tensor_tensor(
                 out=u[:, 0:HERE, :],
                 in0=dots[:, 0:1, :].to_broadcast([P, HERE, HEADS]),
@@ -279,18 +341,18 @@ def attend(tc, ident, q_t, k_t, v_t, gains, tap_bias, bypass, out_rows):
                 in1=tap_bias[:, ODD_FIRST:ENTRIES, :],
                 op=ALU.add,
             )
-            decay = taps.tile([P, ENTRIES, HEADS], F32, name="decay")
+            decay = taps.tile([P, ENTRIES, HEADS], F32, name="decay", bufs=1)
             nc.scalar.activation(out=decay[:], in_=u[:], func=ACT.Relu, scale=-1.0)
             nc.scalar.activation(out=decay[:], in_=decay[:], func=ACT.Exp, scale=-1.0)
             score_of[t] = (u, decay)
 
         def weigh_entries(t):
             u, decay = score_of[t]
-            feat = taps.tile([P, ENTRIES, HEADS], F32, name="feat")
+            feat = taps.tile([P, ENTRIES, HEADS], F32, name="feat", bufs=1)
             nc.vector.scalar_tensor_tensor(
                 out=feat[:], in0=u[:], scalar=0.0, in1=decay[:], op0=ALU.max, op1=ALU.add
             )
-            term = taps.tile([P, ENTRIES, HEADS], F32, name="term")
+            term = taps.tile([P, ENTRIES, HEADS], F32, name="term", bufs=1)
             nc.vector.tensor_tensor(out=term[:], in0=feat[:], in1=gain_of[t][:], op=ALU.mult)
 
             def sum_entries(name, first, last):
@@ -349,7 +411,6 @@ def attend(tc, ident, q_t, k_t, v_t, gains, tap_bias, bypass, out_rows):
                     psum.tile([P, BLOCK], F32, name="sum_hi", bufs=1),
                 ]
             last_slot = max(s for g in range(GROUPS) for s in slots_of(t, g))
-            per_bank = HIGH // 2
             for i, slot in enumerate(slots):
                 first = PAD + t * P - OFFSETS[slot]
                 part = work.tile([P, HIGH, P], F32, name="part")
@@ -360,26 +421,26 @@ def attend(tc, ident, q_t, k_t, v_t, gains, tap_bias, bypass, out_rows):
                     op=ALU.mult,
                 )
                 for a in range(HIGH):
-                    column = (a % per_bank) * P
+                    column = (a % PER_BANK) * P
                     nc.tensor.matmul(
-                        out=sum_of[t][a // per_bank][:, column : column + P],
+                        out=sum_of[t][a // PER_BANK][:, column : column + P],
                         lhsT=part[:, a, :],
                         rhs=ident[:],
                         is_transpose=True,
-                        start=(slot == 0 and a % per_bank == 0),
-                        stop=(slot == last_slot and a % per_bank == per_bank - 1),
+                        start=(slot == 0 and a % PER_BANK == 0),
+                        stop=(slot == last_slot and a % PER_BANK == PER_BANK - 1),
                     )
 
         def store(t):
-            per_bank = HIGH // 2
-            result = work.tile([P, HEADS, HIGH, LOW], F32, name="result", bufs=2)
-            for bank in range(2):
+            result = work.tile([P, HEADS, HIGH, LOW], F32, name="result", bufs=1)
+            for bank in range(HIGH // PER_BANK):
                 nc.scalar.copy(
-                    out=result[:, :, bank * per_bank : (bank + 1) * per_bank, :],
-                    in_=sum_of[t][bank][:].rearrange("p (a h l) -> p h a l", a=per_bank, h=HEADS),
+                    out=result[:, :, bank * PER_BANK : (bank + 1) * PER_BANK, :],
+                    in_=sum_of[t][bank][:].rearrange("p (a h l) -> p h a l", a=PER_BANK, h=HEADS),
                 )
             nc.sync.dma_start(out=out_rows[t * P : (t + 1) * P, :], in_=result[:].rearrange("p h a l -> p (h a l)"))
 
+        copy_q(0)
         for step in range(TILES + 2):
             dot_tile, weight_tile, out_tile = step, step - 1, step - 2
             dotting = dot_tile < TILES
@@ -387,6 +448,7 @@ def attend(tc, ident, q_t, k_t, v_t, gains, tap_bias, bypass, out_rows):
             summing = out_tile >= 0
             if dotting:
                 load_gains(dot_tile)
+                turn_q(dot_tile)
             if weighing:
                 score_entries(weight_tile)
             if summing:
@@ -402,6 +464,8 @@ def attend(tc, ident, q_t, k_t, v_t, gains, tap_bias, bypass, out_rows):
                     finish_dots(dot_tile, group)
                 if weighing and group == 0:
                     weigh_entries(weight_tile)
+                if group == GROUPS // 2 and dot_tile + 1 < TILES:
+                    copy_q(dot_tile + 1)
             if summing:
                 store(out_tile)
 
@@ -413,14 +477,16 @@ def tile_dwarfattention_pa_kernel(
     with tc.tile_pool(name="keep", bufs=1) as keep:
         ident = keep.tile([P, P], F32, name="ident")
         make_identity(nc, ident[:])
-        bias_col = keep.tile([P, CHUNKS], F32, name="bias_col")
         tap_bias = keep.tile([P, ENTRIES, HEADS], F32, name="tap_bias")
         bypass = keep.tile([P, HEADS], F32, name="bypass")
-        q_t = keep.tile([P, HIGH, TOKENS], F32, name="q_t")
+        q_tok = keep.tile([P, TILES, WIDTH], F32, name="q_tok")
         k_t = keep.tile([P, HIGH, PAD + TOKENS], F32, name="k_t")
         v_t = keep.tile([P, HIGH, PAD + TOKENS], F32, name="v_t")
         nc.vector.memset(k_t[:, :, 0:PAD], 0.0)
         nc.vector.memset(v_t[:, :, 0:PAD], 0.0)
-        load_tables(tc, ident, b_qkv, pos_bias, identity_bypass, bias_col, tap_bias, bypass)
-        project(tc, ident, x.flatten_outer_dims(), W_qkv_words, W_qkv_scales, bias_col, q_t, k_t, v_t)
-        attend(tc, ident, q_t, k_t, v_t, gains, tap_bias, bypass, out.flatten_outer_dims())
+        with tc.tile_pool(name="bias", bufs=1) as bias:
+            bias_col = bias.tile([P, CHUNKS], F32, name="bias_col")
+            bias_row = bias.tile([P, WIDTH], F32, name="bias_row")
+            load_tables(tc, ident, b_qkv, pos_bias, identity_bypass, bias_col, bias_row, tap_bias, bypass)
+            project(tc, ident, x.flatten_outer_dims(), W_qkv_words, W_qkv_scales, bias_col, bias_row, q_tok, k_t, v_t)
+        attend(tc, ident, q_tok, k_t, v_t, gains, tap_bias, bypass, out.flatten_outer_dims())

@@ -18,7 +18,9 @@ D_IN = 1024
 HEADS = 16
 HEAD_DIM = 64
 WIDTH = HEADS * HEAD_DIM
-SECTIONS = 3
+Q_AT = 0
+K_AT = WIDTH
+V_AT = 2 * WIDTH
 SCALES = 11
 TAUS = 4
 D4 = [0.4829629131445341, 0.8365163037378079, 0.2241438680420134, -0.1294095225512604]
@@ -30,11 +32,11 @@ BLOCK = 512
 BLOCKS = TOKENS // BLOCK
 TILES = TOKENS // P
 TILES_PER_BLOCK = BLOCK // P
+HALVES = WIDTH // BLOCK
+PER_BANK = BLOCK // P
 
 LOW = P // HEADS
 HIGH = HEAD_DIM // LOW
-CHUNKS = 2 * HIGH
-PER_BANK = BLOCK // P
 PAD = P
 
 OFFSETS = sorted(set(tau << j for j in range(SCALES) for tau in range(TAUS) if (tau << j) < TOKENS))
@@ -44,7 +46,8 @@ assert all(OFFSETS[2 * i] == 1 << i for i in range(1, 11))
 assert all(OFFSETS[2 * i + 1] == 3 << (i - 1) for i in range(1, 10))
 GROUP = 4
 GROUPS = (SLOTS + GROUP - 1) // GROUP
-GPSIMD_SHARE = 3
+VECTOR_TURNS = (2, 5)
+TURNS = 7
 
 ENTRY_RUNS = [(0, 11, 0, 0), (12, 10, 1, 1), (22, 10, 0, 2), (32, 1, 0, 1), (33, 9, 0, 3)]
 LOCAL = 11
@@ -54,7 +57,7 @@ ODD_FIRST = HERE + 2 * EVEN
 NEGATIVE_FIRST = ODD_FIRST + 1
 ENTRIES = ODD_FIRST + EVEN
 
-FLOPS = 2 * TOKENS * D_IN * SECTIONS * WIDTH + 4 * TOKENS * WIDTH * ENTRIES
+FLOPS = 2 * TOKENS * D_IN * 3 * WIDTH + 4 * TOKENS * WIDTH * ENTRIES
 
 
 def slots_of(tile_index, group):
@@ -62,30 +65,30 @@ def slots_of(tile_index, group):
     return [s for s in range(group * GROUP, min((group + 1) * GROUP, SLOTS)) if OFFSETS[s] <= last_token]
 
 
-def load_tables(tc, ident, b_qkv, pos_bias, identity_bypass, bias_col, bias_row, tap_bias, bypass):
+def load_tables(tc, ident, b_qkv, pos_bias, identity_bypass, gains, bias_k, bias_q, bias_v, tap_bias, bypass, gains_raw):
     nc = tc.nc
     with tc.tile_pool(name="setup", bufs=1) as setup, tc.psum_pool(name="setup_ps", bufs=1) as psum:
         bias_rows = setup.tile([P, P], BF16, name="bias_rows")
         nc.vector.memset(bias_rows[:], 0.0)
-        for section in range(1, SECTIONS):
-            nc.sync.dma_start(
-                out=bias_rows[(section - 1) * HIGH : section * HIGH, :].rearrange("a (h l) -> a h l", l=LOW),
-                in_=b_qkv[section * WIDTH : (section + 1) * WIDTH].rearrange(
-                    "(h a l) -> a h l", h=HEADS, a=HIGH, l=LOW
-                ),
-            )
+        nc.sync.dma_start(
+            out=bias_rows[0:HIGH, :].rearrange("a (h l) -> a h l", l=LOW),
+            in_=b_qkv[K_AT : K_AT + WIDTH].rearrange("(h a l) -> a h l", h=HEADS, a=HIGH, l=LOW),
+        )
         bias_rows_f32 = setup.tile([P, P], F32, name="bias_rows_f32")
         nc.vector.tensor_copy(out=bias_rows_f32[:], in_=bias_rows[:])
         bias_ps = psum.tile([P, P], F32, name="bias_ps")
         nc.tensor.transpose(out=bias_ps[:], in_=bias_rows_f32[:], identity=ident[:])
-        nc.vector.tensor_copy(out=bias_col[:], in_=bias_ps[:, 0:CHUNKS])
+        nc.vector.tensor_copy(out=bias_k[:], in_=bias_ps[:, 0:HIGH])
 
         bias_q_raw = setup.tile([P, WIDTH], BF16, name="bias_q_raw")
-        nc.sync.dma_start(out=bias_q_raw[:], in_=b_qkv[0:WIDTH].partition_broadcast(P))
+        nc.sync.dma_start(out=bias_q_raw[:], in_=b_qkv[Q_AT : Q_AT + WIDTH].partition_broadcast(P))
         nc.vector.tensor_copy(
-            out=bias_row[:].rearrange("p (a h l) -> p a h l", a=HIGH, h=HEADS),
+            out=bias_q[:].rearrange("p (a h l) -> p a h l", a=HIGH, h=HEADS),
             in_=bias_q_raw[:].rearrange("p (h a l) -> p a h l", h=HEADS, a=HIGH),
         )
+        bias_v_raw = setup.tile([P, WIDTH], BF16, name="bias_v_raw")
+        nc.sync.dma_start(out=bias_v_raw[:], in_=b_qkv[V_AT : V_AT + WIDTH].partition_broadcast(P))
+        nc.vector.tensor_copy(out=bias_v[:], in_=bias_v_raw[:])
 
         pos_raw = setup.tile([P, SCALES * TAUS * HEADS], BF16, name="pos_raw")
         nc.sync.dma_start(out=pos_raw[:], in_=pos_bias.rearrange("r h -> (r h)").partition_broadcast(P))
@@ -107,23 +110,27 @@ def load_tables(tc, ident, b_qkv, pos_bias, identity_bypass, bias_col, bias_row,
             out=bypass[:], in0=bypass_f32[:], scalar=0.0, in1=tail[:], op0=ALU.max, op1=ALU.add
         )
 
+    for t in range(TILES):
+        nc.gpsimd.dma_start(out=gains_raw[:, t], in_=gains[0, :, t * P : (t + 1) * P, :].rearrange("h n j -> n h j"))
 
-def project(tc, ident, x_rows, w_words, w_scales, bias_col, bias_row, q_tok, k_t, v_t):
+
+def project(tc, ident, x_rows, w_words, w_scales, bias_k, bias_q, bias_v, q_tok, k_t, v_rows):
     nc = tc.nc
     with (
         tc.tile_pool(name="mx", bufs=1) as mx,
         tc.tile_pool(name="stage", bufs=2) as stage,
         tc.psum_pool(name="mx_ps", bufs=2) as psum,
     ):
-        scales_raw = mx.tile([P, PASSES, SECTIONS * WIDTH], U8, name="scales_raw", align_bytes=64)
-        nc.vector.memset(scales_raw[:].bitcast(I32), 0)
+        w_planes = mx.tile([P, PASSES, 3 * WIDTH], U8, name="w_planes", align_bytes=64)
+        nc.vector.memset(w_planes[:].bitcast(I32), 0)
         for quadrant in range(4):
             nc.sync.dma_start(
-                out=scales_raw[32 * quadrant : 32 * quadrant + 4, :, :].bitcast(I32),
+                out=w_planes[32 * quadrant : 32 * quadrant + 4, :, :].bitcast(I32),
                 in_=w_scales[:, 4 * quadrant : 4 * quadrant + 4, :].bitcast(I32).rearrange("g r n -> r g n"),
             )
-        w_codes = mx.tile([P, PASSES, 2 * SECTIONS * WIDTH], U8, name="w_codes", align_bytes=64)
-        w_planes = mx.tile([P, PASSES, SECTIONS * WIDTH], U8, name="w_planes", align_bytes=64)
+        w_codes = mx.tile([P, PASSES, 2 * 3 * WIDTH], U8, name="w_codes", align_bytes=64)
+        sorted_planes = mx.tile([P, PASSES, 2 * WIDTH], U8, name="sorted_planes", align_bytes=64)
+        sorted_codes = mx.tile([P, PASSES, 2 * 2 * WIDTH], U8, name="sorted_codes", align_bytes=64)
 
         def sort_columns(sorted_bytes, given_bytes):
             nc.vector.tensor_copy(
@@ -142,13 +149,10 @@ def project(tc, ident, x_rows, w_words, w_scales, bias_col, bias_row, q_tok, k_t
             )
             if block == 0:
                 for g in range(PASSES):
-                    w_raw = stage.tile([P, 2 * SECTIONS * WIDTH], U8, name="w_raw", bufs=1)
-                    nc.sync.dma_start(out=w_raw[:].bitcast(I32), in_=w_words[g].bitcast(I32))
-                    for section in range(SECTIONS):
-                        code_bytes = slice(section * 2 * WIDTH, (section + 1) * 2 * WIDTH)
-                        scale_bytes = slice(section * WIDTH, (section + 1) * WIDTH)
-                        sort_columns(w_codes[:, g, code_bytes], w_raw[:, code_bytes])
-                        sort_columns(w_planes[:, g, scale_bytes], scales_raw[:, g, scale_bytes])
+                    nc.sync.dma_start(out=w_codes[:, g, :].bitcast(I32), in_=w_words[g].bitcast(I32))
+                    for at in (Q_AT, K_AT):
+                        sort_columns(sorted_codes[:, g, 2 * at : 2 * (at + WIDTH)], w_codes[:, g, 2 * at : 2 * (at + WIDTH)])
+                        sort_columns(sorted_planes[:, g, at : at + WIDTH], w_planes[:, g, at : at + WIDTH])
             for g in range(PASSES):
                 grouped = stage.tile([P, BLOCK, PACK], BF16, name="grouped", align_bytes=64)
                 grouped_words = (
@@ -180,71 +184,77 @@ def project(tc, ident, x_rows, w_words, w_scales, bias_col, bias_row, q_tok, k_t
                     in_=grouped[:].rearrange("p r t -> p (r t)"),
                 )
 
-        for block in range(BLOCKS):
-            for t in range(block * TILES_PER_BLOCK, (block + 1) * TILES_PER_BLOCK):
-                for half in range(WIDTH // BLOCK):
-                    product = psum.tile([P, BLOCK], F32, name="product", bufs=4)
-                    for g in range(PASSES):
-                        nc.tensor.matmul_mx(
-                            out=product[:],
-                            lhsT=x_codes[:, g, t * P : (t + 1) * P].bitcast(FP8X4),
-                            lhsT_scale=x_planes[:, g, t * P : (t + 1) * P],
-                            rhs=w_codes[:, g, half * 2 * BLOCK : (half + 1) * 2 * BLOCK].bitcast(FP4X4),
-                            rhs_scale=w_planes[:, g, half * BLOCK : (half + 1) * BLOCK],
-                            start=(g == 0),
-                            stop=(g == PASSES - 1),
-                        )
-                    features = slice(half * BLOCK, (half + 1) * BLOCK)
-                    nc.vector.tensor_tensor(
-                        out=q_tok[:, t, features], in0=product[:], in1=bias_row[:, features], op=ALU.add
-                    )
-            token_cols = slice(block * BLOCK, (block + 1) * BLOCK)
-            padded_cols = slice(PAD + block * BLOCK, PAD + (block + 1) * BLOCK)
-            for chunk in range(CHUNKS):
-                column = WIDTH + chunk * P
+        def tokens_by_features(t, codes, planes, at, bias_row, home):
+            for half in range(HALVES):
+                column = at + half * BLOCK
                 product = psum.tile([P, BLOCK], F32, name="product", bufs=4)
                 for g in range(PASSES):
                     nc.tensor.matmul_mx(
                         out=product[:],
-                        lhsT=w_codes[:, g, 2 * column : 2 * (column + P)].bitcast(FP4X4),
-                        lhsT_scale=w_planes[:, g, column : column + P],
+                        lhsT=x_codes[:, g, t * P : (t + 1) * P].bitcast(FP8X4),
+                        lhsT_scale=x_planes[:, g, t * P : (t + 1) * P],
+                        rhs=codes[:, g, 2 * column : 2 * (column + BLOCK)].bitcast(FP4X4),
+                        rhs_scale=planes[:, g, column : column + BLOCK],
+                        start=(g == 0),
+                        stop=(g == PASSES - 1),
+                    )
+                features = slice(half * BLOCK, (half + 1) * BLOCK)
+                nc.vector.tensor_tensor(out=home[:, features], in0=product[:], in1=bias_row[:, features], op=ALU.add)
+
+        for block in range(BLOCKS):
+            for t in range(block * TILES_PER_BLOCK, (block + 1) * TILES_PER_BLOCK):
+                tokens_by_features(t, sorted_codes, sorted_planes, Q_AT, bias_q, q_tok[:, t, :])
+                v_tok = stage.tile([P, WIDTH], F32, name="v_tok", bufs=3)
+                tokens_by_features(t, w_codes, w_planes, V_AT, bias_v, v_tok)
+                nc.sync.dma_start(out=v_rows[t * P : (t + 1) * P, :], in_=v_tok[:])
+            token_cols = slice(block * BLOCK, (block + 1) * BLOCK)
+            for a in range(HIGH):
+                column = K_AT + a * P
+                product = psum.tile([P, BLOCK], F32, name="product", bufs=4)
+                for g in range(PASSES):
+                    nc.tensor.matmul_mx(
+                        out=product[:],
+                        lhsT=sorted_codes[:, g, 2 * column : 2 * (column + P)].bitcast(FP4X4),
+                        lhsT_scale=sorted_planes[:, g, column : column + P],
                         rhs=x_codes[:, g, token_cols].bitcast(FP8X4),
                         rhs_scale=x_planes[:, g, token_cols],
                         start=(g == 0),
                         stop=(g == PASSES - 1),
                     )
-                home = [k_t, v_t][chunk // HIGH]
                 nc.scalar.activation(
-                    out=home[:, chunk % HIGH, padded_cols],
+                    out=k_t[:, a, PAD + block * BLOCK : PAD + (block + 1) * BLOCK],
                     in_=product[:],
                     func=ACT.Identity,
-                    bias=bias_col[:, chunk : chunk + 1],
+                    bias=bias_k[:, a : a + 1],
                     scale=1.0,
                 )
 
 
-def attend(tc, ident, q_tok, k_t, v_t, gains, tap_bias, bypass, out_rows):
+def attend(tc, ident, q_tok, k_t, v_rows, gains_raw, tap_bias, bypass):
     nc = tc.nc
     with (
-        tc.tile_pool(name="work", bufs=3) as work,
+        tc.tile_pool(name="work", bufs=2) as work,
         tc.tile_pool(name="taps", bufs=2) as taps,
-        tc.psum_pool(name="att_ps", bufs=2) as psum,
+        tc.psum_pool(name="att_ps", bufs=1) as psum,
     ):
         q_ps_of = {}
         q_sb_of = {}
         gain_of = {}
         dots_of = {}
-        dots_ps_of = {}
         score_of = {}
         weight_of = {}
-        spread_ps_of = {}
         sum_of = {}
+        rows_of = {}
+
+        head_of = taps.tile([P, HEADS], F32, name="head_of", bufs=1)
+        nc.vector.tensor_reduce(
+            out=head_of[:], in_=ident[:].rearrange("p (h l) -> p h l", l=LOW), axis=AXIS.X, op=ALU.add
+        )
+        zeros = taps.tile([P, P], F32, name="zeros", bufs=1)
+        nc.vector.memset(zeros[:], 0.0)
 
         def turn_q(t):
-            q_ps_of[t] = [
-                psum.tile([P, PER_BANK, P], F32, name="q_lo", bufs=1),
-                psum.tile([P, PER_BANK, P], F32, name="q_hi", bufs=1),
-            ]
+            q_ps_of[t] = [psum.tile([P, PER_BANK, P], F32, name="q_ps%d" % bank) for bank in range(HALVES)]
             for a in range(HIGH):
                 nc.tensor.transpose(
                     out=q_ps_of[t][a // PER_BANK][:, a % PER_BANK, :],
@@ -253,19 +263,17 @@ def attend(tc, ident, q_tok, k_t, v_t, gains, tap_bias, bypass, out_rows):
                 )
 
         def copy_q(t):
-            q_sb = work.tile([P, HIGH, P], F32, name="q_sb", bufs=2)
-            for bank in range(HIGH // PER_BANK):
-                staged = psum.tile([P, PER_BANK, P], F32, name="staged", tag="dots_ps")
+            q_sb = work.tile([P, HIGH, P], F32, name="q_sb")
+            for bank in range(HALVES):
+                staged = psum.tile([P, PER_BANK, P], F32, name="staged", tag="dots_ps", bufs=2)
                 for i in range(PER_BANK):
                     a = bank * PER_BANK + i
                     nc.tensor.transpose(out=staged[:, i, :], in_=q_tok[:, t, a * P : (a + 1) * P], identity=ident[:])
                 nc.scalar.copy(out=q_sb[:, bank * PER_BANK : (bank + 1) * PER_BANK, :], in_=staged[:])
             q_sb_of[t] = q_sb
 
-        def load_gains(t):
-            gains_raw = taps.tile([P, HEADS, SCALES], BF16, name="gains_raw")
-            nc.sync.dma_start(out=gains_raw[:], in_=gains[0, :, t * P : (t + 1) * P, :].rearrange("h n j -> n h j"))
-            by_scale = gains_raw[:].rearrange("p h j -> p j h")
+        def scale_gains(t):
+            by_scale = gains_raw[:, t].rearrange("p h j -> p j h")
             gain = taps.tile([P, ENTRIES, HEADS], F32, name="gain")
             for first, count, j0, tau in ENTRY_RUNS:
                 nc.scalar.mul(out=gain[:, first : first + count, :], in_=by_scale[:, j0 : j0 + count, :], mul=D4[tau])
@@ -277,20 +285,26 @@ def attend(tc, ident, q_tok, k_t, v_t, gains, tap_bias, bypass, out_rows):
             if not slots:
                 return
             if group == 0:
-                dots = taps.tile([P, SLOTS, HEADS], F32, name="dots")
-                nc.vector.memset(dots[:], 0.0)
-                dots_of[t] = dots
-            dots_ps = psum.tile([P, GROUP, P], F32, name="dots_ps")
-            for i, slot in enumerate(slots):
+                dots_of[t] = psum.tile([P, SLOTS, HEADS], F32, name="dots_ps", bufs=2)
+                used = sum(len(slots_of(t, g)) for g in range(GROUPS))
+                if used < SLOTS:
+                    nc.tensor.matmul(
+                        out=dots_of[t][:, used:SLOTS, :].rearrange("p s h -> p (s h)"),
+                        lhsT=zeros[:],
+                        rhs=ident[:, 0 : (SLOTS - used) * HEADS],
+                        start=True,
+                        stop=True,
+                    )
+            for slot in slots:
                 first = PAD + t * P - OFFSETS[slot]
-                if i < GPSIMD_SHARE:
+                if slot % TURNS not in VECTOR_TURNS:
                     prod = work.tile([P, HIGH, P], F32, name="prod_gpsimd", bufs=4)
                     nc.gpsimd.tensor_tensor(
                         out=prod[:], in0=q_sb_of[t][:], in1=k_t[:, :, first : first + P], op=ALU.mult
                     )
                 else:
-                    prod = work.tile([P, HIGH, P], F32, name="prod_vector", bufs=2)
-                    for bank in range(HIGH // PER_BANK):
+                    prod = work.tile([P, HIGH, P], F32, name="prod_vector")
+                    for bank in range(HALVES):
                         slices = slice(bank * PER_BANK, (bank + 1) * PER_BANK)
                         nc.vector.tensor_tensor(
                             out=prod[:, slices, :],
@@ -298,27 +312,11 @@ def attend(tc, ident, q_tok, k_t, v_t, gains, tap_bias, bypass, out_rows):
                             in1=q_ps_of[t][bank][:],
                             op=ALU.mult,
                         )
-                for a in range(HIGH):
-                    nc.tensor.matmul(
-                        out=dots_ps[:, i, :],
-                        lhsT=prod[:, a, :],
-                        rhs=ident[:],
-                        is_transpose=True,
-                        start=(a == 0),
-                        stop=(a == HIGH - 1),
-                    )
-            dots_ps_of[(t, group)] = dots_ps
-
-        def finish_dots(t, group):
-            slots = slots_of(t, group)
-            if not slots:
-                return
-            nc.vector.tensor_reduce(
-                out=dots_of[t][:, slots[0] : slots[-1] + 1, :],
-                in_=dots_ps_of[(t, group)][:, 0 : len(slots), :].rearrange("p s (h l) -> p s h l", l=LOW),
-                axis=AXIS.X,
-                op=ALU.add,
-            )
+                folded = work.tile([P, P], F32, name="folded", bufs=4)
+                nc.vector.tensor_reduce(
+                    out=folded[:], in_=prod[:].rearrange("p a n -> p n a"), axis=AXIS.X, op=ALU.add
+                )
+                nc.tensor.matmul(out=dots_of[t][:, slot, :], lhsT=folded[:], rhs=head_of[:], start=True, stop=True)
 
         def score_entries(t):
             dots = dots_of[t]
@@ -386,107 +384,102 @@ def attend(tc, ident, q_tok, k_t, v_t, gains, tap_bias, bypass, out_rows):
             )
             weight_of[t] = weight
 
-        def spread_weights(t, group):
-            slots = slots_of(t, group)
-            if not slots:
-                return
-            count = len(slots)
-            repeated = work.tile([P, GROUP, P], F32, name="repeated", bufs=2)
-            nc.scalar.copy(
-                out=repeated[:, 0:count, :].rearrange("p s (h l) -> p s h l", l=LOW),
-                in_=weight_of[t][:, slots[0] : slots[-1] + 1, :].unsqueeze(3).to_broadcast([P, count, HEADS, LOW]),
-            )
-            spread_ps = psum.tile([P, GROUP, P], F32, name="spread_ps")
-            for i in range(count):
-                nc.tensor.transpose(out=spread_ps[:, i, :], in_=repeated[:, i, :], identity=ident[:])
-            spread_ps_of[(t, group)] = spread_ps
-
         def multiply_w_v(t, group):
             slots = slots_of(t, group)
             if not slots:
                 return
             if group == 0:
-                sum_of[t] = [
-                    psum.tile([P, BLOCK], F32, name="sum_lo", bufs=1),
-                    psum.tile([P, BLOCK], F32, name="sum_hi", bufs=1),
-                ]
+                sum_of[t] = [psum.tile([P, PER_BANK, P], F32, name="sum_ps%d" % bank) for bank in range(HALVES)]
             last_slot = max(s for g in range(GROUPS) for s in slots_of(t, g))
-            for i, slot in enumerate(slots):
-                first = PAD + t * P - OFFSETS[slot]
-                part = work.tile([P, HIGH, P], F32, name="part")
-                nc.vector.tensor_tensor(
-                    out=part[:],
-                    in0=v_t[:, :, first : first + P],
-                    in1=spread_ps_of[(t, group)][:, i, :].unsqueeze(1).to_broadcast([P, HIGH, P]),
-                    op=ALU.mult,
-                )
-                for a in range(HIGH):
-                    column = (a % PER_BANK) * P
+            for slot in slots:
+                first = t * P - OFFSETS[slot]
+                missing = max(0, -first)
+                shifted = work.tile([P, WIDTH], F32, name="shifted", bufs=6)
+                if missing:
+                    nc.vector.memset(shifted[0:missing, :], 0.0)
+                nc.sync.dma_start(out=shifted[missing:P, :], in_=v_rows[first + missing : first + P, :])
+                scaled = work.tile([P, WIDTH], F32, name="scaled", bufs=4)
+                for h in range(HEADS):
+                    features = slice(h * HEAD_DIM, (h + 1) * HEAD_DIM)
+                    nc.scalar.activation(
+                        out=scaled[:, features],
+                        in_=shifted[:, features],
+                        func=ACT.Copy,
+                        scale=weight_of[t][:, slot, h : h + 1],
+                    )
+                for c in range(WIDTH // P):
                     nc.tensor.matmul(
-                        out=sum_of[t][a // PER_BANK][:, column : column + P],
-                        lhsT=part[:, a, :],
+                        out=sum_of[t][c // PER_BANK][:, c % PER_BANK, :],
+                        lhsT=scaled[:, c * P : (c + 1) * P],
                         rhs=ident[:],
                         is_transpose=True,
-                        start=(slot == 0 and a % PER_BANK == 0),
-                        stop=(slot == last_slot and a % PER_BANK == PER_BANK - 1),
+                        start=(slot == 0 and c % PER_BANK == 0),
+                        stop=(slot == last_slot and c % PER_BANK == PER_BANK - 1),
                     )
 
-        def store(t):
-            result = work.tile([P, HEADS, HIGH, LOW], F32, name="result", bufs=1)
-            for bank in range(HIGH // PER_BANK):
-                nc.scalar.copy(
-                    out=result[:, :, bank * PER_BANK : (bank + 1) * PER_BANK, :],
-                    in_=sum_of[t][bank][:].rearrange("p (a h l) -> p h a l", a=PER_BANK, h=HEADS),
+        def finish_output(t):
+            sum_sb = work.tile([P, WIDTH // P, P], F32, name="sum_sb", bufs=1)
+            for bank in range(HALVES):
+                nc.scalar.copy(out=sum_sb[:, bank * PER_BANK : (bank + 1) * PER_BANK, :], in_=sum_of[t][bank][:])
+            rows = work.tile([P, WIDTH], F32, name="rows")
+            for bank in range(HALVES):
+                rows_ps = psum.tile([P, PER_BANK, P], F32, name="rows_ps%d" % bank)
+                for i in range(PER_BANK):
+                    nc.tensor.transpose(out=rows_ps[:, i, :], in_=sum_sb[:, bank * PER_BANK + i, :], identity=ident[:])
+                nc.vector.tensor_copy(
+                    out=rows[:, bank * BLOCK : (bank + 1) * BLOCK], in_=rows_ps[:].rearrange("p c f -> p (c f)")
                 )
-            nc.sync.dma_start(out=out_rows[t * P : (t + 1) * P, :], in_=result[:].rearrange("p h a l -> p (h a l)"))
+            rows_of[t] = rows
 
-        copy_q(0)
-        for step in range(TILES + 2):
-            dot_tile, weight_tile, out_tile = step, step - 1, step - 2
-            dotting = dot_tile < TILES
-            weighing = 0 <= weight_tile < TILES
-            summing = out_tile >= 0
-            if dotting:
-                load_gains(dot_tile)
+        def store(t):
+            nc.sync.dma_start(out=v_rows[t * P : (t + 1) * P, :], in_=rows_of[t][:])
+
+        def tile_at(step):
+            return TILES - 1 - step if 0 <= step < TILES else None
+
+        copy_q(tile_at(0))
+        for step in range(TILES + 3):
+            dot_tile, weight_tile, out_tile, done_tile = [tile_at(step - lag) for lag in range(4)]
+            if dot_tile is not None:
+                scale_gains(dot_tile)
                 turn_q(dot_tile)
-            if weighing:
+            if weight_tile is not None:
                 score_entries(weight_tile)
-            if summing:
-                spread_weights(out_tile, 0)
             for group in range(GROUPS):
-                if dotting:
+                if dot_tile is not None:
                     multiply_q_k(dot_tile, group)
-                if summing:
+                if out_tile is not None:
                     multiply_w_v(out_tile, group)
-                    if group + 1 < GROUPS:
-                        spread_weights(out_tile, group + 1)
-                if dotting:
-                    finish_dots(dot_tile, group)
-                if weighing and group == 0:
+                if group == 0 and weight_tile is not None:
                     weigh_entries(weight_tile)
-                if group == GROUPS // 2 and dot_tile + 1 < TILES:
-                    copy_q(dot_tile + 1)
-            if summing:
-                store(out_tile)
+                if group == 0 and done_tile is not None:
+                    store(done_tile)
+                if group == GROUPS // 2 and tile_at(step + 1) is not None:
+                    copy_q(tile_at(step + 1))
+            if out_tile is not None:
+                finish_output(out_tile)
 
 
 def tile_dwarfattention_pa_kernel(
     tc, x, W_qkv_words, W_qkv_scales, b_qkv, gains, pos_bias, identity_bypass, out
 ):
     nc = tc.nc
+    out_rows = out.flatten_outer_dims()
     with tc.tile_pool(name="keep", bufs=1) as keep:
         ident = keep.tile([P, P], F32, name="ident")
         make_identity(nc, ident[:])
         tap_bias = keep.tile([P, ENTRIES, HEADS], F32, name="tap_bias")
         bypass = keep.tile([P, HEADS], F32, name="bypass")
+        gains_raw = keep.tile([P, TILES, HEADS, SCALES], BF16, name="gains_raw")
         q_tok = keep.tile([P, TILES, WIDTH], F32, name="q_tok")
         k_t = keep.tile([P, HIGH, PAD + TOKENS], F32, name="k_t")
-        v_t = keep.tile([P, HIGH, PAD + TOKENS], F32, name="v_t")
         nc.vector.memset(k_t[:, :, 0:PAD], 0.0)
-        nc.vector.memset(v_t[:, :, 0:PAD], 0.0)
         with tc.tile_pool(name="bias", bufs=1) as bias:
-            bias_col = bias.tile([P, CHUNKS], F32, name="bias_col")
-            bias_row = bias.tile([P, WIDTH], F32, name="bias_row")
-            load_tables(tc, ident, b_qkv, pos_bias, identity_bypass, bias_col, bias_row, tap_bias, bypass)
-            project(tc, ident, x.flatten_outer_dims(), W_qkv_words, W_qkv_scales, bias_col, bias_row, q_tok, k_t, v_t)
-        attend(tc, ident, q_tok, k_t, v_t, gains, tap_bias, bypass, out.flatten_outer_dims())
+            bias_k = bias.tile([P, HIGH], F32, name="bias_k")
+            bias_q = bias.tile([P, WIDTH], F32, name="bias_q")
+            bias_v = bias.tile([P, WIDTH], F32, name="bias_v")
+            load_tables(
+                tc, ident, b_qkv, pos_bias, identity_bypass, gains, bias_k, bias_q, bias_v, tap_bias, bypass, gains_raw
+            )
+            project(tc, ident, x.flatten_outer_dims(), W_qkv_words, W_qkv_scales, bias_k, bias_q, bias_v, q_tok, k_t, out_rows)
+        attend(tc, ident, q_tok, k_t, out_rows, gains_raw, tap_bias, bypass)

@@ -207,27 +207,27 @@ def project(tc, ident, x_rows, w_words, w_scales, bias_k, bias_q, bias_v, q_tok,
                 v_tok = stage.tile([P, WIDTH], F32, name="v_tok", bufs=3)
                 tokens_by_features(t, w_codes, w_planes, V_AT, bias_v, v_tok)
                 nc.sync.dma_start(out=v_rows[t * P : (t + 1) * P, :], in_=v_tok[:])
-            token_cols = slice(block * BLOCK, (block + 1) * BLOCK)
-            for a in range(HIGH):
-                column = K_AT + a * P
-                product = psum.tile([P, BLOCK], F32, name="product", bufs=4)
-                for g in range(PASSES):
-                    nc.tensor.matmul_mx(
-                        out=product[:],
-                        lhsT=sorted_codes[:, g, 2 * column : 2 * (column + P)].bitcast(FP4X4),
-                        lhsT_scale=sorted_planes[:, g, column : column + P],
-                        rhs=x_codes[:, g, token_cols].bitcast(FP8X4),
-                        rhs_scale=x_planes[:, g, token_cols],
-                        start=(g == 0),
-                        stop=(g == PASSES - 1),
+                for bank in range(HALVES):
+                    slices = slice(bank * PER_BANK, (bank + 1) * PER_BANK)
+                    product = psum.tile([P, PER_BANK, P], F32, name="product", bufs=4)
+                    for i in range(PER_BANK):
+                        column = K_AT + (bank * PER_BANK + i) * P
+                        for g in range(PASSES):
+                            nc.tensor.matmul_mx(
+                                out=product[:, i, :],
+                                lhsT=sorted_codes[:, g, 2 * column : 2 * (column + P)].bitcast(FP4X4),
+                                lhsT_scale=sorted_planes[:, g, column : column + P],
+                                rhs=x_codes[:, g, t * P : (t + 1) * P].bitcast(FP8X4),
+                                rhs_scale=x_planes[:, g, t * P : (t + 1) * P],
+                                start=(g == 0),
+                                stop=(g == PASSES - 1),
+                            )
+                    nc.vector.tensor_tensor(
+                        out=k_t[:, PAD + t * P : PAD + (t + 1) * P, slices],
+                        in0=product[:].rearrange("p a n -> p n a"),
+                        in1=bias_k[:, slices].unsqueeze(1).to_broadcast([P, P, PER_BANK]),
+                        op=ALU.add,
                     )
-                nc.scalar.activation(
-                    out=k_t[:, a, PAD + block * BLOCK : PAD + (block + 1) * BLOCK],
-                    in_=product[:],
-                    func=ACT.Identity,
-                    bias=bias_k[:, a : a + 1],
-                    scale=1.0,
-                )
 
 
 def attend(tc, ident, q_tok, k_t, v_rows, gains_raw, tap_bias, bypass):
@@ -263,13 +263,15 @@ def attend(tc, ident, q_tok, k_t, v_rows, gains_raw, tap_bias, bypass):
                 )
 
         def copy_q(t):
-            q_sb = work.tile([P, HIGH, P], F32, name="q_sb")
+            q_sb = work.tile([P, P, HIGH], F32, name="q_sb")
             for bank in range(HALVES):
                 staged = psum.tile([P, PER_BANK, P], F32, name="staged", tag="dots_ps", bufs=2)
                 for i in range(PER_BANK):
                     a = bank * PER_BANK + i
                     nc.tensor.transpose(out=staged[:, i, :], in_=q_tok[:, t, a * P : (a + 1) * P], identity=ident[:])
-                nc.scalar.copy(out=q_sb[:, bank * PER_BANK : (bank + 1) * PER_BANK, :], in_=staged[:])
+                nc.scalar.copy(
+                    out=q_sb[:, :, bank * PER_BANK : (bank + 1) * PER_BANK], in_=staged[:].rearrange("p a n -> p n a")
+                )
             q_sb_of[t] = q_sb
 
         def scale_gains(t):
@@ -298,24 +300,22 @@ def attend(tc, ident, q_tok, k_t, v_rows, gains_raw, tap_bias, bypass):
             for slot in slots:
                 first = PAD + t * P - OFFSETS[slot]
                 if slot % TURNS not in VECTOR_TURNS:
-                    prod = work.tile([P, HIGH, P], F32, name="prod_gpsimd", bufs=4)
+                    prod = work.tile([P, P, HIGH], F32, name="prod_gpsimd", bufs=4)
                     nc.gpsimd.tensor_tensor(
-                        out=prod[:], in0=q_sb_of[t][:], in1=k_t[:, :, first : first + P], op=ALU.mult
+                        out=prod[:], in0=q_sb_of[t][:], in1=k_t[:, first : first + P, :], op=ALU.mult
                     )
                 else:
-                    prod = work.tile([P, HIGH, P], F32, name="prod_vector")
+                    prod = work.tile([P, P, HIGH], F32, name="prod_vector")
                     for bank in range(HALVES):
                         slices = slice(bank * PER_BANK, (bank + 1) * PER_BANK)
                         nc.vector.tensor_tensor(
-                            out=prod[:, slices, :],
-                            in0=k_t[:, slices, first : first + P],
-                            in1=q_ps_of[t][bank][:],
+                            out=prod[:, :, slices],
+                            in0=k_t[:, first : first + P, slices],
+                            in1=q_ps_of[t][bank][:].rearrange("p a n -> p n a"),
                             op=ALU.mult,
                         )
                 folded = work.tile([P, P], F32, name="folded", bufs=4)
-                nc.vector.tensor_reduce(
-                    out=folded[:], in_=prod[:].rearrange("p a n -> p n a"), axis=AXIS.X, op=ALU.add
-                )
+                nc.vector.tensor_reduce(out=folded[:], in_=prod[:], axis=AXIS.X, op=ALU.add)
                 nc.tensor.matmul(out=dots_of[t][:, slot, :], lhsT=folded[:], rhs=head_of[:], start=True, stop=True)
 
         def score_entries(t):
@@ -472,8 +472,8 @@ def tile_dwarfattention_pa_kernel(
         bypass = keep.tile([P, HEADS], F32, name="bypass")
         gains_raw = keep.tile([P, TILES, HEADS, SCALES], BF16, name="gains_raw")
         q_tok = keep.tile([P, TILES, WIDTH], F32, name="q_tok")
-        k_t = keep.tile([P, HIGH, PAD + TOKENS], F32, name="k_t")
-        nc.vector.memset(k_t[:, :, 0:PAD], 0.0)
+        k_t = keep.tile([P, PAD + TOKENS, HIGH], F32, name="k_t")
+        nc.vector.memset(k_t[:, 0:PAD, :], 0.0)
         with tc.tile_pool(name="bias", bufs=1) as bias:
             bias_k = bias.tile([P, HIGH], F32, name="bias_k")
             bias_q = bias.tile([P, WIDTH], F32, name="bias_q")

@@ -46,6 +46,7 @@ assert all(OFFSETS[2 * i] == 1 << i for i in range(1, 11))
 assert all(OFFSETS[2 * i + 1] == 3 << (i - 1) for i in range(1, 10))
 GROUP = 4
 GROUPS = (SLOTS + GROUP - 1) // GROUP
+GAIN_RUN = 6
 VECTOR_TURNS = (2, 5)
 TURNS = 7
 
@@ -110,8 +111,24 @@ def load_tables(tc, ident, b_qkv, pos_bias, identity_bypass, gains, bias_k, bias
             out=bypass[:], in0=bypass_f32[:], scalar=0.0, in1=tail[:], op0=ALU.max, op1=ALU.add
         )
 
-    for t in range(TILES):
-        nc.gpsimd.dma_start(out=gains_raw[:, t], in_=gains[0, :, t * P : (t + 1) * P, :].rearrange("h n j -> n h j"))
+        ident_bf16 = setup.tile([P, P], BF16, name="ident_bf16")
+        make_identity(nc, ident_bf16[:])
+        gain_rows = gains.rearrange("b h (t n) j -> (b h t) (n j)", n=P)
+        for first_row in (0, HEADS * TILES - P):
+            new = 0 if first_row == 0 else P - first_row
+            by_row = setup.tile([P, P * SCALES], BF16, name="by_row%d" % first_row)
+            nc.sync.dma_start(out=by_row[:], in_=gain_rows[first_row : first_row + P, :])
+            for j0 in range(0, SCALES, GAIN_RUN):
+                count = min(GAIN_RUN, SCALES - j0)
+                by_token = psum.tile([P, GAIN_RUN, P], BF16, name="by_token")
+                for j in range(j0, j0 + count):
+                    nc.tensor.transpose(
+                        out=by_token[:, j - j0, :], in_=by_row[:, j : P * SCALES : SCALES], identity=ident_bf16[:]
+                    )
+                nc.vector.tensor_copy(
+                    out=gains_raw[:, first_row + new : first_row + P, j0 : j0 + count],
+                    in_=by_token[:, 0:count, new:P].rearrange("p j r -> p r j"),
+                )
 
 
 def project(tc, ident, x_rows, w_words, w_scales, bias_k, bias_q, bias_v, q_tok, k_t, v_rows):
@@ -275,7 +292,7 @@ def attend(tc, ident, q_tok, k_t, v_rows, gains_raw, tap_bias, bypass):
             q_sb_of[t] = q_sb
 
         def scale_gains(t):
-            by_scale = gains_raw[:, t].rearrange("p h j -> p j h")
+            by_scale = gains_raw[:].rearrange("p (h t) j -> p t j h", t=TILES)[:, t]
             gain = taps.tile([P, ENTRIES, HEADS], F32, name="gain")
             for first, count, j0, tau in ENTRY_RUNS:
                 nc.scalar.mul(out=gain[:, first : first + count, :], in_=by_scale[:, j0 : j0 + count, :], mul=D4[tau])
@@ -470,7 +487,7 @@ def tile_dwarfattention_pa_kernel(
         make_identity(nc, ident[:])
         tap_bias = keep.tile([P, ENTRIES, HEADS], F32, name="tap_bias")
         bypass = keep.tile([P, HEADS], F32, name="bypass")
-        gains_raw = keep.tile([P, TILES, HEADS, SCALES], BF16, name="gains_raw")
+        gains_raw = keep.tile([P, HEADS * TILES, SCALES], BF16, name="gains_raw")
         q_tok = keep.tile([P, TILES, WIDTH], F32, name="q_tok")
         k_t = keep.tile([P, PAD + TOKENS, HIGH], F32, name="k_t")
         nc.vector.memset(k_t[:, 0:PAD, :], 0.0)

@@ -259,7 +259,9 @@ def attend(tc, ident, q_tok, k_t, v_rows, gains_raw, tap_bias, bypass):
         gain_of = {}
         dots_of = {}
         score_of = {}
+        term_of = {}
         weight_of = {}
+        inv_z_of = {}
         sum_of = {}
         rows_of = {}
 
@@ -295,7 +297,7 @@ def attend(tc, ident, q_tok, k_t, v_rows, gains_raw, tap_bias, bypass):
             by_scale = gains_raw[:].rearrange("p (h t) j -> p t j h", t=TILES)[:, t]
             gain = taps.tile([P, ENTRIES, HEADS], F32, name="gain")
             for first, count, j0, tau in ENTRY_RUNS:
-                nc.scalar.mul(out=gain[:, first : first + count, :], in_=by_scale[:, j0 : j0 + count, :], mul=D4[tau])
+                nc.scalar.mul(out=gain[:, first : first + count, :], in_=by_scale[:, j0 : j0 + count, :], mul=abs(D4[tau]))
             nc.scalar.copy(out=gain[:, LOCAL, :], in_=bypass[:])
             gain_of[t] = gain
 
@@ -369,37 +371,30 @@ def attend(tc, ident, q_tok, k_t, v_rows, gains_raw, tap_bias, bypass):
             )
             term = taps.tile([P, ENTRIES, HEADS], F32, name="term", bufs=1)
             nc.vector.tensor_tensor(out=term[:], in0=feat[:], in1=gain_of[t][:], op=ALU.mult)
-
-            def sum_entries(name, first, last):
-                total = taps.tile([P, HEADS], F32, name=name)
-                nc.vector.tensor_reduce(
-                    out=total[:], in_=term[:, first:last, :].rearrange("p e h -> p h e"), axis=AXIS.X, op=ALU.add
-                )
-                return total
-
-            here = sum_entries("here", 0, HERE)
-            positive = sum_entries("positive", HERE, NEGATIVE_FIRST)
-            negative = sum_entries("negative", NEGATIVE_FIRST, ENTRIES)
-            z = taps.tile([P, HEADS], F32, name="z")
-            nc.vector.scalar_tensor_tensor(
-                out=z[:], in0=here[:], scalar=1e-6, in1=positive[:], op0=ALU.add, op1=ALU.add
-            )
-            nc.vector.tensor_tensor(out=z[:], in0=z[:], in1=negative[:], op=ALU.subtract)
-            inv_z = taps.tile([P, HEADS], F32, name="inv_z")
-            nc.vector.reciprocal(out=inv_z[:], in_=z[:])
-            inv_z_rows = inv_z[:].unsqueeze(1).to_broadcast([P, EVEN, HEADS])
-
             weight = taps.tile([P, SLOTS, HEADS], F32, name="weight")
-            nc.vector.tensor_tensor(out=weight[:, 0, :], in0=here[:], in1=inv_z[:], op=ALU.mult)
-            both = taps.tile([P, EVEN, HEADS], F32, name="both")
-            nc.vector.tensor_tensor(
-                out=both[:], in0=term[:, HERE : HERE + EVEN, :], in1=term[:, HERE + EVEN : ODD_FIRST, :], op=ALU.add
+            nc.vector.tensor_reduce(
+                out=weight[:, 0, :], in_=term[:, 0:HERE, :].rearrange("p e h -> p h e"), axis=AXIS.X, op=ALU.add
             )
-            nc.vector.tensor_tensor(out=weight[:, 2:SLOTS:2, :], in0=both[:], in1=inv_z_rows, op=ALU.mult)
-            nc.vector.tensor_tensor(
-                out=weight[:, 1:SLOTS:2, :], in0=term[:, ODD_FIRST:ENTRIES, :], in1=inv_z_rows, op=ALU.mult
+            nc.vector.tensor_reduce(
+                out=weight[:, 2:SLOTS:2, :],
+                in_=term[:, HERE:ODD_FIRST, :].rearrange("p (c e) h -> p e h c", c=2),
+                axis=AXIS.X,
+                op=ALU.add,
             )
+            z = taps.tile([P, HEADS], F32, name="z")
+            nc.vector.tensor_reduce(out=z[:], in_=term[:].rearrange("p e h -> p h e"), axis=AXIS.X, op=ALU.add)
             weight_of[t] = weight
+            term_of[t] = (term, z)
+
+        def sign_weights(t):
+            term, z = term_of[t]
+            nc.scalar.copy(out=weight_of[t][:, 1, :], in_=term[:, ODD_FIRST, :])
+            nc.scalar.mul(out=weight_of[t][:, 3:SLOTS:2, :], in_=term[:, NEGATIVE_FIRST:ENTRIES, :], mul=-1.0)
+            z_safe = taps.tile([P, HEADS], F32, name="z_safe")
+            nc.scalar.activation(out=z_safe[:], in_=z[:], func=ACT.Identity, bias=1e-6)
+            inv_z = taps.tile([P, HEADS], F32, name="inv_z")
+            nc.vector.reciprocal(out=inv_z[:], in_=z_safe[:])
+            inv_z_of[t] = inv_z
 
         def multiply_w_v(t, group):
             slots = slots_of(t, group)
@@ -443,9 +438,13 @@ def attend(tc, ident, q_tok, k_t, v_rows, gains_raw, tap_bias, bypass):
                 rows_ps = psum.tile([P, PER_BANK, P], F32, name="rows_ps%d" % bank)
                 for i in range(PER_BANK):
                     nc.tensor.transpose(out=rows_ps[:, i, :], in_=sum_sb[:, bank * PER_BANK + i, :], identity=ident[:])
-                nc.vector.tensor_copy(
-                    out=rows[:, bank * BLOCK : (bank + 1) * BLOCK], in_=rows_ps[:].rearrange("p c f -> p (c f)")
-                )
+                for h in range(bank * HEADS // HALVES, (bank + 1) * HEADS // HALVES):
+                    nc.scalar.activation(
+                        out=rows[:, h * HEAD_DIM : (h + 1) * HEAD_DIM],
+                        in_=rows_ps[:].rearrange("p c f -> p (c f)")[:, h * HEAD_DIM - bank * BLOCK : (h + 1) * HEAD_DIM - bank * BLOCK],
+                        func=ACT.Copy,
+                        scale=inv_z_of[t][:, h : h + 1],
+                    )
             rows_of[t] = rows
 
         def store(t):
@@ -471,6 +470,8 @@ def attend(tc, ident, q_tok, k_t, v_rows, gains_raw, tap_bias, bypass):
                     weigh_entries(weight_tile)
                 if group == 0 and done_tile is not None:
                     store(done_tile)
+                if group == 1 and weight_tile is not None:
+                    sign_weights(weight_tile)
                 if group == GROUPS // 2 and tile_at(step + 1) is not None:
                     copy_q(tile_at(step + 1))
             if out_tile is not None:

@@ -47,8 +47,9 @@ assert all(OFFSETS[2 * i + 1] == 3 << (i - 1) for i in range(1, 10))
 GROUP = 4
 GROUPS = (SLOTS + GROUP - 1) // GROUP
 GAIN_RUN = 6
-VECTOR_TURNS = (2, 5)
-TURNS = 7
+VECTOR_TURNS = (1,)
+TURNS = 3
+DMA_ENGINES = 16
 
 ENTRY_RUNS = [(0, 11, 0, 0), (12, 10, 1, 1), (22, 10, 0, 2), (32, 1, 0, 1), (33, 9, 0, 3)]
 LOCAL = 11
@@ -409,7 +410,10 @@ def attend(tc, ident, q_tok, k_t, v_rows, gains_raw, tap_bias, bypass):
                 shifted = work.tile([P, WIDTH], F32, name="shifted", bufs=6)
                 if missing:
                     nc.vector.memset(shifted[0:missing, :], 0.0)
-                nc.sync.dma_start(out=shifted[missing:P, :], in_=v_rows[first + missing : first + P, :])
+                split = P - (P - missing) % DMA_ENGINES
+                for low, high in ((missing, split), (split, P)):
+                    if low < high:
+                        nc.sync.dma_start(out=shifted[low:high, :], in_=v_rows[first + low : first + high, :])
                 scaled = work.tile([P, WIDTH], F32, name="scaled", bufs=4)
                 for h in range(HEADS):
                     features = slice(h * HEAD_DIM, (h + 1) * HEAD_DIM)
@@ -454,24 +458,23 @@ def attend(tc, ident, q_tok, k_t, v_rows, gains_raw, tap_bias, bypass):
             return TILES - 1 - step if 0 <= step < TILES else None
 
         copy_q(tile_at(0))
-        for step in range(TILES + 3):
-            dot_tile, weight_tile, out_tile, done_tile = [tile_at(step - lag) for lag in range(4)]
+        for step in range(TILES + 2):
+            dot_tile, out_tile, done_tile = [tile_at(step - lag) for lag in range(3)]
             if dot_tile is not None:
                 scale_gains(dot_tile)
                 turn_q(dot_tile)
-            if weight_tile is not None:
-                score_entries(weight_tile)
-            for group in range(GROUPS):
-                if dot_tile is not None:
+            if out_tile is not None:
+                score_entries(out_tile)
+            for group in range(GROUPS + 1):
+                if dot_tile is not None and group < GROUPS:
                     multiply_q_k(dot_tile, group)
-                if out_tile is not None:
-                    multiply_w_v(out_tile, group)
-                if group == 0 and weight_tile is not None:
-                    weigh_entries(weight_tile)
-                if group == 0 and done_tile is not None:
+                if group == 0 and out_tile is not None:
+                    weigh_entries(out_tile)
+                    sign_weights(out_tile)
+                if group > 0 and out_tile is not None:
+                    multiply_w_v(out_tile, group - 1)
+                if group == 1 and done_tile is not None:
                     store(done_tile)
-                if group == 1 and weight_tile is not None:
-                    sign_weights(weight_tile)
                 if group == GROUPS // 2 and tile_at(step + 1) is not None:
                     copy_q(tile_at(step + 1))
             if out_tile is not None:

@@ -46,9 +46,11 @@ assert all(OFFSETS[2 * i] == 1 << i for i in range(1, 11))
 assert all(OFFSETS[2 * i + 1] == 3 << (i - 1) for i in range(1, 10))
 GROUP = 4
 GROUPS = (SLOTS + GROUP - 1) // GROUP
+DELAY = GROUPS + 2
+STORE_DELAY = 2
 GAIN_RUN = 6
-VECTOR_TURNS = (1,)
-TURNS = 3
+VECTOR_TURNS = (1, 4, 6)
+TURNS = 8
 DMA_ENGINES = 16
 
 ENTRY_RUNS = [(0, 11, 0, 0), (12, 10, 1, 1), (22, 10, 0, 2), (32, 1, 0, 1), (33, 9, 0, 3)]
@@ -458,27 +460,30 @@ def attend(tc, ident, q_tok, k_t, v_rows, gains_raw, tap_bias, bypass):
             return TILES - 1 - step if 0 <= step < TILES else None
 
         copy_q(tile_at(0))
-        for step in range(TILES + 2):
-            dot_tile, out_tile, done_tile = [tile_at(step - lag) for lag in range(3)]
-            if dot_tile is not None:
+        for tick in range(TILES * GROUPS + DELAY + STORE_DELAY):
+            step, group = divmod(tick, GROUPS)
+            dot_tile, weight_tile = tile_at(step), tile_at(step - 1)
+            if group == 0 and dot_tile is not None:
                 scale_gains(dot_tile)
                 turn_q(dot_tile)
-            if out_tile is not None:
-                score_entries(out_tile)
-            for group in range(GROUPS + 1):
-                if dot_tile is not None and group < GROUPS:
-                    multiply_q_k(dot_tile, group)
-                if group == 0 and out_tile is not None:
-                    weigh_entries(out_tile)
-                    sign_weights(out_tile)
-                if group > 0 and out_tile is not None:
-                    multiply_w_v(out_tile, group - 1)
-                if group == 1 and done_tile is not None:
-                    store(done_tile)
-                if group == GROUPS // 2 and tile_at(step + 1) is not None:
-                    copy_q(tile_at(step + 1))
-            if out_tile is not None:
-                finish_output(out_tile)
+            if group == 0 and weight_tile is not None:
+                score_entries(weight_tile)
+            if dot_tile is not None:
+                multiply_q_k(dot_tile, group)
+            out_step, out_group = divmod(tick - DELAY, GROUPS)
+            if tile_at(out_step) is not None:
+                multiply_w_v(tile_at(out_step), out_group)
+                if out_group == GROUPS - 1:
+                    finish_output(tile_at(out_step))
+            if group == 0 and weight_tile is not None:
+                weigh_entries(weight_tile)
+            if group == DELAY - GROUPS - 1 and weight_tile is not None:
+                sign_weights(weight_tile)
+            done_step, done_group = divmod(tick - DELAY - STORE_DELAY, GROUPS)
+            if done_group == GROUPS - 1 and tile_at(done_step) is not None:
+                store(tile_at(done_step))
+            if group == GROUPS // 2 and tile_at(step + 1) is not None:
+                copy_q(tile_at(step + 1))
 
 
 def tile_dwarfattention_pa_kernel(

@@ -52,6 +52,9 @@ GAIN_RUN = 6
 VECTOR_TURNS = (1, 4, 6)
 TURNS = 8
 DMA_ENGINES = 16
+HELPED_TILE = 0
+FIRST_TILE = TILES - 1
+FIRST_VECTOR_TURNS = (0, 1, 3, 4, 6)
 
 ENTRY_RUNS = [(0, 11, 0, 0), (12, 10, 1, 1), (22, 10, 0, 2), (32, 1, 0, 1), (33, 9, 0, 3)]
 LOCAL = 11
@@ -128,7 +131,7 @@ def load_tables(tc, ident, b_qkv, pos_bias, identity_bypass, gains, bias_k, bias
                     nc.tensor.transpose(
                         out=by_token[:, j - j0, :], in_=by_row[:, j : P * SCALES : SCALES], identity=ident_bf16[:]
                     )
-                nc.vector.tensor_copy(
+                nc.scalar.copy(
                     out=gains_raw[:, first_row + new : first_row + P, j0 : j0 + count],
                     in_=by_token[:, 0:count, new:P].rearrange("p j r -> p r j"),
                 )
@@ -191,12 +194,7 @@ def project(tc, ident, x_rows, w_words, w_scales, bias_k, bias_q, bias_v, q_tok,
                                 in_=x_words[:, words_per_pass * g + u : words_per_pass * (g + 1) : 2],
                                 identity=ident[:],
                             )
-                    if half == 0:
-                        nc.vector.tensor_copy(
-                            out=grouped_words[:, half], in_=turned[:].rearrange("p i u r -> p i r u")
-                        )
-                    else:
-                        nc.scalar.copy(out=grouped_words[:, half], in_=turned[:].rearrange("p i u r -> p i r u"))
+                    nc.scalar.copy(out=grouped_words[:, half], in_=turned[:].rearrange("p i u r -> p i r u"))
                 token_cols = slice(block * BLOCK, (block + 1) * BLOCK)
                 nc.vector.quantize_mx(
                     out=x_codes[:, g, token_cols].bitcast(FP8X4),
@@ -265,6 +263,8 @@ def attend(tc, ident, q_tok, k_t, v_rows, gains_raw, tap_bias, bypass):
         term_of = {}
         weight_of = {}
         inv_z_of = {}
+        normal_of = {}
+        helped_of = {}
         sum_of = {}
         rows_of = {}
 
@@ -308,7 +308,10 @@ def attend(tc, ident, q_tok, k_t, v_rows, gains_raw, tap_bias, bypass):
             slots = slots_of(t, group)
             if not slots:
                 return
-            if group == 0:
+            turned = t == FIRST_TILE
+            if group == 0 and turned:
+                dots_of[t] = taps.tile([P, SLOTS, HEADS], F32, name="dots_sb", bufs=1)
+            if group == 0 and not turned:
                 dots_of[t] = psum.tile([P, SLOTS, HEADS], F32, name="dots_ps", bufs=2)
                 used = sum(len(slots_of(t, g)) for g in range(GROUPS))
                 if used < SLOTS:
@@ -319,9 +322,11 @@ def attend(tc, ident, q_tok, k_t, v_rows, gains_raw, tap_bias, bypass):
                         start=True,
                         stop=True,
                     )
-            for slot in slots:
+            if turned:
+                by_token = psum.tile([P, GROUP, P], F32, name="by_token", tag="dots_ps", bufs=2)
+            for i, slot in enumerate(slots):
                 first = PAD + t * P - OFFSETS[slot]
-                if slot % TURNS not in VECTOR_TURNS:
+                if slot % TURNS not in (FIRST_VECTOR_TURNS if turned else VECTOR_TURNS):
                     prod = work.tile([P, P, HIGH], F32, name="prod_gpsimd", bufs=4)
                     nc.gpsimd.tensor_tensor(
                         out=prod[:], in0=q_sb_of[t][:], in1=k_t[:, first : first + P, :], op=ALU.mult
@@ -336,9 +341,27 @@ def attend(tc, ident, q_tok, k_t, v_rows, gains_raw, tap_bias, bypass):
                             in1=q_ps_of[t][bank][:].rearrange("p a n -> p n a"),
                             op=ALU.mult,
                         )
-                folded = work.tile([P, P], F32, name="folded", bufs=4)
-                nc.vector.tensor_reduce(out=folded[:], in_=prod[:], axis=AXIS.X, op=ALU.add)
-                nc.tensor.matmul(out=dots_of[t][:, slot, :], lhsT=folded[:], rhs=head_of[:], start=True, stop=True)
+                if turned:
+                    for a in range(HIGH):
+                        nc.tensor.matmul(
+                            out=by_token[:, i, :],
+                            lhsT=prod[:, :, a],
+                            rhs=ident[:],
+                            is_transpose=True,
+                            start=(a == 0),
+                            stop=(a == HIGH - 1),
+                        )
+                else:
+                    folded = work.tile([P, P], F32, name="folded", bufs=4)
+                    nc.vector.tensor_reduce(out=folded[:], in_=prod[:], axis=AXIS.X, op=ALU.add)
+                    nc.tensor.matmul(out=dots_of[t][:, slot, :], lhsT=folded[:], rhs=head_of[:], start=True, stop=True)
+            if turned:
+                nc.vector.tensor_reduce(
+                    out=dots_of[t][:, slots[0] : slots[-1] + 1, :],
+                    in_=by_token[:, 0 : len(slots), :].rearrange("p s (h l) -> p s h l", l=LOW),
+                    axis=AXIS.X,
+                    op=ALU.add,
+                )
 
         def score_entries(t):
             dots = dots_of[t]
@@ -398,6 +421,14 @@ def attend(tc, ident, q_tok, k_t, v_rows, gains_raw, tap_bias, bypass):
             inv_z = taps.tile([P, HEADS], F32, name="inv_z")
             nc.vector.reciprocal(out=inv_z[:], in_=z_safe[:])
             inv_z_of[t] = inv_z
+            if t == HELPED_TILE:
+                normal_of[t] = taps.tile([P, EVEN, HEADS], F32, name="normal", bufs=1)
+                nc.vector.tensor_tensor(
+                    out=normal_of[t][:],
+                    in0=weight_of[t][:, 1:SLOTS:2, :],
+                    in1=inv_z[:].unsqueeze(1).to_broadcast([P, EVEN, HEADS]),
+                    op=ALU.mult,
+                )
 
         def multiply_w_v(t, group):
             slots = slots_of(t, group)
@@ -405,7 +436,9 @@ def attend(tc, ident, q_tok, k_t, v_rows, gains_raw, tap_bias, bypass):
                 return
             if group == 0:
                 sum_of[t] = [psum.tile([P, PER_BANK, P], F32, name="sum_ps%d" % bank) for bank in range(HALVES)]
-            last_slot = max(s for g in range(GROUPS) for s in slots_of(t, g))
+            used = [s for g in range(GROUPS) for s in slots_of(t, g)]
+            helped = [s for s in used if t == HELPED_TILE and s % 2 == 1]
+            turned = [s for s in used if s not in helped]
             for slot in slots:
                 first = t * P - OFFSETS[slot]
                 missing = max(0, -first)
@@ -416,24 +449,44 @@ def attend(tc, ident, q_tok, k_t, v_rows, gains_raw, tap_bias, bypass):
                 for low, high in ((missing, split), (split, P)):
                     if low < high:
                         nc.sync.dma_start(out=shifted[low:high, :], in_=v_rows[first + low : first + high, :])
-                scaled = work.tile([P, WIDTH], F32, name="scaled", bufs=4)
-                for h in range(HEADS):
-                    features = slice(h * HEAD_DIM, (h + 1) * HEAD_DIM)
-                    nc.scalar.activation(
-                        out=scaled[:, features],
-                        in_=shifted[:, features],
-                        func=ACT.Copy,
-                        scale=weight_of[t][:, slot, h : h + 1],
-                    )
-                for c in range(WIDTH // P):
-                    nc.tensor.matmul(
-                        out=sum_of[t][c // PER_BANK][:, c % PER_BANK, :],
-                        lhsT=scaled[:, c * P : (c + 1) * P],
-                        rhs=ident[:],
-                        is_transpose=True,
-                        start=(slot == 0 and c % PER_BANK == 0),
-                        stop=(slot == last_slot and c % PER_BANK == PER_BANK - 1),
-                    )
+                if slot in helped:
+                    if slot == helped[0]:
+                        helped_of[t] = work.tile([P, WIDTH], F32, name="helped_sum", bufs=1)
+                    for h in range(HEADS):
+                        features = slice(h * HEAD_DIM, (h + 1) * HEAD_DIM)
+                        share = normal_of[t][:, slot // 2, h : h + 1]
+                        if slot == helped[0]:
+                            nc.vector.tensor_scalar_mul(
+                                out=helped_of[t][:, features], in0=shifted[:, features], scalar1=share
+                            )
+                        else:
+                            nc.vector.scalar_tensor_tensor(
+                                out=helped_of[t][:, features],
+                                in0=shifted[:, features],
+                                scalar=share,
+                                in1=helped_of[t][:, features],
+                                op0=ALU.mult,
+                                op1=ALU.add,
+                            )
+                else:
+                    scaled = work.tile([P, WIDTH], F32, name="scaled", bufs=4)
+                    for h in range(HEADS):
+                        features = slice(h * HEAD_DIM, (h + 1) * HEAD_DIM)
+                        nc.scalar.activation(
+                            out=scaled[:, features],
+                            in_=shifted[:, features],
+                            func=ACT.Copy,
+                            scale=weight_of[t][:, slot, h : h + 1],
+                        )
+                    for c in range(WIDTH // P):
+                        nc.tensor.matmul(
+                            out=sum_of[t][c // PER_BANK][:, c % PER_BANK, :],
+                            lhsT=scaled[:, c * P : (c + 1) * P],
+                            rhs=ident[:],
+                            is_transpose=True,
+                            start=(slot == turned[0] and c % PER_BANK == 0),
+                            stop=(slot == turned[-1] and c % PER_BANK == PER_BANK - 1),
+                        )
 
         def finish_output(t):
             sum_sb = work.tile([P, WIDTH // P, P], F32, name="sum_sb", bufs=1)
@@ -445,12 +498,21 @@ def attend(tc, ident, q_tok, k_t, v_rows, gains_raw, tap_bias, bypass):
                 for i in range(PER_BANK):
                     nc.tensor.transpose(out=rows_ps[:, i, :], in_=sum_sb[:, bank * PER_BANK + i, :], identity=ident[:])
                 for h in range(bank * HEADS // HALVES, (bank + 1) * HEADS // HALVES):
-                    nc.scalar.activation(
-                        out=rows[:, h * HEAD_DIM : (h + 1) * HEAD_DIM],
-                        in_=rows_ps[:].rearrange("p c f -> p (c f)")[:, h * HEAD_DIM - bank * BLOCK : (h + 1) * HEAD_DIM - bank * BLOCK],
-                        func=ACT.Copy,
-                        scale=inv_z_of[t][:, h : h + 1],
-                    )
+                    features = slice(h * HEAD_DIM, (h + 1) * HEAD_DIM)
+                    summed = rows_ps[:].rearrange("p c f -> p (c f)")[:, h * HEAD_DIM - bank * BLOCK : (h + 1) * HEAD_DIM - bank * BLOCK]
+                    if t == HELPED_TILE:
+                        nc.vector.scalar_tensor_tensor(
+                            out=rows[:, features],
+                            in0=summed,
+                            scalar=inv_z_of[t][:, h : h + 1],
+                            in1=helped_of[t][:, features],
+                            op0=ALU.mult,
+                            op1=ALU.add,
+                        )
+                    else:
+                        nc.scalar.activation(
+                            out=rows[:, features], in_=summed, func=ACT.Copy, scale=inv_z_of[t][:, h : h + 1]
+                        )
             rows_of[t] = rows
 
         def store(t):
@@ -499,7 +561,7 @@ def tile_dwarfattention_pa_kernel(
         gains_raw = keep.tile([P, HEADS * TILES, SCALES], BF16, name="gains_raw")
         q_tok = keep.tile([P, TILES, WIDTH], F32, name="q_tok")
         k_t = keep.tile([P, PAD + TOKENS, HIGH], F32, name="k_t")
-        nc.vector.memset(k_t[:, 0:PAD, :], 0.0)
+        nc.gpsimd.memset(k_t[:, 0:PAD, :], 0.0)
         with tc.tile_pool(name="bias", bufs=1) as bias:
             bias_k = bias.tile([P, HIGH], F32, name="bias_k")
             bias_q = bias.tile([P, WIDTH], F32, name="bias_q")

@@ -28,81 +28,85 @@ D4 = [0.4829629131445341, 0.8365163037378079, 0.2241438680420134, -0.12940952255
 PACK = 4
 K_PASS = P * PACK
 PASSES = D_IN // K_PASS
-BLOCK = 512
-BLOCKS = TOKENS // BLOCK
+BANK = 512
 TILES = TOKENS // P
-TILES_PER_BLOCK = BLOCK // P
-HALVES = WIDTH // BLOCK
-PER_BANK = BLOCK // P
-
-LOW = P // HEADS
-HIGH = HEAD_DIM // LOW
+CHUNKS = WIDTH // P
+PER_BANK = BANK // P
+HALVES = CHUNKS // PER_BANK
+HEADS_PER_BANK = HEADS // HALVES
 PAD = P
 
-OFFSETS = sorted(set(tau << j for j in range(SCALES) for tau in range(TAUS) if (tau << j) < TOKENS))
-SLOTS = len(OFFSETS)
-assert OFFSETS[0] == 0 and OFFSETS[1] == 1
-assert all(OFFSETS[2 * i] == 1 << i for i in range(1, 11))
-assert all(OFFSETS[2 * i + 1] == 3 << (i - 1) for i in range(1, 10))
-GROUP = 4
-GROUPS = (SLOTS + GROUP - 1) // GROUP
-DELAY = GROUPS + 2
-STORE_DELAY = 2
-GAIN_RUN = 6
-VECTOR_TURNS = (1, 4, 6)
-TURNS = 8
-DMA_ENGINES = 16
-HELPED_TILE = 0
-FIRST_TILE = TILES - 1
-FIRST_VECTOR_TURNS = (0, 1, 3, 4, 6)
+KEYS = HEAD_DIM
+BLOCKS = TOKENS // KEYS
+NEAR_MAX = KEYS
+ROW = 2 * KEYS * HEADS
+UNIT = P * WIDTH
 
-ENTRY_RUNS = [(0, 11, 0, 0), (12, 10, 1, 1), (22, 10, 0, 2), (32, 1, 0, 1), (33, 9, 0, 3)]
+OFFSETS = sorted(set(tau << j for j in range(SCALES) for tau in range(TAUS) if (tau << j) < TOKENS), reverse=True)
+SLOTS = len(OFFSETS)
+HERE_SLOT = SLOTS - 1
+assert OFFSETS[HERE_SLOT] == 0
+assert all(OFFSETS[2 * i] == 1 << (10 - i) for i in range(10))
+assert all(OFFSETS[2 * i + 1] == 3 << (8 - i) for i in range(9)) and OFFSETS[19] == 1
+FAR_SLOTS = len([o for o in OFFSETS if o > NEAR_MAX])
+NEAR_RUNS = [(8, 2, 16), (10, 2, 8), (12, 2, 4), (14, 2, 2), (16, 5, 1)]
+
+V_SLOTS = 5
+GAIN_RUN = 6
+DMA_ENGINES = 16
+
+ENTRY_RUNS = [(0, 11, 0, 0), (12, 10, 0, 1), (22, 10, 1, 2), (32, 9, 2, 3), (41, 1, 10, 1)]
 LOCAL = 11
 HERE = 12
 EVEN = 10
 ODD_FIRST = HERE + 2 * EVEN
-NEGATIVE_FIRST = ODD_FIRST + 1
 ENTRIES = ODD_FIRST + EVEN
+LAST = ENTRIES - 1
 
 FLOPS = 2 * TOKENS * D_IN * 3 * WIDTH + 4 * TOKENS * WIDTH * ENTRIES
 
 
-def slots_of(tile_index, group):
-    last_token = tile_index * P + P - 1
-    return [s for s in range(group * GROUP, min((group + 1) * GROUP, SLOTS)) if OFFSETS[s] <= last_token]
+def slots_of(t):
+    return [i for i in range(SLOTS) if OFFSETS[i] <= t * P + P - 1]
 
 
-def load_tables(tc, ident, b_qkv, pos_bias, identity_bypass, gains, bias_k, bias_q, bias_v, tap_bias, bypass, gains_raw):
+def unit_of(block):
+    return 9 + block % 3 if block < BLOCKS - 3 else (10 if block < BLOCKS - 1 else 11)
+
+
+def weave(streams):
+    done = [0] * len(streams)
+    total = sum(len(s) for s in streams)
+    for n in range(total):
+        pick = min(
+            (i for i in range(len(streams)) if done[i] < len(streams[i])), key=lambda i: (done[i] + 0.5) / len(streams[i])
+        )
+        streams[pick][done[pick]]()
+        done[pick] += 1
+
+
+def load_tables(tc, ident, b_qkv, pos_bias, identity_bypass, gains, bias_qk, bias_v, tap_bias, bypass, gains_raw):
     nc = tc.nc
     with tc.tile_pool(name="setup", bufs=1) as setup, tc.psum_pool(name="setup_ps", bufs=1) as psum:
         bias_rows = setup.tile([P, P], BF16, name="bias_rows")
         nc.vector.memset(bias_rows[:], 0.0)
         nc.sync.dma_start(
-            out=bias_rows[0:HIGH, :].rearrange("a (h l) -> a h l", l=LOW),
-            in_=b_qkv[K_AT : K_AT + WIDTH].rearrange("(h a l) -> a h l", h=HEADS, a=HIGH, l=LOW),
+            out=bias_rows[0 : 2 * CHUNKS, :], in_=b_qkv[Q_AT : Q_AT + 2 * WIDTH].rearrange("(c p) -> c p", p=P)
         )
         bias_rows_f32 = setup.tile([P, P], F32, name="bias_rows_f32")
         nc.vector.tensor_copy(out=bias_rows_f32[:], in_=bias_rows[:])
         bias_ps = psum.tile([P, P], F32, name="bias_ps")
         nc.tensor.transpose(out=bias_ps[:], in_=bias_rows_f32[:], identity=ident[:])
-        nc.vector.tensor_copy(out=bias_k[:], in_=bias_ps[:, 0:HIGH])
-
-        bias_q_raw = setup.tile([P, WIDTH], BF16, name="bias_q_raw")
-        nc.sync.dma_start(out=bias_q_raw[:], in_=b_qkv[Q_AT : Q_AT + WIDTH].partition_broadcast(P))
-        nc.vector.tensor_copy(
-            out=bias_q[:].rearrange("p (a h l) -> p a h l", a=HIGH, h=HEADS),
-            in_=bias_q_raw[:].rearrange("p (h a l) -> p a h l", h=HEADS, a=HIGH),
-        )
-        bias_v_raw = setup.tile([P, WIDTH], BF16, name="bias_v_raw")
-        nc.sync.dma_start(out=bias_v_raw[:], in_=b_qkv[V_AT : V_AT + WIDTH].partition_broadcast(P))
-        nc.vector.tensor_copy(out=bias_v[:], in_=bias_v_raw[:])
+        nc.vector.tensor_copy(out=bias_qk[:], in_=bias_ps[:, 0 : 2 * CHUNKS])
+        nc.sync.dma_start(out=bias_v[:], in_=b_qkv[V_AT : V_AT + WIDTH].partition_broadcast(P))
 
         pos_raw = setup.tile([P, SCALES * TAUS * HEADS], BF16, name="pos_raw")
         nc.sync.dma_start(out=pos_raw[:], in_=pos_bias.rearrange("r h -> (r h)").partition_broadcast(P))
         pos_view = pos_raw[:].rearrange("p (j t h) -> p j t h", t=TAUS, h=HEADS)
-        nc.vector.memset(tap_bias[:, LOCAL, :], 0.0)
-        for first, count, j0, tau in ENTRY_RUNS:
-            nc.vector.tensor_copy(out=tap_bias[:, first : first + count, :], in_=pos_view[:, j0 : j0 + count, tau, :])
+        nc.gpsimd.memset(tap_bias[:, LOCAL, :], 0.0)
+        for first, count, s0, tau in ENTRY_RUNS:
+            for e in range(count):
+                nc.gpsimd.tensor_copy(out=tap_bias[:, first + e, :], in_=pos_view[:, SCALES - 1 - s0 - e, tau, :])
 
         bypass_raw = setup.tile([P, HEADS], BF16, name="bypass_raw")
         nc.sync.dma_start(out=bypass_raw[:], in_=identity_bypass.partition_broadcast(P))
@@ -129,423 +133,15 @@ def load_tables(tc, ident, b_qkv, pos_bias, identity_bypass, gains, bias_k, bias
                 by_token = psum.tile([P, GAIN_RUN, P], BF16, name="by_token")
                 for j in range(j0, j0 + count):
                     nc.tensor.transpose(
-                        out=by_token[:, j - j0, :], in_=by_row[:, j : P * SCALES : SCALES], identity=ident_bf16[:]
+                        out=by_token[:, j0 + count - 1 - j, :],
+                        in_=by_row[:, j : P * SCALES : SCALES],
+                        identity=ident_bf16[:],
                     )
+                s0 = SCALES - j0 - count
                 nc.scalar.copy(
-                    out=gains_raw[:, first_row + new : first_row + P, j0 : j0 + count],
+                    out=gains_raw[:, first_row + new : first_row + P, s0 : s0 + count],
                     in_=by_token[:, 0:count, new:P].rearrange("p j r -> p r j"),
                 )
-
-
-def project(tc, ident, x_rows, w_words, w_scales, bias_k, bias_q, bias_v, q_tok, k_t, v_rows):
-    nc = tc.nc
-    with (
-        tc.tile_pool(name="mx", bufs=1) as mx,
-        tc.tile_pool(name="stage", bufs=2) as stage,
-        tc.psum_pool(name="mx_ps", bufs=2) as psum,
-    ):
-        w_planes = mx.tile([P, PASSES, 3 * WIDTH], U8, name="w_planes", align_bytes=64)
-        nc.vector.memset(w_planes[:].bitcast(I32), 0)
-        for quadrant in range(4):
-            nc.sync.dma_start(
-                out=w_planes[32 * quadrant : 32 * quadrant + 4, :, :].bitcast(I32),
-                in_=w_scales[:, 4 * quadrant : 4 * quadrant + 4, :].bitcast(I32).rearrange("g r n -> r g n"),
-            )
-        w_codes = mx.tile([P, PASSES, 2 * 3 * WIDTH], U8, name="w_codes", align_bytes=64)
-        sorted_planes = mx.tile([P, PASSES, 2 * WIDTH], U8, name="sorted_planes", align_bytes=64)
-        sorted_codes = mx.tile([P, PASSES, 2 * 2 * WIDTH], U8, name="sorted_codes", align_bytes=64)
-
-        def sort_columns(sorted_bytes, given_bytes):
-            nc.vector.tensor_copy(
-                out=sorted_bytes.bitcast(I32).rearrange("p (a h w) -> p a h w", a=HIGH, h=HEADS),
-                in_=given_bytes.bitcast(I32).rearrange("p (h a w) -> p a h w", h=HEADS, a=HIGH),
-            )
-
-        x_codes = mx.tile([P, PASSES, TOKENS], U32, name="x_codes", align_bytes=64)
-        x_planes = mx.tile([P, PASSES, TOKENS], U8, name="x_planes", align_bytes=64)
-        words_per_pass = K_PASS // 2
-        for block in range(BLOCKS):
-            x_sb = stage.tile([P, TILES_PER_BLOCK, D_IN], BF16, name="x_sb")
-            nc.sync.dma_start(
-                out=x_sb[:],
-                in_=x_rows[block * BLOCK : (block + 1) * BLOCK, :].rearrange("(t p) k -> p t k", p=P),
-            )
-            if block == 0:
-                for g in range(PASSES):
-                    nc.sync.dma_start(out=w_codes[:, g, :].bitcast(I32), in_=w_words[g].bitcast(I32))
-                    for at in (Q_AT, K_AT):
-                        sort_columns(sorted_codes[:, g, 2 * at : 2 * (at + WIDTH)], w_codes[:, g, 2 * at : 2 * (at + WIDTH)])
-                        sort_columns(sorted_planes[:, g, at : at + WIDTH], w_planes[:, g, at : at + WIDTH])
-            for g in range(PASSES):
-                grouped = stage.tile([P, BLOCK, PACK], BF16, name="grouped", align_bytes=64)
-                grouped_words = (
-                    grouped[:]
-                    .rearrange("p r t -> p (r t)")
-                    .bitcast(F32)
-                    .rearrange("p (s i r u) -> p s i r u", s=2, i=2, u=2)
-                )
-                for half in range(2):
-                    turned = psum.tile([P, 2, 2, P], F32, name="turned")
-                    for i in range(2):
-                        x_words = x_sb[:, 2 * half + i, :].bitcast(F32)
-                        for u in range(2):
-                            nc.tensor.transpose(
-                                out=turned[:, i, u, :],
-                                in_=x_words[:, words_per_pass * g + u : words_per_pass * (g + 1) : 2],
-                                identity=ident[:],
-                            )
-                    nc.scalar.copy(out=grouped_words[:, half], in_=turned[:].rearrange("p i u r -> p i r u"))
-                token_cols = slice(block * BLOCK, (block + 1) * BLOCK)
-                nc.vector.quantize_mx(
-                    out=x_codes[:, g, token_cols].bitcast(FP8X4),
-                    scales=x_planes[:, g, token_cols],
-                    in_=grouped[:].rearrange("p r t -> p (r t)"),
-                )
-
-        def tokens_by_features(t, codes, planes, at, bias_row, home):
-            for half in range(HALVES):
-                column = at + half * BLOCK
-                product = psum.tile([P, BLOCK], F32, name="product", bufs=4)
-                for g in range(PASSES):
-                    nc.tensor.matmul_mx(
-                        out=product[:],
-                        lhsT=x_codes[:, g, t * P : (t + 1) * P].bitcast(FP8X4),
-                        lhsT_scale=x_planes[:, g, t * P : (t + 1) * P],
-                        rhs=codes[:, g, 2 * column : 2 * (column + BLOCK)].bitcast(FP4X4),
-                        rhs_scale=planes[:, g, column : column + BLOCK],
-                        start=(g == 0),
-                        stop=(g == PASSES - 1),
-                    )
-                features = slice(half * BLOCK, (half + 1) * BLOCK)
-                nc.vector.tensor_tensor(out=home[:, features], in0=product[:], in1=bias_row[:, features], op=ALU.add)
-
-        for block in range(BLOCKS):
-            for t in range(block * TILES_PER_BLOCK, (block + 1) * TILES_PER_BLOCK):
-                tokens_by_features(t, sorted_codes, sorted_planes, Q_AT, bias_q, q_tok[:, t, :])
-                v_tok = stage.tile([P, WIDTH], F32, name="v_tok", bufs=3)
-                tokens_by_features(t, w_codes, w_planes, V_AT, bias_v, v_tok)
-                nc.sync.dma_start(out=v_rows[t * P : (t + 1) * P, :], in_=v_tok[:])
-                for bank in range(HALVES):
-                    slices = slice(bank * PER_BANK, (bank + 1) * PER_BANK)
-                    product = psum.tile([P, PER_BANK, P], F32, name="product", bufs=4)
-                    for i in range(PER_BANK):
-                        column = K_AT + (bank * PER_BANK + i) * P
-                        for g in range(PASSES):
-                            nc.tensor.matmul_mx(
-                                out=product[:, i, :],
-                                lhsT=sorted_codes[:, g, 2 * column : 2 * (column + P)].bitcast(FP4X4),
-                                lhsT_scale=sorted_planes[:, g, column : column + P],
-                                rhs=x_codes[:, g, t * P : (t + 1) * P].bitcast(FP8X4),
-                                rhs_scale=x_planes[:, g, t * P : (t + 1) * P],
-                                start=(g == 0),
-                                stop=(g == PASSES - 1),
-                            )
-                    nc.vector.tensor_tensor(
-                        out=k_t[:, PAD + t * P : PAD + (t + 1) * P, slices],
-                        in0=product[:].rearrange("p a n -> p n a"),
-                        in1=bias_k[:, slices].unsqueeze(1).to_broadcast([P, P, PER_BANK]),
-                        op=ALU.add,
-                    )
-
-
-def attend(tc, ident, q_tok, k_t, v_rows, gains_raw, tap_bias, bypass):
-    nc = tc.nc
-    with (
-        tc.tile_pool(name="work", bufs=2) as work,
-        tc.tile_pool(name="taps", bufs=2) as taps,
-        tc.psum_pool(name="att_ps", bufs=1) as psum,
-    ):
-        q_ps_of = {}
-        q_sb_of = {}
-        gain_of = {}
-        dots_of = {}
-        score_of = {}
-        term_of = {}
-        weight_of = {}
-        inv_z_of = {}
-        normal_of = {}
-        helped_of = {}
-        sum_of = {}
-        rows_of = {}
-
-        head_of = taps.tile([P, HEADS], F32, name="head_of", bufs=1)
-        nc.vector.tensor_reduce(
-            out=head_of[:], in_=ident[:].rearrange("p (h l) -> p h l", l=LOW), axis=AXIS.X, op=ALU.add
-        )
-        zeros = taps.tile([P, P], F32, name="zeros", bufs=1)
-        nc.vector.memset(zeros[:], 0.0)
-
-        def turn_q(t):
-            q_ps_of[t] = [psum.tile([P, PER_BANK, P], F32, name="q_ps%d" % bank) for bank in range(HALVES)]
-            for a in range(HIGH):
-                nc.tensor.transpose(
-                    out=q_ps_of[t][a // PER_BANK][:, a % PER_BANK, :],
-                    in_=q_tok[:, t, a * P : (a + 1) * P],
-                    identity=ident[:],
-                )
-
-        def copy_q(t):
-            q_sb = work.tile([P, P, HIGH], F32, name="q_sb")
-            for bank in range(HALVES):
-                staged = psum.tile([P, PER_BANK, P], F32, name="staged", tag="dots_ps", bufs=2)
-                for i in range(PER_BANK):
-                    a = bank * PER_BANK + i
-                    nc.tensor.transpose(out=staged[:, i, :], in_=q_tok[:, t, a * P : (a + 1) * P], identity=ident[:])
-                nc.scalar.copy(
-                    out=q_sb[:, :, bank * PER_BANK : (bank + 1) * PER_BANK], in_=staged[:].rearrange("p a n -> p n a")
-                )
-            q_sb_of[t] = q_sb
-
-        def scale_gains(t):
-            by_scale = gains_raw[:].rearrange("p (h t) j -> p t j h", t=TILES)[:, t]
-            gain = taps.tile([P, ENTRIES, HEADS], F32, name="gain")
-            for first, count, j0, tau in ENTRY_RUNS:
-                nc.scalar.mul(out=gain[:, first : first + count, :], in_=by_scale[:, j0 : j0 + count, :], mul=abs(D4[tau]))
-            nc.scalar.copy(out=gain[:, LOCAL, :], in_=bypass[:])
-            gain_of[t] = gain
-
-        def multiply_q_k(t, group):
-            slots = slots_of(t, group)
-            if not slots:
-                return
-            turned = t == FIRST_TILE
-            if group == 0 and turned:
-                dots_of[t] = taps.tile([P, SLOTS, HEADS], F32, name="dots_sb", bufs=1)
-            if group == 0 and not turned:
-                dots_of[t] = psum.tile([P, SLOTS, HEADS], F32, name="dots_ps", bufs=2)
-                used = sum(len(slots_of(t, g)) for g in range(GROUPS))
-                if used < SLOTS:
-                    nc.tensor.matmul(
-                        out=dots_of[t][:, used:SLOTS, :].rearrange("p s h -> p (s h)"),
-                        lhsT=zeros[:],
-                        rhs=ident[:, 0 : (SLOTS - used) * HEADS],
-                        start=True,
-                        stop=True,
-                    )
-            if turned:
-                by_token = psum.tile([P, GROUP, P], F32, name="by_token", tag="dots_ps", bufs=2)
-            for i, slot in enumerate(slots):
-                first = PAD + t * P - OFFSETS[slot]
-                if slot % TURNS not in (FIRST_VECTOR_TURNS if turned else VECTOR_TURNS):
-                    prod = work.tile([P, P, HIGH], F32, name="prod_gpsimd", bufs=4)
-                    nc.gpsimd.tensor_tensor(
-                        out=prod[:], in0=q_sb_of[t][:], in1=k_t[:, first : first + P, :], op=ALU.mult
-                    )
-                else:
-                    prod = work.tile([P, P, HIGH], F32, name="prod_vector")
-                    for bank in range(HALVES):
-                        slices = slice(bank * PER_BANK, (bank + 1) * PER_BANK)
-                        nc.vector.tensor_tensor(
-                            out=prod[:, :, slices],
-                            in0=k_t[:, first : first + P, slices],
-                            in1=q_ps_of[t][bank][:].rearrange("p a n -> p n a"),
-                            op=ALU.mult,
-                        )
-                if turned:
-                    for a in range(HIGH):
-                        nc.tensor.matmul(
-                            out=by_token[:, i, :],
-                            lhsT=prod[:, :, a],
-                            rhs=ident[:],
-                            is_transpose=True,
-                            start=(a == 0),
-                            stop=(a == HIGH - 1),
-                        )
-                else:
-                    folded = work.tile([P, P], F32, name="folded", bufs=4)
-                    nc.vector.tensor_reduce(out=folded[:], in_=prod[:], axis=AXIS.X, op=ALU.add)
-                    nc.tensor.matmul(out=dots_of[t][:, slot, :], lhsT=folded[:], rhs=head_of[:], start=True, stop=True)
-            if turned:
-                nc.vector.tensor_reduce(
-                    out=dots_of[t][:, slots[0] : slots[-1] + 1, :],
-                    in_=by_token[:, 0 : len(slots), :].rearrange("p s (h l) -> p s h l", l=LOW),
-                    axis=AXIS.X,
-                    op=ALU.add,
-                )
-
-        def score_entries(t):
-            dots = dots_of[t]
-            u = taps.tile([P, ENTRIES, HEADS], F32, name="u", bufs=1)
-            nc.vector.tensor_tensor(
-                out=u[:, 0:HERE, :],
-                in0=dots[:, 0:1, :].to_broadcast([P, HERE, HEADS]),
-                in1=tap_bias[:, 0:HERE, :],
-                op=ALU.add,
-            )
-            nc.vector.tensor_tensor(
-                out=u[:, HERE:ODD_FIRST, :].rearrange("p (c e) h -> p c e h", c=2),
-                in0=dots[:, 2:SLOTS:2, :].unsqueeze(1).to_broadcast([P, 2, EVEN, HEADS]),
-                in1=tap_bias[:, HERE:ODD_FIRST, :].rearrange("p (c e) h -> p c e h", c=2),
-                op=ALU.add,
-            )
-            nc.vector.tensor_tensor(
-                out=u[:, ODD_FIRST:ENTRIES, :],
-                in0=dots[:, 1:SLOTS:2, :],
-                in1=tap_bias[:, ODD_FIRST:ENTRIES, :],
-                op=ALU.add,
-            )
-            decay = taps.tile([P, ENTRIES, HEADS], F32, name="decay", bufs=1)
-            nc.scalar.activation(out=decay[:], in_=u[:], func=ACT.Relu, scale=-1.0)
-            nc.scalar.activation(out=decay[:], in_=decay[:], func=ACT.Exp, scale=-1.0)
-            score_of[t] = (u, decay)
-
-        def weigh_entries(t):
-            u, decay = score_of[t]
-            feat = taps.tile([P, ENTRIES, HEADS], F32, name="feat", bufs=1)
-            nc.vector.scalar_tensor_tensor(
-                out=feat[:], in0=u[:], scalar=0.0, in1=decay[:], op0=ALU.max, op1=ALU.add
-            )
-            term = taps.tile([P, ENTRIES, HEADS], F32, name="term", bufs=1)
-            nc.vector.tensor_tensor(out=term[:], in0=feat[:], in1=gain_of[t][:], op=ALU.mult)
-            weight = taps.tile([P, SLOTS, HEADS], F32, name="weight")
-            nc.vector.tensor_reduce(
-                out=weight[:, 0, :], in_=term[:, 0:HERE, :].rearrange("p e h -> p h e"), axis=AXIS.X, op=ALU.add
-            )
-            nc.vector.tensor_reduce(
-                out=weight[:, 2:SLOTS:2, :],
-                in_=term[:, HERE:ODD_FIRST, :].rearrange("p (c e) h -> p e h c", c=2),
-                axis=AXIS.X,
-                op=ALU.add,
-            )
-            z = taps.tile([P, HEADS], F32, name="z")
-            nc.vector.tensor_reduce(out=z[:], in_=term[:].rearrange("p e h -> p h e"), axis=AXIS.X, op=ALU.add)
-            weight_of[t] = weight
-            term_of[t] = (term, z)
-
-        def sign_weights(t):
-            term, z = term_of[t]
-            nc.scalar.copy(out=weight_of[t][:, 1, :], in_=term[:, ODD_FIRST, :])
-            nc.scalar.mul(out=weight_of[t][:, 3:SLOTS:2, :], in_=term[:, NEGATIVE_FIRST:ENTRIES, :], mul=-1.0)
-            z_safe = taps.tile([P, HEADS], F32, name="z_safe")
-            nc.scalar.activation(out=z_safe[:], in_=z[:], func=ACT.Identity, bias=1e-6)
-            inv_z = taps.tile([P, HEADS], F32, name="inv_z")
-            nc.vector.reciprocal(out=inv_z[:], in_=z_safe[:])
-            inv_z_of[t] = inv_z
-            if t == HELPED_TILE:
-                normal_of[t] = taps.tile([P, EVEN, HEADS], F32, name="normal", bufs=1)
-                nc.vector.tensor_tensor(
-                    out=normal_of[t][:],
-                    in0=weight_of[t][:, 1:SLOTS:2, :],
-                    in1=inv_z[:].unsqueeze(1).to_broadcast([P, EVEN, HEADS]),
-                    op=ALU.mult,
-                )
-
-        def multiply_w_v(t, group):
-            slots = slots_of(t, group)
-            if not slots:
-                return
-            if group == 0:
-                sum_of[t] = [psum.tile([P, PER_BANK, P], F32, name="sum_ps%d" % bank) for bank in range(HALVES)]
-            used = [s for g in range(GROUPS) for s in slots_of(t, g)]
-            helped = [s for s in used if t == HELPED_TILE and s % 2 == 1]
-            turned = [s for s in used if s not in helped]
-            for slot in slots:
-                first = t * P - OFFSETS[slot]
-                missing = max(0, -first)
-                shifted = work.tile([P, WIDTH], F32, name="shifted", bufs=6)
-                if missing:
-                    nc.vector.memset(shifted[0:missing, :], 0.0)
-                split = P - (P - missing) % DMA_ENGINES
-                for low, high in ((missing, split), (split, P)):
-                    if low < high:
-                        nc.sync.dma_start(out=shifted[low:high, :], in_=v_rows[first + low : first + high, :])
-                if slot in helped:
-                    if slot == helped[0]:
-                        helped_of[t] = work.tile([P, WIDTH], F32, name="helped_sum", bufs=1)
-                    for h in range(HEADS):
-                        features = slice(h * HEAD_DIM, (h + 1) * HEAD_DIM)
-                        share = normal_of[t][:, slot // 2, h : h + 1]
-                        if slot == helped[0]:
-                            nc.vector.tensor_scalar_mul(
-                                out=helped_of[t][:, features], in0=shifted[:, features], scalar1=share
-                            )
-                        else:
-                            nc.vector.scalar_tensor_tensor(
-                                out=helped_of[t][:, features],
-                                in0=shifted[:, features],
-                                scalar=share,
-                                in1=helped_of[t][:, features],
-                                op0=ALU.mult,
-                                op1=ALU.add,
-                            )
-                else:
-                    scaled = work.tile([P, WIDTH], F32, name="scaled", bufs=4)
-                    for h in range(HEADS):
-                        features = slice(h * HEAD_DIM, (h + 1) * HEAD_DIM)
-                        nc.scalar.activation(
-                            out=scaled[:, features],
-                            in_=shifted[:, features],
-                            func=ACT.Copy,
-                            scale=weight_of[t][:, slot, h : h + 1],
-                        )
-                    for c in range(WIDTH // P):
-                        nc.tensor.matmul(
-                            out=sum_of[t][c // PER_BANK][:, c % PER_BANK, :],
-                            lhsT=scaled[:, c * P : (c + 1) * P],
-                            rhs=ident[:],
-                            is_transpose=True,
-                            start=(slot == turned[0] and c % PER_BANK == 0),
-                            stop=(slot == turned[-1] and c % PER_BANK == PER_BANK - 1),
-                        )
-
-        def finish_output(t):
-            sum_sb = work.tile([P, WIDTH // P, P], F32, name="sum_sb", bufs=1)
-            for bank in range(HALVES):
-                nc.scalar.copy(out=sum_sb[:, bank * PER_BANK : (bank + 1) * PER_BANK, :], in_=sum_of[t][bank][:])
-            rows = work.tile([P, WIDTH], F32, name="rows")
-            for bank in range(HALVES):
-                rows_ps = psum.tile([P, PER_BANK, P], F32, name="rows_ps%d" % bank)
-                for i in range(PER_BANK):
-                    nc.tensor.transpose(out=rows_ps[:, i, :], in_=sum_sb[:, bank * PER_BANK + i, :], identity=ident[:])
-                for h in range(bank * HEADS // HALVES, (bank + 1) * HEADS // HALVES):
-                    features = slice(h * HEAD_DIM, (h + 1) * HEAD_DIM)
-                    summed = rows_ps[:].rearrange("p c f -> p (c f)")[:, h * HEAD_DIM - bank * BLOCK : (h + 1) * HEAD_DIM - bank * BLOCK]
-                    if t == HELPED_TILE:
-                        nc.vector.scalar_tensor_tensor(
-                            out=rows[:, features],
-                            in0=summed,
-                            scalar=inv_z_of[t][:, h : h + 1],
-                            in1=helped_of[t][:, features],
-                            op0=ALU.mult,
-                            op1=ALU.add,
-                        )
-                    else:
-                        nc.scalar.activation(
-                            out=rows[:, features], in_=summed, func=ACT.Copy, scale=inv_z_of[t][:, h : h + 1]
-                        )
-            rows_of[t] = rows
-
-        def store(t):
-            nc.sync.dma_start(out=v_rows[t * P : (t + 1) * P, :], in_=rows_of[t][:])
-
-        def tile_at(step):
-            return TILES - 1 - step if 0 <= step < TILES else None
-
-        copy_q(tile_at(0))
-        for tick in range(TILES * GROUPS + DELAY + STORE_DELAY):
-            step, group = divmod(tick, GROUPS)
-            dot_tile, weight_tile = tile_at(step), tile_at(step - 1)
-            if group == 0 and dot_tile is not None:
-                scale_gains(dot_tile)
-                turn_q(dot_tile)
-            if group == 0 and weight_tile is not None:
-                score_entries(weight_tile)
-            if dot_tile is not None:
-                multiply_q_k(dot_tile, group)
-            out_step, out_group = divmod(tick - DELAY, GROUPS)
-            if tile_at(out_step) is not None:
-                multiply_w_v(tile_at(out_step), out_group)
-                if out_group == GROUPS - 1:
-                    finish_output(tile_at(out_step))
-            if group == 0 and weight_tile is not None:
-                weigh_entries(weight_tile)
-            if group == DELAY - GROUPS - 1 and weight_tile is not None:
-                sign_weights(weight_tile)
-            done_step, done_group = divmod(tick - DELAY - STORE_DELAY, GROUPS)
-            if done_group == GROUPS - 1 and tile_at(done_step) is not None:
-                store(tile_at(done_step))
-            if group == GROUPS // 2 and tile_at(step + 1) is not None:
-                copy_q(tile_at(step + 1))
 
 
 def tile_dwarfattention_pa_kernel(
@@ -553,21 +149,450 @@ def tile_dwarfattention_pa_kernel(
 ):
     nc = tc.nc
     out_rows = out.flatten_outer_dims()
-    with tc.tile_pool(name="keep", bufs=1) as keep:
+    x_rows = x.flatten_outer_dims()
+    with (
+        tc.tile_pool(name="keep", bufs=1) as keep,
+    ):
         ident = keep.tile([P, P], F32, name="ident")
         make_identity(nc, ident[:])
         tap_bias = keep.tile([P, ENTRIES, HEADS], F32, name="tap_bias")
         bypass = keep.tile([P, HEADS], F32, name="bypass")
+        bias_qk = keep.tile([P, 2 * CHUNKS], F32, name="bias_qk")
+        bias_v = keep.tile([P, WIDTH], BF16, name="bias_v")
         gains_raw = keep.tile([P, HEADS * TILES, SCALES], BF16, name="gains_raw")
-        q_tok = keep.tile([P, TILES, WIDTH], F32, name="q_tok")
-        k_t = keep.tile([P, PAD + TOKENS, HIGH], F32, name="k_t")
-        nc.gpsimd.memset(k_t[:, 0:PAD, :], 0.0)
-        with tc.tile_pool(name="bias", bufs=1) as bias:
-            bias_k = bias.tile([P, HIGH], F32, name="bias_k")
-            bias_q = bias.tile([P, WIDTH], F32, name="bias_q")
-            bias_v = bias.tile([P, WIDTH], F32, name="bias_v")
-            load_tables(
-                tc, ident, b_qkv, pos_bias, identity_bypass, gains, bias_k, bias_q, bias_v, tap_bias, bypass, gains_raw
+        k_all = keep.tile([P, CHUNKS, PAD + TOKENS], F32, name="k_all")
+        nc.gpsimd.memset(k_all[:, :, 0:PAD], 0.0)
+        key_blocks = [keep.tile([P, CHUNKS, 2, KEYS], F32, name="key_block%d" % i) for i in range(3)]
+        for kb in key_blocks:
+            nc.gpsimd.memset(kb[:], 0.0)
+        w_planes = keep.tile([P, PASSES, 3 * WIDTH], U8, name="w_planes", align_bytes=64)
+        nc.vector.memset(w_planes[:].bitcast(I32), 0)
+        for quadrant in range(4):
+            nc.sync.dma_start(
+                out=w_planes[32 * quadrant : 32 * quadrant + 4, :, :].bitcast(I32),
+                in_=W_qkv_scales[:, 4 * quadrant : 4 * quadrant + 4, :].bitcast(I32).rearrange("g r n -> r g n"),
             )
-            project(tc, ident, x.flatten_outer_dims(), W_qkv_words, W_qkv_scales, bias_k, bias_q, bias_v, q_tok, k_t, out_rows)
-        attend(tc, ident, q_tok, k_t, out_rows, gains_raw, tap_bias, bypass)
+        w_codes = keep.tile([P, PASSES, 2 * 3 * WIDTH], U8, name="w_codes", align_bytes=64)
+        for at in (K_AT, Q_AT, V_AT):
+            for g in range(PASSES):
+                nc.sync.dma_start(
+                    out=w_codes[:, g, 2 * at : 2 * (at + WIDTH)].bitcast(I32),
+                    in_=W_qkv_words[g, :, 2 * at : 2 * (at + WIDTH)].bitcast(I32),
+                )
+        load_tables(
+            tc, ident, b_qkv, pos_bias, identity_bypass, gains, bias_qk, bias_v, tap_bias, bypass, gains_raw
+        )
+        stream(
+            tc, ident, x_rows, out_rows, w_codes, w_planes, bias_qk, bias_v, gains_raw, tap_bias, bypass, k_all, key_blocks
+        )
+
+
+def stream(tc, ident, x_rows, out_rows, w_codes, w_planes, bias_qk, bias_v, gains_raw, tap_bias, bypass, k_all, key_blocks):
+    nc = tc.nc
+    with (
+        tc.tile_pool(name="work", bufs=2) as work,
+        tc.tile_pool(name="taps", bufs=1) as taps,
+        tc.psum_pool(name="ps", bufs=1) as psum,
+    ):
+        x_sb_of, codes_of, q_of, near_of, dots_of = {}, {}, {}, {}, {}
+        gain_of, score_of, weight_of, weight_ps_of, term_of, inv_z_of = {}, {}, {}, {}, {}, {}
+        v_of, sum_of, rows_of = {}, {}, {}
+
+        def bank(name, shape):
+            return psum.tile(shape, F32, name=name, tag="bank", bufs=5)
+
+        def load_x(t):
+            x_sb_of[t] = work.tile([P, D_IN], BF16, name="x_sb")
+            nc.sync.dma_start(out=x_sb_of[t][:], in_=x_rows[t * P : (t + 1) * P, :])
+
+        def quantise_x(t):
+            turned = bank("turned", [P, PASSES, 2, P])
+            words = x_sb_of[t][:].bitcast(F32)
+            per_pass = K_PASS // 2
+            for g in range(PASSES):
+                for u in range(2):
+                    nc.tensor.transpose(
+                        out=turned[:, g, u, :], in_=words[:, per_pass * g + u : per_pass * (g + 1) : 2], identity=ident[:]
+                    )
+            grouped = work.tile([P, PASSES, P, PACK], BF16, name="grouped", align_bytes=64)
+            nc.scalar.copy(
+                out=grouped[:]
+                .rearrange("p g r t -> p (g r t)")
+                .bitcast(F32)
+                .rearrange("p (g r u) -> p g r u", g=PASSES, u=2),
+                in_=turned[:].rearrange("p g u r -> p g r u"),
+            )
+            codes = work.tile([P, PASSES, P], U32, name="x_codes", align_bytes=64, bufs=4)
+            planes = work.tile([P, PASSES, P], U8, name="x_planes", align_bytes=64, bufs=4)
+            nc.vector.quantize_mx(
+                out=codes[:].rearrange("p g r -> p (g r)").bitcast(FP8X4),
+                scales=planes[:].rearrange("p g r -> p (g r)"),
+                in_=grouped[:].rearrange("p g r t -> p (g r t)"),
+            )
+            codes_of[t] = (codes, planes)
+
+        def project_features(t, at, half, home, bias_column):
+            codes, planes = codes_of[t]
+            product = bank("product", [P, PER_BANK, P])
+            for i in range(PER_BANK):
+                column = at + (half * PER_BANK + i) * P
+                for g in range(PASSES):
+                    nc.tensor.matmul_mx(
+                        out=product[:, i, :],
+                        lhsT=w_codes[:, g, 2 * column : 2 * (column + P)].bitcast(FP4X4),
+                        lhsT_scale=w_planes[:, g, column : column + P],
+                        rhs=codes[:, g, :].bitcast(FP8X4),
+                        rhs_scale=planes[:, g, :],
+                        start=(g == 0),
+                        stop=(g == PASSES - 1),
+                    )
+            first = bias_column + half * PER_BANK
+            nc.vector.tensor_tensor(
+                out=home,
+                in0=product[:],
+                in1=bias_qk[:, first : first + PER_BANK].unsqueeze(2).to_broadcast([P, PER_BANK, P]),
+                op=ALU.add,
+            )
+
+        def project_k(t, half):
+            chunks = slice(half * PER_BANK, (half + 1) * PER_BANK)
+            project_features(t, K_AT, half, k_all[:, chunks, PAD + t * P : PAD + (t + 1) * P], CHUNKS)
+
+        def open_q(t):
+            q_of[t] = work.tile([P, CHUNKS, KEYS + P], F32, name="q_tile")
+            if t > 0:
+                nc.vector.tensor_copy(out=q_of[t][:, :, 0:KEYS], in_=q_of[t - 1][:, :, P : P + KEYS])
+            if t == TILES:
+                nc.gpsimd.memset(q_of[t][:, :, KEYS:P], 0.0)
+
+        def project_q(t, half):
+            chunks = slice(half * PER_BANK, (half + 1) * PER_BANK)
+            project_features(t, Q_AT, half, q_of[t][:, chunks, KEYS : KEYS + P], 0)
+
+        def mask_keys(block):
+            first = PAD + block * KEYS
+            for odd in range(2):
+                rows = slice(odd * HEAD_DIM, (odd + 1) * HEAD_DIM)
+                nc.vector.tensor_copy(
+                    out=key_blocks[block % 3][rows, :, odd, :], in_=k_all[rows, :, first : first + KEYS]
+                )
+
+        def project_v(t):
+            codes, planes = codes_of[t]
+            v_tok = work.tile([P, WIDTH], F32, name="v_tok", bufs=10)
+            for half in range(HALVES):
+                column = V_AT + half * BANK
+                product = bank("product_v", [P, BANK])
+                for g in range(PASSES):
+                    nc.tensor.matmul_mx(
+                        out=product[:],
+                        lhsT=codes[:, g, :].bitcast(FP8X4),
+                        lhsT_scale=planes[:, g, :],
+                        rhs=w_codes[:, g, 2 * column : 2 * (column + BANK)].bitcast(FP4X4),
+                        rhs_scale=w_planes[:, g, column : column + BANK],
+                        start=(g == 0),
+                        stop=(g == PASSES - 1),
+                    )
+                features = slice(half * BANK, (half + 1) * BANK)
+                nc.vector.tensor_tensor(out=v_tok[:, features], in0=product[:], in1=bias_v[:, features], op=ALU.add)
+            v_of[t] = v_tok
+            nc.sync.dma_start(out=out_rows[t * P : (t + 1) * P, :], in_=v_tok[:])
+
+        def scratch(block):
+            first = unit_of(block) * P
+            return out_rows[first : first + P, :]
+
+        def scratch_rows(block):
+            return scratch(block).rearrange("(n two) f -> n (two f)", two=2)
+
+        staged_of = {}
+
+        def multiply_block(block, half):
+            t, at = ((block + 1) // 2, 0) if block % 2 == 1 else (block // 2, KEYS)
+            if half == 0:
+                staged_of[block] = work.tile([P, KEYS, HEADS], F32, name="staged")
+            dots = bank("block_dots", [P, PER_BANK, 2, KEYS])
+            for i in range(PER_BANK):
+                c = half * PER_BANK + i
+                nc.tensor.matmul(
+                    out=dots[:, i, :, :].rearrange("p e m -> p (e m)"),
+                    lhsT=q_of[t][:, c, at : at + P],
+                    rhs=key_blocks[block % 3][:, c, :, :].rearrange("p e m -> p (e m)"),
+                    start=True,
+                    stop=True,
+                )
+            heads = slice(half * HEADS_PER_BANK, (half + 1) * HEADS_PER_BANK)
+            nc.vector.tensor_copy(
+                out=staged_of[block][:, :, heads], in_=dots[:].rearrange("p c e m -> p m (c e)")
+            )
+
+        def write_block(block):
+            staged = staged_of[block][:].rearrange("p m h -> p (m h)")
+            nc.sync.dma_start(out=scratch_rows(block)[:, ROW // 2 : ROW], in_=staged[0:KEYS, :])
+
+        def write_next(block):
+            staged = staged_of[block][:].rearrange("p m h -> p (m h)")
+            nc.sync.dma_start(out=scratch_rows(block + 1)[:, 0 : ROW // 2], in_=staged[KEYS:P, :])
+
+        def read_block(block):
+            t, odd = divmod(block, 2)
+            if odd == 0:
+                near_of[t] = work.tile([P, NEAR_MAX + 1, HEADS], F32, name="near", bufs=1)
+            near = near_of[t][:].rearrange("p o h -> p (o h)")
+            step = ROW + HEADS
+            wanted = (NEAR_MAX + 1) * HEADS
+            flat = scratch(block).rearrange("n f -> (n f)")
+            for first, count in ((0, 48), (48, 15)):
+                nc.sync.dma_start(
+                    out=near[odd * KEYS + first : odd * KEYS + first + count, :],
+                    in_=flat[first * step : (first + count) * step].rearrange("(r w) -> r w", w=step)[:, 0:wanted],
+                )
+            nc.sync.dma_start(
+                out=near[odd * KEYS + KEYS - 1 : odd * KEYS + KEYS, :],
+                in_=flat[(KEYS - 1) * step : (KEYS - 1) * step + wanted].unsqueeze(0),
+            )
+
+        def gather_near(t):
+            for first, count, step in NEAR_RUNS:
+                at = NEAR_MAX - OFFSETS[first]
+                nc.scalar.copy(
+                    out=dots_of[t][:, first : first + count, :],
+                    in_=near_of[t][:, at : at + (count - 1) * step + 1 : step, :],
+                )
+
+        def open_dots(t):
+            dots_of[t] = taps.tile([P, SLOTS, HEADS], F32, name="dots", bufs=2)
+            unused = slots_of(t)[0]
+            if unused > 0:
+                nc.gpsimd.memset(dots_of[t][:, 0:unused, :], 0.0)
+
+        def far_dot(t, slot):
+            first = PAD + t * P - OFFSETS[slot]
+            prod = work.tile([P, CHUNKS, P], F32, name="prod")
+            nc.gpsimd.tensor_tensor(
+                out=prod[:], in0=q_of[t][:, :, KEYS : KEYS + P], in1=k_all[:, :, first : first + P], op=ALU.mult
+            )
+            for half in range(HALVES):
+                by_token = bank("by_token", [P, PER_BANK, P])
+                for i in range(PER_BANK):
+                    nc.tensor.transpose(out=by_token[:, i, :], in_=prod[:, half * PER_BANK + i, :], identity=ident[:])
+                nc.vector.tensor_reduce(
+                    out=dots_of[t][:, slot, half * HEADS_PER_BANK : (half + 1) * HEADS_PER_BANK],
+                    in_=by_token[:].rearrange("p c (e d) -> p (c e) d", d=HEAD_DIM),
+                    axis=AXIS.X,
+                    op=ALU.add,
+                )
+
+        def scale_gains(t):
+            by_scale = gains_raw[:].rearrange("p (h t) s -> p t s h", t=TILES)[:, t]
+            gain = taps.tile([P, ENTRIES, HEADS], F32, name="gain")
+            for first, count, s0, tau in ENTRY_RUNS:
+                nc.scalar.mul(out=gain[:, first : first + count, :], in_=by_scale[:, s0 : s0 + count, :], mul=abs(D4[tau]))
+            nc.scalar.copy(out=gain[:, LOCAL, :], in_=bypass[:])
+            gain_of[t] = gain
+
+        def score_entries(t):
+            dots = dots_of[t]
+            u = taps.tile([P, ENTRIES, HEADS], F32, name="u")
+            nc.gpsimd.tensor_tensor(
+                out=u[:, 0:HERE, :],
+                in0=dots[:, HERE_SLOT : HERE_SLOT + 1, :].to_broadcast([P, HERE, HEADS]),
+                in1=tap_bias[:, 0:HERE, :],
+                op=ALU.add,
+            )
+            nc.gpsimd.tensor_tensor(
+                out=u[:, HERE:ODD_FIRST, :].rearrange("p (c e) h -> p c e h", c=2),
+                in0=dots[:, 0 : 2 * EVEN : 2, :].unsqueeze(1).to_broadcast([P, 2, EVEN, HEADS]),
+                in1=tap_bias[:, HERE:ODD_FIRST, :].rearrange("p (c e) h -> p c e h", c=2),
+                op=ALU.add,
+            )
+            nc.gpsimd.tensor_tensor(
+                out=u[:, ODD_FIRST:ENTRIES, :],
+                in0=dots[:, 1 : 2 * EVEN : 2, :],
+                in1=tap_bias[:, ODD_FIRST:ENTRIES, :],
+                op=ALU.add,
+            )
+            decay = taps.tile([P, ENTRIES, HEADS], F32, name="decay")
+            nc.scalar.activation(out=decay[:], in_=u[:], func=ACT.Relu, scale=-1.0)
+            nc.scalar.activation(out=decay[:], in_=decay[:], func=ACT.Exp, scale=-1.0)
+            score_of[t] = (u, decay)
+
+        def weigh_entries(t):
+            u, decay = score_of[t]
+            nc.vector.scalar_tensor_tensor(out=decay[:], in0=u[:], scalar=0.0, in1=decay[:], op0=ALU.max, op1=ALU.add)
+            term = decay
+            nc.vector.tensor_tensor(out=term[:], in0=decay[:], in1=gain_of[t][:], op=ALU.mult)
+            weight = taps.tile([P, SLOTS, HEADS], F32, name="weight", bufs=2)
+            nc.vector.tensor_reduce(
+                out=weight[:, HERE_SLOT, :], in_=term[:, 0:HERE, :].rearrange("p e h -> p h e"), axis=AXIS.X, op=ALU.add
+            )
+            nc.vector.tensor_reduce(
+                out=weight[:, 0 : 2 * EVEN : 2, :],
+                in_=term[:, HERE:ODD_FIRST, :].rearrange("p (c e) h -> p e h c", c=2),
+                axis=AXIS.X,
+                op=ALU.add,
+            )
+            z = taps.tile([P, HEADS], F32, name="z")
+            nc.vector.tensor_reduce(out=z[:], in_=term[:].rearrange("p e h -> p h e"), axis=AXIS.X, op=ALU.add)
+            nc.scalar.mul(out=weight[:, 1 : 2 * EVEN - 1 : 2, :], in_=term[:, ODD_FIRST:LAST, :], mul=-1.0)
+            nc.scalar.copy(out=weight[:, 2 * EVEN - 1, :], in_=term[:, LAST, :])
+            z_safe = taps.tile([P, HEADS], F32, name="z_safe")
+            nc.scalar.activation(out=z_safe[:], in_=z[:], func=ACT.Identity, bias=1e-6)
+            inv_z = taps.tile([P, HEADS], F32, name="inv_z", bufs=2)
+            nc.vector.reciprocal(out=inv_z[:], in_=z_safe[:])
+            inv_z_of[t] = inv_z
+            weight_of[t] = weight
+            weight_ps = psum.tile([P, V_SLOTS, HEADS], F32, name="weight_ps")
+            nc.tensor.matmul(
+                out=weight_ps[:].rearrange("p s h -> p (s h)"),
+                lhsT=ident[:],
+                rhs=weight[:, SLOTS - V_SLOTS : SLOTS, :].rearrange("p s h -> p (s h)"),
+                start=True,
+                stop=True,
+            )
+            weight_ps_of[t] = weight_ps
+
+        def order_of(t):
+            used = slots_of(t)
+            theirs = [s for s in used if s < SLOTS - V_SLOTS]
+            own = [s for s in used if s >= SLOTS - V_SLOTS]
+            merged = [((n + 0.5) / len(theirs), s) for n, s in enumerate(theirs)]
+            merged += [((n + 0.5) / len(own), s) for n, s in enumerate(own)]
+            return [s for at, s in sorted(merged)]
+
+        def multiply_w_v(t, slot, is_first, is_last):
+            if is_first:
+                sum_of[t] = [psum.tile([P, PER_BANK, P], F32, name="sum_ps%d" % b) for b in range(HALVES)]
+            offset = OFFSETS[slot]
+            if offset % P == 0:
+                shifted = v_of[t - offset // P]
+            else:
+                first = t * P - offset
+                missing = max(0, -first)
+                shifted = work.tile([P, WIDTH], F32, name="shifted", bufs=5)
+                if missing:
+                    nc.vector.memset(shifted[0:missing, :], 0.0)
+                split = P - (P - missing) % DMA_ENGINES
+                for low, high in ((missing, split), (split, P)):
+                    if low < high:
+                        nc.sync.dma_start(out=shifted[low:high, :], in_=out_rows[first + low : first + high, :])
+            scaled = work.tile([P, WIDTH], F32, name="scaled", bufs=3)
+            if slot >= SLOTS - V_SLOTS:
+                nc.vector.tensor_tensor(
+                    out=scaled[:].rearrange("p (h d) -> p h d", h=HEADS),
+                    in0=shifted[:].rearrange("p (h d) -> p h d", h=HEADS),
+                    in1=weight_ps_of[t][:, slot - (SLOTS - V_SLOTS), :].unsqueeze(2).to_broadcast([P, HEADS, HEAD_DIM]),
+                    op=ALU.mult,
+                )
+            else:
+                for h in range(HEADS):
+                    features = slice(h * HEAD_DIM, (h + 1) * HEAD_DIM)
+                    nc.scalar.activation(
+                        out=scaled[:, features],
+                        in_=shifted[:, features],
+                        func=ACT.Copy,
+                        scale=weight_of[t][:, slot, h : h + 1],
+                    )
+            for c in range(CHUNKS):
+                nc.tensor.matmul(
+                    out=sum_of[t][c // PER_BANK][:, c % PER_BANK, :],
+                    lhsT=scaled[:, c * P : (c + 1) * P],
+                    rhs=ident[:],
+                    is_transpose=True,
+                    start=(is_first and c % PER_BANK == 0),
+                    stop=(is_last and c % PER_BANK == PER_BANK - 1),
+                )
+
+        def finish_output(t):
+            sum_sb = work.tile([P, CHUNKS, P], F32, name="sum_sb", bufs=1)
+            for b in range(HALVES):
+                nc.scalar.copy(out=sum_sb[:, b * PER_BANK : (b + 1) * PER_BANK, :], in_=sum_of[t][b][:])
+            rows = work.tile([P, HEADS, HEAD_DIM], F32, name="rows", bufs=3)
+            for b in range(HALVES):
+                rows_ps = bank("rows_ps", [P, PER_BANK, P])
+                for i in range(PER_BANK):
+                    nc.tensor.transpose(out=rows_ps[:, i, :], in_=sum_sb[:, b * PER_BANK + i, :], identity=ident[:])
+                heads = slice(b * HEADS_PER_BANK, (b + 1) * HEADS_PER_BANK)
+                nc.vector.tensor_tensor(
+                    out=rows[:, heads, :],
+                    in0=rows_ps[:].rearrange("p c (e d) -> p (c e) d", d=HEAD_DIM),
+                    in1=inv_z_of[t][:, heads].unsqueeze(2).to_broadcast([P, HEADS_PER_BANK, HEAD_DIM]),
+                    op=ALU.mult,
+                )
+            rows_of[t] = rows
+
+        def store(t):
+            nc.sync.dma_start(
+                out=out_rows[t * P : (t + 1) * P, :], in_=rows_of[t][:].rearrange("p h d -> p (h d)")
+            )
+
+        def output_tasks(t):
+            order = order_of(t)
+            tasks = [
+                lambda s=s, n=n: multiply_w_v(t, s, n == 0, n == len(order) - 1) for n, s in enumerate(order)
+            ]
+            tasks.append(lambda: finish_output(t))
+            if t >= 2:
+                tasks.append(lambda: store(t - 2))
+            if t == TILES - 1:
+                tasks += [lambda: store(t - 1), lambda: store(t)]
+            return tasks
+
+        def projection_tasks(t):
+            tasks = []
+            if t <= TILES:
+                tasks.append(lambda: open_q(t))
+            if t + 1 < TILES:
+                tasks.append(lambda: load_x(t + 1))
+            if t < TILES:
+                for half in range(HALVES):
+                    tasks.append(lambda half=half: project_q(t, half))
+                for half in range(HALVES):
+                    tasks.append(lambda half=half: project_k(t, half))
+            for block in (2 * t - 1, 2 * t):
+                if 0 <= block < BLOCKS:
+                    if block % 2 == 0:
+                        tasks.append(lambda b=block: mask_keys(b))
+                        tasks.append(lambda b=block: mask_keys(b + 1))
+                    for half in range(HALVES):
+                        tasks.append(lambda b=block, half=half: multiply_block(b, half))
+                    tasks.append(lambda b=block: write_block(b))
+                    tasks.append(lambda b=block: read_block(b))
+                    if block + 1 < BLOCKS:
+                        tasks.append(lambda b=block: write_next(b))
+            if t + 1 < TILES:
+                tasks.append(lambda: quantise_x(t + 1))
+            return tasks
+
+        def dot_tasks(t):
+            tasks = [lambda: open_dots(t)]
+            tasks += [lambda s=s: far_dot(t, s) for s in slots_of(t) if s < FAR_SLOTS]
+            tasks.append(lambda: gather_near(t))
+            return tasks
+
+        load_x(0)
+        nc.sync.dma_start(
+            out=scratch_rows(0)[:, 0 : ROW // 2].rearrange("r (c n) -> r c n", n=PAD), in_=k_all[0:KEYS, :, 0:PAD]
+        )
+        quantise_x(0)
+        waiting = []
+        for step in range(TILES + 3):
+            done = step - 2
+            if 0 <= done < TILES:
+                scale_gains(done)
+                score_entries(done)
+                weigh_entries(done)
+                project_v(done)
+            outputs = waiting
+            waiting = []
+            if 0 <= done < TILES:
+                tasks = output_tasks(done)
+                cut = len(tasks) if done == TILES - 1 else 2 * len(tasks) // 3
+                outputs = outputs + tasks[:cut]
+                waiting = tasks[cut:]
+            streams = [outputs]
+            if step <= TILES:
+                streams.append(projection_tasks(step))
+            if 0 <= step - 1 < TILES:
+                streams.append(dot_tasks(step - 1))
+            weave([s for s in streams if s])

@@ -33,6 +33,7 @@ TILES = TOKENS // P
 CHUNKS = WIDTH // P
 PER_BANK = BANK // P
 HALVES = CHUNKS // PER_BANK
+PART = PER_BANK // 2
 HEADS_PER_BANK = HEADS // HALVES
 PAD = P
 
@@ -197,6 +198,7 @@ def stream(tc, ident, x_rows, out_rows, w_codes, w_planes, bias_qk, bias_v, gain
         x_sb_of, codes_of, q_of, near_of, dots_of = {}, {}, {}, {}, {}
         gain_of, score_of, weight_of, weight_ps_of, term_of, inv_z_of = {}, {}, {}, {}, {}, {}
         v_of, sum_of, rows_of = {}, {}, {}
+        product_of, block_dots_of = {}, {}
 
         def bank(name, shape):
             return psum.tile(shape, F32, name=name, tag="bank", bufs=5)
@@ -231,10 +233,12 @@ def stream(tc, ident, x_rows, out_rows, w_codes, w_planes, bias_qk, bias_v, gain
             )
             codes_of[t] = (codes, planes)
 
-        def project_features(t, at, half, home, bias_column):
+        def project_features(t, at, half, part, home, bias_column):
             codes, planes = codes_of[t]
-            product = bank("product", [P, PER_BANK, P])
-            for i in range(PER_BANK):
+            if part == 0:
+                product_of[at] = bank("product", [P, PER_BANK, P])
+            product = product_of[at]
+            for i in range(part * PART, (part + 1) * PART):
                 column = at + (half * PER_BANK + i) * P
                 for g in range(PASSES):
                     nc.tensor.matmul_mx(
@@ -246,6 +250,8 @@ def stream(tc, ident, x_rows, out_rows, w_codes, w_planes, bias_qk, bias_v, gain
                         start=(g == 0),
                         stop=(g == PASSES - 1),
                     )
+            if part == 0:
+                return
             first = bias_column + half * PER_BANK
             nc.vector.tensor_tensor(
                 out=home,
@@ -254,9 +260,9 @@ def stream(tc, ident, x_rows, out_rows, w_codes, w_planes, bias_qk, bias_v, gain
                 op=ALU.add,
             )
 
-        def project_k(t, half):
+        def project_k(t, half, part):
             chunks = slice(half * PER_BANK, (half + 1) * PER_BANK)
-            project_features(t, K_AT, half, k_all[:, chunks, PAD + t * P : PAD + (t + 1) * P], CHUNKS)
+            project_features(t, K_AT, half, part, k_all[:, chunks, PAD + t * P : PAD + (t + 1) * P], CHUNKS)
 
         def open_q(t):
             q_of[t] = work.tile([P, CHUNKS, KEYS + P], F32, name="q_tile")
@@ -265,9 +271,9 @@ def stream(tc, ident, x_rows, out_rows, w_codes, w_planes, bias_qk, bias_v, gain
             if t == TILES:
                 nc.gpsimd.memset(q_of[t][:, :, KEYS:P], 0.0)
 
-        def project_q(t, half):
+        def project_q(t, half, part):
             chunks = slice(half * PER_BANK, (half + 1) * PER_BANK)
-            project_features(t, Q_AT, half, q_of[t][:, chunks, KEYS : KEYS + P], 0)
+            project_features(t, Q_AT, half, part, q_of[t][:, chunks, KEYS : KEYS + P], 0)
 
         def mask_keys(block):
             first = PAD + block * KEYS
@@ -307,12 +313,14 @@ def stream(tc, ident, x_rows, out_rows, w_codes, w_planes, bias_qk, bias_v, gain
 
         staged_of = {}
 
-        def multiply_block(block, half):
+        def multiply_block(block, half, part):
             t, at = ((block + 1) // 2, 0) if block % 2 == 1 else (block // 2, KEYS)
-            if half == 0:
+            if half == 0 and part == 0:
                 staged_of[block] = work.tile([P, KEYS, HEADS], F32, name="staged")
-            dots = bank("block_dots", [P, PER_BANK, 2, KEYS])
-            for i in range(PER_BANK):
+            if part == 0:
+                block_dots_of[block] = bank("block_dots", [P, PER_BANK, 2, KEYS])
+            dots = block_dots_of[block]
+            for i in range(part * PART, (part + 1) * PART):
                 c = half * PER_BANK + i
                 nc.tensor.matmul(
                     out=dots[:, i, :, :].rearrange("p e m -> p (e m)"),
@@ -321,6 +329,8 @@ def stream(tc, ident, x_rows, out_rows, w_codes, w_planes, bias_qk, bias_v, gain
                     start=True,
                     stop=True,
                 )
+            if part == 0:
+                return
             heads = slice(half * HEADS_PER_BANK, (half + 1) * HEADS_PER_BANK)
             nc.vector.tensor_copy(
                 out=staged_of[block][:, :, heads], in_=dots[:].rearrange("p c e m -> p m (c e)")
@@ -539,30 +549,29 @@ def stream(tc, ident, x_rows, out_rows, w_codes, w_planes, bias_qk, bias_v, gain
             return tasks
 
         def projection_tasks(t):
-            tasks = []
-            if t <= TILES:
-                tasks.append(lambda: open_q(t))
+            runs = [[lambda: open_q(t)]]
             if t + 1 < TILES:
-                tasks.append(lambda: load_x(t + 1))
+                runs[0].append(lambda: load_x(t + 1))
             if t < TILES:
-                for half in range(HALVES):
-                    tasks.append(lambda half=half: project_q(t, half))
-                for half in range(HALVES):
-                    tasks.append(lambda half=half: project_k(t, half))
+                for project in (project_q, project_k):
+                    for half in range(HALVES):
+                        for part in range(PER_BANK // PART):
+                            runs.append([lambda f=project, half=half, part=part: f(t, half, part)])
+                runs[-1].append(lambda: mask_keys(2 * t))
+                runs[-1].append(lambda: mask_keys(2 * t + 1))
             for block in (2 * t - 1, 2 * t):
                 if 0 <= block < BLOCKS:
-                    if block % 2 == 0:
-                        tasks.append(lambda b=block: mask_keys(b))
-                        tasks.append(lambda b=block: mask_keys(b + 1))
                     for half in range(HALVES):
-                        tasks.append(lambda b=block, half=half: multiply_block(b, half))
-                    tasks.append(lambda b=block: write_block(b))
-                    tasks.append(lambda b=block: read_block(b))
+                        for part in range(PER_BANK // PART):
+                            runs.append([lambda b=block, half=half, part=part: multiply_block(b, half, part)])
+                    runs[-1].append(lambda b=block: write_block(b))
+                    runs[-1].append(lambda b=block: read_block(b))
                     if block + 1 < BLOCKS:
-                        tasks.append(lambda b=block: write_next(b))
+                        runs[-1].append(lambda b=block: write_next(b))
             if t + 1 < TILES:
-                tasks.append(lambda: quantise_x(t + 1))
-            return tasks
+                runs[-1].append(lambda: quantise_x(t + 1))
+            runs[1] = runs[0] + runs[1]
+            return [lambda run=run: [task() for task in run] for run in runs[1:]]
 
         def dot_tasks(t):
             tasks = [lambda: open_dots(t)]

@@ -52,7 +52,12 @@ assert all(OFFSETS[2 * i + 1] == 3 << (8 - i) for i in range(9)) and OFFSETS[19]
 FAR_SLOTS = len([o for o in OFFSETS if o > NEAR_MAX])
 NEAR_RUNS = [(8, 2, 16), (10, 2, 8), (12, 2, 4), (14, 2, 2), (16, 5, 1)]
 
-V_SLOTS = 5
+LATE_TILE = 8
+MAX_VECTOR_SLOTS = 10
+EARLY_VECTOR_SLOTS = 3
+RUNS_PER_PRODUCT = 1.5
+DOTS_PER_PRODUCT = 0.5
+LEAD = 5
 GAIN_RUN = 6
 DMA_ENGINES = 16
 
@@ -75,15 +80,8 @@ def unit_of(block):
     return 9 + block % 3 if block < BLOCKS - 3 else (10 if block < BLOCKS - 1 else 11)
 
 
-def weave(streams):
-    done = [0] * len(streams)
-    total = sum(len(s) for s in streams)
-    for n in range(total):
-        pick = min(
-            (i for i in range(len(streams)) if done[i] < len(streams[i])), key=lambda i: (done[i] + 0.5) / len(streams[i])
-        )
-        streams[pick][done[pick]]()
-        done[pick] += 1
+def vector_slots(t):
+    return EARLY_VECTOR_SLOTS if t < LATE_TILE else MAX_VECTOR_SLOTS
 
 
 def load_tables(tc, ident, b_qkv, pos_bias, identity_bypass, gains, bias_qk, bias_v, tap_bias, bypass, gains_raw):
@@ -204,7 +202,7 @@ def stream(tc, ident, x_rows, out_rows, w_codes, w_planes, bias_qk, bias_v, gain
             return psum.tile(shape, F32, name=name, tag="bank", bufs=5)
 
         def load_x(t):
-            x_sb_of[t] = work.tile([P, D_IN], BF16, name="x_sb")
+            x_sb_of[t] = work.tile([P, D_IN], BF16, name="x_sb", bufs=1)
             nc.sync.dma_start(out=x_sb_of[t][:], in_=x_rows[t * P : (t + 1) * P, :])
 
         def quantise_x(t):
@@ -216,7 +214,7 @@ def stream(tc, ident, x_rows, out_rows, w_codes, w_planes, bias_qk, bias_v, gain
                     nc.tensor.transpose(
                         out=turned[:, g, u, :], in_=words[:, per_pass * g + u : per_pass * (g + 1) : 2], identity=ident[:]
                     )
-            grouped = work.tile([P, PASSES, P, PACK], BF16, name="grouped", align_bytes=64)
+            grouped = work.tile([P, PASSES, P, PACK], BF16, name="grouped", align_bytes=64, bufs=1)
             nc.scalar.copy(
                 out=grouped[:]
                 .rearrange("p g r t -> p (g r t)")
@@ -224,8 +222,8 @@ def stream(tc, ident, x_rows, out_rows, w_codes, w_planes, bias_qk, bias_v, gain
                 .rearrange("p (g r u) -> p g r u", g=PASSES, u=2),
                 in_=turned[:].rearrange("p g u r -> p g r u"),
             )
-            codes = work.tile([P, PASSES, P], U32, name="x_codes", align_bytes=64, bufs=4)
-            planes = work.tile([P, PASSES, P], U8, name="x_planes", align_bytes=64, bufs=4)
+            codes = work.tile([P, PASSES, P], U32, name="x_codes", align_bytes=64, bufs=LEAD)
+            planes = work.tile([P, PASSES, P], U8, name="x_planes", align_bytes=64, bufs=LEAD)
             nc.vector.quantize_mx(
                 out=codes[:].rearrange("p g r -> p (g r)").bitcast(FP8X4),
                 scales=planes[:].rearrange("p g r -> p (g r)"),
@@ -253,12 +251,13 @@ def stream(tc, ident, x_rows, out_rows, w_codes, w_planes, bias_qk, bias_v, gain
             if part == 0:
                 return
             first = bias_column + half * PER_BANK
+            bias = bias_qk[:, first : first + PER_BANK].unsqueeze(2)
             nc.vector.tensor_tensor(
-                out=home,
-                in0=product[:],
-                in1=bias_qk[:, first : first + PER_BANK].unsqueeze(2).to_broadcast([P, PER_BANK, P]),
-                op=ALU.add,
+                out=home, in0=product[:], in1=bias.to_broadcast([P, PER_BANK, P]), op=ALU.add
             )
+            if at == K_AT:
+                mask_keys(2 * t, half, product, bias)
+                mask_keys(2 * t + 1, half, product, bias)
 
         def project_k(t, half, part):
             chunks = slice(half * PER_BANK, (half + 1) * PER_BANK)
@@ -267,7 +266,7 @@ def stream(tc, ident, x_rows, out_rows, w_codes, w_planes, bias_qk, bias_v, gain
         def open_q(t):
             q_of[t] = work.tile([P, CHUNKS, KEYS + P], F32, name="q_tile")
             if t > 0:
-                nc.vector.tensor_copy(out=q_of[t][:, :, 0:KEYS], in_=q_of[t - 1][:, :, P : P + KEYS])
+                nc.scalar.copy(out=q_of[t][:, :, 0:KEYS], in_=q_of[t - 1][:, :, P : P + KEYS])
             if t == TILES:
                 nc.gpsimd.memset(q_of[t][:, :, KEYS:P], 0.0)
 
@@ -275,12 +274,16 @@ def stream(tc, ident, x_rows, out_rows, w_codes, w_planes, bias_qk, bias_v, gain
             chunks = slice(half * PER_BANK, (half + 1) * PER_BANK)
             project_features(t, Q_AT, half, part, q_of[t][:, chunks, KEYS : KEYS + P], 0)
 
-        def mask_keys(block):
-            first = PAD + block * KEYS
+        def mask_keys(block, half, product, bias):
+            chunks = slice(half * PER_BANK, (half + 1) * PER_BANK)
+            tokens = slice(block % 2 * KEYS, (block % 2 + 1) * KEYS)
             for odd in range(2):
                 rows = slice(odd * HEAD_DIM, (odd + 1) * HEAD_DIM)
-                nc.vector.tensor_copy(
-                    out=key_blocks[block % 3][rows, :, odd, :], in_=k_all[rows, :, first : first + KEYS]
+                nc.vector.tensor_tensor(
+                    out=key_blocks[block % 3][rows, chunks, odd, :],
+                    in0=product[rows, :, tokens],
+                    in1=bias[rows].to_broadcast([HEAD_DIM, PER_BANK, KEYS]),
+                    op=ALU.add,
                 )
 
         def project_v(t):
@@ -362,7 +365,13 @@ def stream(tc, ident, x_rows, out_rows, w_codes, w_planes, bias_qk, bias_v, gain
                 in_=flat[(KEYS - 1) * step : (KEYS - 1) * step + wanted].unsqueeze(0),
             )
 
+        gathered = set()
+
         def gather_near(t):
+            if t in gathered:
+                return
+            gathered.add(t)
+            open_dots(t)
             for first, count, step in NEAR_RUNS:
                 at = NEAR_MAX - OFFSETS[first]
                 nc.scalar.copy(
@@ -371,12 +380,15 @@ def stream(tc, ident, x_rows, out_rows, w_codes, w_planes, bias_qk, bias_v, gain
                 )
 
         def open_dots(t):
-            dots_of[t] = taps.tile([P, SLOTS, HEADS], F32, name="dots", bufs=2)
+            if t in dots_of:
+                return
+            dots_of[t] = taps.tile([P, SLOTS, HEADS], F32, name="dots", bufs=LEAD)
             unused = slots_of(t)[0]
             if unused > 0:
                 nc.gpsimd.memset(dots_of[t][:, 0:unused, :], 0.0)
 
         def far_dot(t, slot):
+            open_dots(t)
             first = PAD + t * P - OFFSETS[slot]
             prod = work.tile([P, CHUNKS, P], F32, name="prod")
             nc.gpsimd.tensor_tensor(
@@ -452,11 +464,14 @@ def stream(tc, ident, x_rows, out_rows, w_codes, w_planes, bias_qk, bias_v, gain
             nc.vector.reciprocal(out=inv_z[:], in_=z_safe[:])
             inv_z_of[t] = inv_z
             weight_of[t] = weight
-            weight_ps = psum.tile([P, V_SLOTS, HEADS], F32, name="weight_ps")
+
+        def show_weights(t):
+            count = vector_slots(t)
+            weight_ps = psum.tile([P, MAX_VECTOR_SLOTS, HEADS], F32, name="weight_ps")
             nc.tensor.matmul(
-                out=weight_ps[:].rearrange("p s h -> p (s h)"),
+                out=weight_ps[:, 0:count, :].rearrange("p s h -> p (s h)"),
                 lhsT=ident[:],
-                rhs=weight[:, SLOTS - V_SLOTS : SLOTS, :].rearrange("p s h -> p (s h)"),
+                rhs=weight_of[t][:, SLOTS - count : SLOTS, :].rearrange("p s h -> p (s h)"),
                 start=True,
                 stop=True,
             )
@@ -464,8 +479,8 @@ def stream(tc, ident, x_rows, out_rows, w_codes, w_planes, bias_qk, bias_v, gain
 
         def order_of(t):
             used = slots_of(t)
-            theirs = [s for s in used if s < SLOTS - V_SLOTS]
-            own = [s for s in used if s >= SLOTS - V_SLOTS]
+            theirs = [s for s in used if s < SLOTS - vector_slots(t)]
+            own = [s for s in used if s >= SLOTS - vector_slots(t)]
             merged = [((n + 0.5) / len(theirs), s) for n, s in enumerate(theirs)]
             merged += [((n + 0.5) / len(own), s) for n, s in enumerate(own)]
             return [s for at, s in sorted(merged)]
@@ -486,12 +501,12 @@ def stream(tc, ident, x_rows, out_rows, w_codes, w_planes, bias_qk, bias_v, gain
                 for low, high in ((missing, split), (split, P)):
                     if low < high:
                         nc.sync.dma_start(out=shifted[low:high, :], in_=out_rows[first + low : first + high, :])
-            scaled = work.tile([P, WIDTH], F32, name="scaled", bufs=3)
-            if slot >= SLOTS - V_SLOTS:
+            scaled = work.tile([P, WIDTH], F32, name="scaled", bufs=4)
+            if slot >= SLOTS - vector_slots(t):
                 nc.vector.tensor_tensor(
                     out=scaled[:].rearrange("p (h d) -> p h d", h=HEADS),
                     in0=shifted[:].rearrange("p (h d) -> p h d", h=HEADS),
-                    in1=weight_ps_of[t][:, slot - (SLOTS - V_SLOTS), :].unsqueeze(2).to_broadcast([P, HEADS, HEAD_DIM]),
+                    in1=weight_ps_of[t][:, slot - (SLOTS - vector_slots(t)), :].unsqueeze(2).to_broadcast([P, HEADS, HEAD_DIM]),
                     op=ALU.mult,
                 )
             else:
@@ -514,7 +529,8 @@ def stream(tc, ident, x_rows, out_rows, w_codes, w_planes, bias_qk, bias_v, gain
                 )
 
         def finish_output(t):
-            sum_sb = work.tile([P, CHUNKS, P], F32, name="sum_sb", bufs=1)
+            sum_flat = work.tile([P, WIDTH], F32, name="sum_sb", tag="scaled", bufs=4)
+            sum_sb = sum_flat[:].rearrange("p (c n) -> p c n", c=CHUNKS)
             for b in range(HALVES):
                 nc.scalar.copy(out=sum_sb[:, b * PER_BANK : (b + 1) * PER_BANK, :], in_=sum_of[t][b][:])
             rows = work.tile([P, HEADS, HEAD_DIM], F32, name="rows", bufs=3)
@@ -536,16 +552,8 @@ def stream(tc, ident, x_rows, out_rows, w_codes, w_planes, bias_qk, bias_v, gain
                 out=out_rows[t * P : (t + 1) * P, :], in_=rows_of[t][:].rearrange("p h d -> p (h d)")
             )
 
-        def output_tasks(t):
-            order = order_of(t)
-            tasks = [
-                lambda s=s, n=n: multiply_w_v(t, s, n == 0, n == len(order) - 1) for n, s in enumerate(order)
-            ]
-            tasks.append(lambda: finish_output(t))
-            if t >= 2:
-                tasks.append(lambda: store(t - 2))
-            if t == TILES - 1:
-                tasks += [lambda: store(t - 1), lambda: store(t)]
+        def dot_tasks(t):
+            tasks = [lambda s=s: far_dot(t, s) for s in slots_of(t) if s < FAR_SLOTS]
             return tasks
 
         def projection_tasks(t):
@@ -557,51 +565,77 @@ def stream(tc, ident, x_rows, out_rows, w_codes, w_planes, bias_qk, bias_v, gain
                     for half in range(HALVES):
                         for part in range(PER_BANK // PART):
                             runs.append([lambda f=project, half=half, part=part: f(t, half, part)])
-                runs[-1].append(lambda: mask_keys(2 * t))
-                runs[-1].append(lambda: mask_keys(2 * t + 1))
             for block in (2 * t - 1, 2 * t):
                 if 0 <= block < BLOCKS:
                     for half in range(HALVES):
                         for part in range(PER_BANK // PART):
                             runs.append([lambda b=block, half=half, part=part: multiply_block(b, half, part)])
                     runs[-1].append(lambda b=block: write_block(b))
-                    runs[-1].append(lambda b=block: read_block(b))
+                    if block % 2 == 1:
+                        runs[-1].append(lambda b=block: read_block(b - 1))
+                        runs[-1].append(lambda b=block: read_block(b))
                     if block + 1 < BLOCKS:
                         runs[-1].append(lambda b=block: write_next(b))
             if t + 1 < TILES:
                 runs[-1].append(lambda: quantise_x(t + 1))
+            if t >= 2:
+                runs[3].append(lambda: gather_near(t - 2))
             runs[1] = runs[0] + runs[1]
             return [lambda run=run: [task() for task in run] for run in runs[1:]]
 
-        def dot_tasks(t):
-            tasks = [lambda: open_dots(t)]
-            tasks += [lambda s=s: far_dot(t, s) for s in slots_of(t) if s < FAR_SLOTS]
-            tasks.append(lambda: gather_near(t))
-            return tasks
+        projection = [(t, task) for t in range(TILES + 1) for task in projection_tasks(t)]
+        far_dots = [(t, task) for t in range(TILES) for task in dot_tasks(t)]
+        issued = {"runs": 0, "dots": 0}
+
+        def next_tile(tasks, name):
+            return tasks[issued[name]][0] if issued[name] < len(tasks) else TILES + 1
+
+        def issue_run():
+            if issued["runs"] < len(projection):
+                issued["runs"] += 1
+                projection[issued["runs"] - 1][1]()
+
+        def issue_dot():
+            if issued["dots"] < len(far_dots) and far_dots[issued["dots"]][0] < next_tile(projection, "runs"):
+                issued["dots"] += 1
+                far_dots[issued["dots"] - 1][1]()
+
+        def prepare_output(t):
+            while next_tile(projection, "runs") <= t + 1:
+                issue_run()
+            while next_tile(far_dots, "dots") <= t:
+                issue_dot()
+            gather_near(t)
+            scale_gains(t)
+            score_entries(t)
+            weigh_entries(t)
+            project_v(t)
 
         load_x(0)
         nc.sync.dma_start(
             out=scratch_rows(0)[:, 0 : ROW // 2].rearrange("r (c n) -> r c n", n=PAD), in_=k_all[0:KEYS, :, 0:PAD]
         )
         quantise_x(0)
-        waiting = []
-        for step in range(TILES + 3):
-            done = step - 2
-            if 0 <= done < TILES:
-                scale_gains(done)
-                score_entries(done)
-                weigh_entries(done)
-                project_v(done)
-            outputs = waiting
-            waiting = []
-            if 0 <= done < TILES:
-                tasks = output_tasks(done)
-                cut = len(tasks) if done == TILES - 1 else 2 * len(tasks) // 3
-                outputs = outputs + tasks[:cut]
-                waiting = tasks[cut:]
-            streams = [outputs]
-            if step <= TILES:
-                streams.append(projection_tasks(step))
-            if 0 <= step - 1 < TILES:
-                streams.append(dot_tasks(step - 1))
-            weave([s for s in streams if s])
+        prepare_output(0)
+        owed = {"runs": 0.0, "dots": 0.0}
+        for t in range(TILES):
+            order = order_of(t)
+            show_weights(t)
+            for n, slot in enumerate(order):
+                if n == 2 * len(order) // 3 and t + 1 < TILES:
+                    prepare_output(t + 1)
+                multiply_w_v(t, slot, n == 0, n == len(order) - 1)
+                owed["runs"] += RUNS_PER_PRODUCT
+                owed["dots"] += DOTS_PER_PRODUCT
+                while owed["runs"] >= 1.0:
+                    owed["runs"] -= 1.0
+                    if next_tile(projection, "runs") < t + LEAD - 1:
+                        issue_run()
+                while owed["dots"] >= 1.0:
+                    owed["dots"] -= 1.0
+                    issue_dot()
+            finish_output(t)
+            if t >= 2:
+                store(t - 2)
+        store(TILES - 2)
+        store(TILES - 1)

@@ -35,7 +35,7 @@ PER_BANK = BANK // P
 HALVES = CHUNKS // PER_BANK
 PART = PER_BANK // 2
 HEADS_PER_BANK = HEADS // HALVES
-PAD = P
+PAD = P // 2
 
 KEYS = HEAD_DIM
 BLOCKS = TOKENS // KEYS
@@ -53,11 +53,14 @@ FAR_SLOTS = len([o for o in OFFSETS if o > NEAR_MAX])
 NEAR_RUNS = [(8, 2, 16), (10, 2, 8), (12, 2, 4), (14, 2, 2), (16, 5, 1)]
 
 LATE_TILE = 8
-MAX_VECTOR_SLOTS = 10
-EARLY_VECTOR_SLOTS = 3
+MAX_VECTOR_SLOTS = 8
+EARLY_VECTOR_SLOTS = 2
+EARLY_PAIRS = 3
+LATE_PAIRS = 4
+SCALED_BUFS = 6
 RUNS_PER_PRODUCT = 1.5
 DOTS_PER_PRODUCT = 0.5
-LEAD = 5
+LEAD = 4
 GAIN_RUN = 6
 DMA_ENGINES = 16
 
@@ -161,7 +164,7 @@ def tile_dwarfattention_pa_kernel(
         gains_raw = keep.tile([P, HEADS * TILES, SCALES], BF16, name="gains_raw")
         k_all = keep.tile([P, CHUNKS, PAD + TOKENS], F32, name="k_all")
         nc.gpsimd.memset(k_all[:, :, 0:PAD], 0.0)
-        key_blocks = [keep.tile([P, CHUNKS, 2, KEYS], F32, name="key_block%d" % i) for i in range(3)]
+        key_blocks = [keep.tile([P, CHUNKS, 2, KEYS], F32, name="key_block%d" % i) for i in range(2)]
         for kb in key_blocks:
             nc.gpsimd.memset(kb[:], 0.0)
         w_planes = keep.tile([P, PASSES, 3 * WIDTH], U8, name="w_planes", align_bytes=64)
@@ -280,7 +283,7 @@ def stream(tc, ident, x_rows, out_rows, w_codes, w_planes, bias_qk, bias_v, gain
             for odd in range(2):
                 rows = slice(odd * HEAD_DIM, (odd + 1) * HEAD_DIM)
                 nc.vector.tensor_tensor(
-                    out=key_blocks[block % 3][rows, chunks, odd, :],
+                    out=key_blocks[block % 2][rows, chunks, odd, :],
                     in0=product[rows, :, tokens],
                     in1=bias[rows].to_broadcast([HEAD_DIM, PER_BANK, KEYS]),
                     op=ALU.add,
@@ -328,7 +331,7 @@ def stream(tc, ident, x_rows, out_rows, w_codes, w_planes, bias_qk, bias_v, gain
                 nc.tensor.matmul(
                     out=dots[:, i, :, :].rearrange("p e m -> p (e m)"),
                     lhsT=q_of[t][:, c, at : at + P],
-                    rhs=key_blocks[block % 3][:, c, :, :].rearrange("p e m -> p (e m)"),
+                    rhs=key_blocks[block % 2][:, c, :, :].rearrange("p e m -> p (e m)"),
                     start=True,
                     stop=True,
                 )
@@ -390,9 +393,15 @@ def stream(tc, ident, x_rows, out_rows, w_codes, w_planes, bias_qk, bias_v, gain
         def far_dot(t, slot):
             open_dots(t)
             first = PAD + t * P - OFFSETS[slot]
+            missing = max(0, -first)
             prod = work.tile([P, CHUNKS, P], F32, name="prod")
+            if missing:
+                nc.gpsimd.memset(prod[:, :, 0:missing], 0.0)
             nc.gpsimd.tensor_tensor(
-                out=prod[:], in0=q_of[t][:, :, KEYS : KEYS + P], in1=k_all[:, :, first : first + P], op=ALU.mult
+                out=prod[:, :, missing:P],
+                in0=q_of[t][:, :, KEYS + missing : KEYS + P],
+                in1=k_all[:, :, first + missing : first + P],
+                op=ALU.mult,
             )
             for half in range(HALVES):
                 by_token = bank("by_token", [P, PER_BANK, P])
@@ -477,17 +486,19 @@ def stream(tc, ident, x_rows, out_rows, w_codes, w_planes, bias_qk, bias_v, gain
             )
             weight_ps_of[t] = weight_ps
 
-        def order_of(t):
+        def groups_of(t):
             used = slots_of(t)
             theirs = [s for s in used if s < SLOTS - vector_slots(t)]
-            own = [s for s in used if s >= SLOTS - vector_slots(t)]
-            merged = [((n + 0.5) / len(theirs), s) for n, s in enumerate(theirs)]
-            merged += [((n + 0.5) / len(own), s) for n, s in enumerate(own)]
-            return [s for at, s in sorted(merged)]
+            own = [[s] for s in used if s >= SLOTS - vector_slots(t)]
+            pairs = EARLY_PAIRS if t < LATE_TILE else LATE_PAIRS
+            paired = [theirs[2 * n : 2 * n + 2] for n in range(pairs)]
+            rest = [[s] for s in theirs[2 * pairs :]]
+            merged = [((n + 0.5) / len(part), group) for part in (paired, rest, own) for n, group in enumerate(part)]
+            return [group for at, group in sorted(merged)]
 
-        def multiply_w_v(t, slot, is_first, is_last):
-            if is_first:
-                sum_of[t] = [psum.tile([P, PER_BANK, P], F32, name="sum_ps%d" % b) for b in range(HALVES)]
+        scaled_of = {}
+
+        def multiply_w_v(t, slot):
             offset = OFFSETS[slot]
             if offset % P == 0:
                 shifted = v_of[t - offset // P]
@@ -496,12 +507,12 @@ def stream(tc, ident, x_rows, out_rows, w_codes, w_planes, bias_qk, bias_v, gain
                 missing = max(0, -first)
                 shifted = work.tile([P, WIDTH], F32, name="shifted", bufs=5)
                 if missing:
-                    nc.vector.memset(shifted[0:missing, :], 0.0)
+                    nc.gpsimd.memset(shifted[0:missing, :], 0.0)
                 split = P - (P - missing) % DMA_ENGINES
                 for low, high in ((missing, split), (split, P)):
                     if low < high:
                         nc.sync.dma_start(out=shifted[low:high, :], in_=out_rows[first + low : first + high, :])
-            scaled = work.tile([P, WIDTH], F32, name="scaled", bufs=4)
+            scaled = work.tile([P, WIDTH], F32, name="scaled", bufs=SCALED_BUFS)
             if slot >= SLOTS - vector_slots(t):
                 nc.vector.tensor_tensor(
                     out=scaled[:].rearrange("p (h d) -> p h d", h=HEADS),
@@ -518,6 +529,19 @@ def stream(tc, ident, x_rows, out_rows, w_codes, w_planes, bias_qk, bias_v, gain
                         func=ACT.Copy,
                         scale=weight_of[t][:, slot, h : h + 1],
                     )
+            scaled_of[t, slot] = scaled
+
+        def make_group(t, group):
+            for slot in group:
+                multiply_w_v(t, slot)
+            if len(group) == 2:
+                one, other = [scaled_of[t, slot] for slot in group]
+                nc.vector.tensor_tensor(out=one[:], in0=one[:], in1=other[:], op=ALU.add)
+
+        def add_group(t, group, is_first, is_last):
+            if is_first:
+                sum_of[t] = [psum.tile([P, PER_BANK, P], F32, name="sum_ps%d" % b) for b in range(HALVES)]
+            scaled = scaled_of[t, group[0]]
             for c in range(CHUNKS):
                 nc.tensor.matmul(
                     out=sum_of[t][c // PER_BANK][:, c % PER_BANK, :],
@@ -529,7 +553,7 @@ def stream(tc, ident, x_rows, out_rows, w_codes, w_planes, bias_qk, bias_v, gain
                 )
 
         def finish_output(t):
-            sum_flat = work.tile([P, WIDTH], F32, name="sum_sb", tag="scaled", bufs=4)
+            sum_flat = work.tile([P, WIDTH], F32, name="sum_sb", tag="scaled", bufs=SCALED_BUFS)
             sum_sb = sum_flat[:].rearrange("p (c n) -> p c n", c=CHUNKS)
             for b in range(HALVES):
                 nc.scalar.copy(out=sum_sb[:, b * PER_BANK : (b + 1) * PER_BANK, :], in_=sum_of[t][b][:])
@@ -560,22 +584,30 @@ def stream(tc, ident, x_rows, out_rows, w_codes, w_planes, bias_qk, bias_v, gain
             runs = [[lambda: open_q(t)]]
             if t + 1 < TILES:
                 runs[0].append(lambda: load_x(t + 1))
+
+            def project(f):
+                for half in range(HALVES):
+                    for part in range(PER_BANK // PART):
+                        runs.append([lambda half=half, part=part: f(t, half, part)])
+
+            def multiply(block):
+                for half in range(HALVES):
+                    for part in range(PER_BANK // PART):
+                        runs.append([lambda half=half, part=part: multiply_block(block, half, part)])
+                runs[-1].append(lambda: write_block(block))
+                if block % 2 == 1:
+                    runs[-1].append(lambda: read_block(block - 1))
+                    runs[-1].append(lambda: read_block(block))
+                if block + 1 < BLOCKS:
+                    runs[-1].append(lambda: write_next(block))
+
             if t < TILES:
-                for project in (project_q, project_k):
-                    for half in range(HALVES):
-                        for part in range(PER_BANK // PART):
-                            runs.append([lambda f=project, half=half, part=part: f(t, half, part)])
-            for block in (2 * t - 1, 2 * t):
-                if 0 <= block < BLOCKS:
-                    for half in range(HALVES):
-                        for part in range(PER_BANK // PART):
-                            runs.append([lambda b=block, half=half, part=part: multiply_block(b, half, part)])
-                    runs[-1].append(lambda b=block: write_block(b))
-                    if block % 2 == 1:
-                        runs[-1].append(lambda b=block: read_block(b - 1))
-                        runs[-1].append(lambda b=block: read_block(b))
-                    if block + 1 < BLOCKS:
-                        runs[-1].append(lambda b=block: write_next(b))
+                project(project_q)
+            if t > 0:
+                multiply(2 * t - 1)
+            if t < TILES:
+                project(project_k)
+                multiply(2 * t)
             if t + 1 < TILES:
                 runs[-1].append(lambda: quantise_x(t + 1))
             if t >= 2:
@@ -601,7 +633,8 @@ def stream(tc, ident, x_rows, out_rows, w_codes, w_planes, bias_qk, bias_v, gain
                 far_dots[issued["dots"] - 1][1]()
 
         def prepare_output(t):
-            while next_tile(projection, "runs") <= t + 1:
+            needed = t + 1 if t < unit_of(BLOCKS - 2) else TILES
+            while next_tile(projection, "runs") <= needed:
                 issue_run()
             while next_tile(far_dots, "dots") <= t:
                 issue_dot()
@@ -612,21 +645,26 @@ def stream(tc, ident, x_rows, out_rows, w_codes, w_planes, bias_qk, bias_v, gain
             project_v(t)
 
         load_x(0)
-        nc.sync.dma_start(
-            out=scratch_rows(0)[:, 0 : ROW // 2].rearrange("r (c n) -> r c n", n=PAD), in_=k_all[0:KEYS, :, 0:PAD]
-        )
+        for part in range(2):
+            quarter = slice(part * ROW // 4, (part + 1) * ROW // 4)
+            nc.sync.dma_start(
+                out=scratch_rows(0)[:, quarter].rearrange("r (c n) -> r c n", n=PAD), in_=k_all[0:KEYS, :, 0:PAD]
+            )
         quantise_x(0)
         prepare_output(0)
         owed = {"runs": 0.0, "dots": 0.0}
         for t in range(TILES):
-            order = order_of(t)
+            groups = groups_of(t)
             show_weights(t)
-            for n, slot in enumerate(order):
-                if n == 2 * len(order) // 3 and t + 1 < TILES:
+            for n in range(len(groups) + 1):
+                if n == 2 * len(groups) // 3 and t + 1 < TILES:
                     prepare_output(t + 1)
-                multiply_w_v(t, slot, n == 0, n == len(order) - 1)
-                owed["runs"] += RUNS_PER_PRODUCT
-                owed["dots"] += DOTS_PER_PRODUCT
+                if n < len(groups):
+                    make_group(t, groups[n])
+                    owed["runs"] += RUNS_PER_PRODUCT * len(groups[n])
+                    owed["dots"] += DOTS_PER_PRODUCT * len(groups[n])
+                if n > 0:
+                    add_group(t, groups[n - 1], n == 1, n == len(groups))
                 while owed["runs"] >= 1.0:
                     owed["runs"] -= 1.0
                     if next_tile(projection, "runs") < t + LEAD - 1:

@@ -33,7 +33,6 @@ TILES = TOKENS // P
 CHUNKS = WIDTH // P
 PER_BANK = BANK // P
 HALVES = CHUNKS // PER_BANK
-PART = PER_BANK // 2
 HEADS_PER_BANK = HEADS // HALVES
 PAD = P // 2
 
@@ -53,12 +52,12 @@ FAR_SLOTS = len([o for o in OFFSETS if o > NEAR_MAX])
 NEAR_RUNS = [(8, 2, 16), (10, 2, 8), (12, 2, 4), (14, 2, 2), (16, 5, 1)]
 
 LATE_TILE = 8
-MAX_VECTOR_SLOTS = 8
-EARLY_VECTOR_SLOTS = 2
-EARLY_PAIRS = 3
-LATE_PAIRS = 4
-SCALED_BUFS = 6
-RUNS_PER_PRODUCT = 1.5
+MAX_VECTOR_SLOTS = 10
+EARLY_VECTOR_SLOTS = 3
+SCALED_BUFS = 5
+SUM_LAG = 2
+TURN_LAG = 2
+RUNS_PER_PRODUCT = 0.75
 DOTS_PER_PRODUCT = 0.5
 LEAD = 4
 GAIN_RUN = 6
@@ -184,9 +183,10 @@ def tile_dwarfattention_pa_kernel(
         load_tables(
             tc, ident, b_qkv, pos_bias, identity_bypass, gains, bias_qk, bias_v, tap_bias, bypass, gains_raw
         )
-        stream(
-            tc, ident, x_rows, out_rows, w_codes, w_planes, bias_qk, bias_v, gains_raw, tap_bias, bypass, k_all, key_blocks
-        )
+        with tc.manual_schedule(engines={mybir.EngineType.PE}):
+            stream(
+                tc, ident, x_rows, out_rows, w_codes, w_planes, bias_qk, bias_v, gains_raw, tap_bias, bypass, k_all, key_blocks
+            )
 
 
 def stream(tc, ident, x_rows, out_rows, w_codes, w_planes, bias_qk, bias_v, gains_raw, tap_bias, bypass, k_all, key_blocks):
@@ -199,10 +199,9 @@ def stream(tc, ident, x_rows, out_rows, w_codes, w_planes, bias_qk, bias_v, gain
         x_sb_of, codes_of, q_of, near_of, dots_of = {}, {}, {}, {}, {}
         gain_of, score_of, weight_of, weight_ps_of, term_of, inv_z_of = {}, {}, {}, {}, {}, {}
         v_of, sum_of, rows_of = {}, {}, {}
-        product_of, block_dots_of = {}, {}
 
         def bank(name, shape):
-            return psum.tile(shape, F32, name=name, tag="bank", bufs=5)
+            return psum.tile(shape, F32, name=name, tag="bank", bufs=4)
 
         def load_x(t):
             x_sb_of[t] = work.tile([P, D_IN], BF16, name="x_sb", bufs=1)
@@ -234,12 +233,10 @@ def stream(tc, ident, x_rows, out_rows, w_codes, w_planes, bias_qk, bias_v, gain
             )
             codes_of[t] = (codes, planes)
 
-        def project_features(t, at, half, part, home, bias_column):
+        def project_features(t, at, half, home, bias_column):
             codes, planes = codes_of[t]
-            if part == 0:
-                product_of[at] = bank("product", [P, PER_BANK, P])
-            product = product_of[at]
-            for i in range(part * PART, (part + 1) * PART):
+            product = bank("product", [P, PER_BANK, P])
+            for i in range(PER_BANK):
                 column = at + (half * PER_BANK + i) * P
                 for g in range(PASSES):
                     nc.tensor.matmul_mx(
@@ -251,8 +248,6 @@ def stream(tc, ident, x_rows, out_rows, w_codes, w_planes, bias_qk, bias_v, gain
                         start=(g == 0),
                         stop=(g == PASSES - 1),
                     )
-            if part == 0:
-                return
             first = bias_column + half * PER_BANK
             bias = bias_qk[:, first : first + PER_BANK].unsqueeze(2)
             nc.vector.tensor_tensor(
@@ -262,9 +257,9 @@ def stream(tc, ident, x_rows, out_rows, w_codes, w_planes, bias_qk, bias_v, gain
                 mask_keys(2 * t, half, product, bias)
                 mask_keys(2 * t + 1, half, product, bias)
 
-        def project_k(t, half, part):
+        def project_k(t, half):
             chunks = slice(half * PER_BANK, (half + 1) * PER_BANK)
-            project_features(t, K_AT, half, part, k_all[:, chunks, PAD + t * P : PAD + (t + 1) * P], CHUNKS)
+            project_features(t, K_AT, half, k_all[:, chunks, PAD + t * P : PAD + (t + 1) * P], CHUNKS)
 
         def open_q(t):
             q_of[t] = work.tile([P, CHUNKS, KEYS + P], F32, name="q_tile")
@@ -273,9 +268,9 @@ def stream(tc, ident, x_rows, out_rows, w_codes, w_planes, bias_qk, bias_v, gain
             if t == TILES:
                 nc.gpsimd.memset(q_of[t][:, :, KEYS:P], 0.0)
 
-        def project_q(t, half, part):
+        def project_q(t, half):
             chunks = slice(half * PER_BANK, (half + 1) * PER_BANK)
-            project_features(t, Q_AT, half, part, q_of[t][:, chunks, KEYS : KEYS + P], 0)
+            project_features(t, Q_AT, half, q_of[t][:, chunks, KEYS : KEYS + P], 0)
 
         def mask_keys(block, half, product, bias):
             chunks = slice(half * PER_BANK, (half + 1) * PER_BANK)
@@ -319,14 +314,12 @@ def stream(tc, ident, x_rows, out_rows, w_codes, w_planes, bias_qk, bias_v, gain
 
         staged_of = {}
 
-        def multiply_block(block, half, part):
+        def multiply_block(block, half):
             t, at = ((block + 1) // 2, 0) if block % 2 == 1 else (block // 2, KEYS)
-            if half == 0 and part == 0:
+            if half == 0:
                 staged_of[block] = work.tile([P, KEYS, HEADS], F32, name="staged")
-            if part == 0:
-                block_dots_of[block] = bank("block_dots", [P, PER_BANK, 2, KEYS])
-            dots = block_dots_of[block]
-            for i in range(part * PART, (part + 1) * PART):
+            dots = bank("block_dots", [P, PER_BANK, 2, KEYS])
+            for i in range(PER_BANK):
                 c = half * PER_BANK + i
                 nc.tensor.matmul(
                     out=dots[:, i, :, :].rearrange("p e m -> p (e m)"),
@@ -335,8 +328,6 @@ def stream(tc, ident, x_rows, out_rows, w_codes, w_planes, bias_qk, bias_v, gain
                     start=True,
                     stop=True,
                 )
-            if part == 0:
-                return
             heads = slice(half * HEADS_PER_BANK, (half + 1) * HEADS_PER_BANK)
             nc.vector.tensor_copy(
                 out=staged_of[block][:, :, heads], in_=dots[:].rearrange("p c e m -> p m (c e)")
@@ -390,11 +381,13 @@ def stream(tc, ident, x_rows, out_rows, w_codes, w_planes, bias_qk, bias_v, gain
             if unused > 0:
                 nc.gpsimd.memset(dots_of[t][:, 0:unused, :], 0.0)
 
+        prod_of = {}
+
         def far_dot(t, slot):
             open_dots(t)
             first = PAD + t * P - OFFSETS[slot]
             missing = max(0, -first)
-            prod = work.tile([P, CHUNKS, P], F32, name="prod")
+            prod = work.tile([P, CHUNKS, P], F32, name="prod", bufs=3)
             if missing:
                 nc.gpsimd.memset(prod[:, :, 0:missing], 0.0)
             nc.gpsimd.tensor_tensor(
@@ -403,6 +396,10 @@ def stream(tc, ident, x_rows, out_rows, w_codes, w_planes, bias_qk, bias_v, gain
                 in1=k_all[:, :, first + missing : first + P],
                 op=ALU.mult,
             )
+            prod_of[t, slot] = prod
+
+        def fold_dot(t, slot):
+            prod = prod_of[t, slot]
             for half in range(HALVES):
                 by_token = bank("by_token", [P, PER_BANK, P])
                 for i in range(PER_BANK):
@@ -486,15 +483,12 @@ def stream(tc, ident, x_rows, out_rows, w_codes, w_planes, bias_qk, bias_v, gain
             )
             weight_ps_of[t] = weight_ps
 
-        def groups_of(t):
+        def order_of(t):
             used = slots_of(t)
             theirs = [s for s in used if s < SLOTS - vector_slots(t)]
-            own = [[s] for s in used if s >= SLOTS - vector_slots(t)]
-            pairs = EARLY_PAIRS if t < LATE_TILE else LATE_PAIRS
-            paired = [theirs[2 * n : 2 * n + 2] for n in range(pairs)]
-            rest = [[s] for s in theirs[2 * pairs :]]
-            merged = [((n + 0.5) / len(part), group) for part in (paired, rest, own) for n, group in enumerate(part)]
-            return [group for at, group in sorted(merged)]
+            own = [s for s in used if s >= SLOTS - vector_slots(t)]
+            merged = [((n + 0.5) / len(part), s) for part in (theirs, own) for n, s in enumerate(part)]
+            return [s for at, s in sorted(merged)]
 
         scaled_of = {}
 
@@ -531,17 +525,10 @@ def stream(tc, ident, x_rows, out_rows, w_codes, w_planes, bias_qk, bias_v, gain
                     )
             scaled_of[t, slot] = scaled
 
-        def make_group(t, group):
-            for slot in group:
-                multiply_w_v(t, slot)
-            if len(group) == 2:
-                one, other = [scaled_of[t, slot] for slot in group]
-                nc.vector.tensor_tensor(out=one[:], in0=one[:], in1=other[:], op=ALU.add)
-
-        def add_group(t, group, is_first, is_last):
+        def add_product(t, slot, is_first, is_last):
             if is_first:
-                sum_of[t] = [psum.tile([P, PER_BANK, P], F32, name="sum_ps%d" % b) for b in range(HALVES)]
-            scaled = scaled_of[t, group[0]]
+                sum_of[t] = [psum.tile([P, PER_BANK, P], F32, name="sum_ps", tag="sum", bufs=3) for b in range(HALVES)]
+            scaled = scaled_of[t, slot]
             for c in range(CHUNKS):
                 nc.tensor.matmul(
                     out=sum_of[t][c // PER_BANK][:, c % PER_BANK, :],
@@ -552,11 +539,17 @@ def stream(tc, ident, x_rows, out_rows, w_codes, w_planes, bias_qk, bias_v, gain
                     stop=(is_last and c % PER_BANK == PER_BANK - 1),
                 )
 
-        def finish_output(t):
+        sum_sb_of = {}
+
+        def copy_sums(t):
             sum_flat = work.tile([P, WIDTH], F32, name="sum_sb", tag="scaled", bufs=SCALED_BUFS)
             sum_sb = sum_flat[:].rearrange("p (c n) -> p c n", c=CHUNKS)
-            for b in range(HALVES):
-                nc.scalar.copy(out=sum_sb[:, b * PER_BANK : (b + 1) * PER_BANK, :], in_=sum_of[t][b][:])
+            nc.scalar.copy(out=sum_sb[:, 0:PER_BANK, :], in_=sum_of[t][0][:])
+            nc.vector.tensor_copy(out=sum_sb[:, PER_BANK:CHUNKS, :], in_=sum_of[t][1][:])
+            sum_sb_of[t] = sum_sb
+
+        def turn_sums(t):
+            sum_sb = sum_sb_of[t]
             rows = work.tile([P, HEADS, HEAD_DIM], F32, name="rows", bufs=3)
             for b in range(HALVES):
                 rows_ps = bank("rows_ps", [P, PER_BANK, P])
@@ -587,13 +580,11 @@ def stream(tc, ident, x_rows, out_rows, w_codes, w_planes, bias_qk, bias_v, gain
 
             def project(f):
                 for half in range(HALVES):
-                    for part in range(PER_BANK // PART):
-                        runs.append([lambda half=half, part=part: f(t, half, part)])
+                    runs.append([lambda half=half: f(t, half)])
 
             def multiply(block):
                 for half in range(HALVES):
-                    for part in range(PER_BANK // PART):
-                        runs.append([lambda half=half, part=part: multiply_block(block, half, part)])
+                    runs.append([lambda half=half: multiply_block(block, half)])
                 runs[-1].append(lambda: write_block(block))
                 if block % 2 == 1:
                     runs[-1].append(lambda: read_block(block - 1))
@@ -611,13 +602,13 @@ def stream(tc, ident, x_rows, out_rows, w_codes, w_planes, bias_qk, bias_v, gain
             if t + 1 < TILES:
                 runs[-1].append(lambda: quantise_x(t + 1))
             if t >= 2:
-                runs[3].append(lambda: gather_near(t - 2))
+                runs[2].append(lambda: gather_near(t - 2))
             runs[1] = runs[0] + runs[1]
             return [lambda run=run: [task() for task in run] for run in runs[1:]]
 
         projection = [(t, task) for t in range(TILES + 1) for task in projection_tasks(t)]
-        far_dots = [(t, task) for t in range(TILES) for task in dot_tasks(t)]
-        issued = {"runs": 0, "dots": 0}
+        far_dots = [(t, slot) for t in range(TILES) for slot in slots_of(t) if slot < FAR_SLOTS]
+        issued = {"runs": 0, "dots": 0, "folds": 0}
 
         def next_tile(tasks, name):
             return tasks[issued[name]][0] if issued[name] < len(tasks) else TILES + 1
@@ -627,10 +618,16 @@ def stream(tc, ident, x_rows, out_rows, w_codes, w_planes, bias_qk, bias_v, gain
                 issued["runs"] += 1
                 projection[issued["runs"] - 1][1]()
 
+        def issue_fold():
+            issued["folds"] += 1
+            fold_dot(*far_dots[issued["folds"] - 1])
+
         def issue_dot():
-            if issued["dots"] < len(far_dots) and far_dots[issued["dots"]][0] < next_tile(projection, "runs"):
+            if next_tile(far_dots, "dots") < min(next_tile(projection, "runs"), TILES):
                 issued["dots"] += 1
-                far_dots[issued["dots"] - 1][1]()
+                far_dot(*far_dots[issued["dots"] - 1])
+            if issued["folds"] < issued["dots"] - 1:
+                issue_fold()
 
         def prepare_output(t):
             needed = t + 1 if t < unit_of(BLOCKS - 2) else TILES
@@ -638,6 +635,8 @@ def stream(tc, ident, x_rows, out_rows, w_codes, w_planes, bias_qk, bias_v, gain
                 issue_run()
             while next_tile(far_dots, "dots") <= t:
                 issue_dot()
+            while next_tile(far_dots, "folds") <= t:
+                issue_fold()
             gather_near(t)
             scale_gains(t)
             score_entries(t)
@@ -653,27 +652,36 @@ def stream(tc, ident, x_rows, out_rows, w_codes, w_planes, bias_qk, bias_v, gain
         quantise_x(0)
         prepare_output(0)
         owed = {"runs": 0.0, "dots": 0.0}
-        for t in range(TILES):
-            groups = groups_of(t)
-            show_weights(t)
-            for n in range(len(groups) + 1):
-                if n == 2 * len(groups) // 3 and t + 1 < TILES:
+        products = [(t, n) for t in range(TILES) for n in range(len(slots_of(t)))]
+        for beat in range(len(products) + SUM_LAG + TURN_LAG):
+            if beat < len(products):
+                t, n = products[beat]
+                order = order_of(t)
+                if n == 0:
+                    show_weights(t)
+                multiply_w_v(t, order[n])
+                if n == 2 * len(order) // 3 and t + 1 < TILES:
                     prepare_output(t + 1)
-                if n < len(groups):
-                    make_group(t, groups[n])
-                    owed["runs"] += RUNS_PER_PRODUCT * len(groups[n])
-                    owed["dots"] += DOTS_PER_PRODUCT * len(groups[n])
-                if n > 0:
-                    add_group(t, groups[n - 1], n == 1, n == len(groups))
-                while owed["runs"] >= 1.0:
-                    owed["runs"] -= 1.0
-                    if next_tile(projection, "runs") < t + LEAD - 1:
-                        issue_run()
-                while owed["dots"] >= 1.0:
-                    owed["dots"] -= 1.0
-                    issue_dot()
-            finish_output(t)
-            if t >= 2:
-                store(t - 2)
+                owed["runs"] += RUNS_PER_PRODUCT
+                owed["dots"] += DOTS_PER_PRODUCT
+            if 0 <= beat - SUM_LAG < len(products):
+                t, n = products[beat - SUM_LAG]
+                order = order_of(t)
+                add_product(t, order[n], n == 0, n == len(order) - 1)
+                if n == len(order) - 1:
+                    copy_sums(t)
+            if 0 <= beat - SUM_LAG - TURN_LAG < len(products):
+                t, n = products[beat - SUM_LAG - TURN_LAG]
+                if n == len(slots_of(t)) - 1:
+                    turn_sums(t)
+                    if t >= 2:
+                        store(t - 2)
+            if owed["runs"] >= 1.0:
+                owed["runs"] -= 1.0
+                if next_tile(projection, "runs") < products[min(beat, len(products) - 1)][0] + LEAD - 1:
+                    issue_run()
+            if owed["dots"] >= 1.0:
+                owed["dots"] -= 1.0
+                issue_dot()
         store(TILES - 2)
         store(TILES - 1)

@@ -54,6 +54,7 @@ NEAR_RUNS = [(8, 2, 16), (10, 2, 8), (12, 2, 4), (14, 2, 2), (16, 5, 1)]
 LATE_TILE = 8
 MAX_VECTOR_SLOTS = 10
 EARLY_VECTOR_SLOTS = 3
+SHIFTED_BUFS = 5
 SCALED_BUFS = 5
 SUM_LAG = 2
 TURN_LAG = 2
@@ -86,65 +87,6 @@ def vector_slots(t):
     return EARLY_VECTOR_SLOTS if t < LATE_TILE else MAX_VECTOR_SLOTS
 
 
-def load_tables(tc, ident, b_qkv, pos_bias, identity_bypass, gains, bias_qk, bias_v, tap_bias, bypass, gains_raw):
-    nc = tc.nc
-    with tc.tile_pool(name="setup", bufs=1) as setup, tc.psum_pool(name="setup_ps", bufs=1) as psum:
-        bias_rows = setup.tile([P, P], BF16, name="bias_rows")
-        nc.vector.memset(bias_rows[:], 0.0)
-        nc.sync.dma_start(
-            out=bias_rows[0 : 2 * CHUNKS, :], in_=b_qkv[Q_AT : Q_AT + 2 * WIDTH].rearrange("(c p) -> c p", p=P)
-        )
-        bias_rows_f32 = setup.tile([P, P], F32, name="bias_rows_f32")
-        nc.vector.tensor_copy(out=bias_rows_f32[:], in_=bias_rows[:])
-        bias_ps = psum.tile([P, P], F32, name="bias_ps")
-        nc.tensor.transpose(out=bias_ps[:], in_=bias_rows_f32[:], identity=ident[:])
-        nc.vector.tensor_copy(out=bias_qk[:], in_=bias_ps[:, 0 : 2 * CHUNKS])
-        nc.sync.dma_start(out=bias_v[:], in_=b_qkv[V_AT : V_AT + WIDTH].partition_broadcast(P))
-
-        pos_raw = setup.tile([P, SCALES * TAUS * HEADS], BF16, name="pos_raw")
-        nc.sync.dma_start(out=pos_raw[:], in_=pos_bias.rearrange("r h -> (r h)").partition_broadcast(P))
-        pos_view = pos_raw[:].rearrange("p (j t h) -> p j t h", t=TAUS, h=HEADS)
-        nc.gpsimd.memset(tap_bias[:, LOCAL, :], 0.0)
-        for first, count, s0, tau in ENTRY_RUNS:
-            for e in range(count):
-                nc.gpsimd.tensor_copy(out=tap_bias[:, first + e, :], in_=pos_view[:, SCALES - 1 - s0 - e, tau, :])
-
-        bypass_raw = setup.tile([P, HEADS], BF16, name="bypass_raw")
-        nc.sync.dma_start(out=bypass_raw[:], in_=identity_bypass.partition_broadcast(P))
-        bypass_f32 = setup.tile([P, HEADS], F32, name="bypass_f32")
-        nc.vector.tensor_copy(out=bypass_f32[:], in_=bypass_raw[:])
-        tail = setup.tile([P, HEADS], F32, name="tail")
-        nc.scalar.activation(out=tail[:], in_=bypass_f32[:], func=ACT.Abs)
-        nc.scalar.activation(out=tail[:], in_=tail[:], func=ACT.Exp, scale=-1.0)
-        nc.vector.tensor_scalar_add(out=tail[:], in0=tail[:], scalar1=1.0)
-        nc.scalar.activation(out=tail[:], in_=tail[:], func=ACT.Ln)
-        nc.vector.scalar_tensor_tensor(
-            out=bypass[:], in0=bypass_f32[:], scalar=0.0, in1=tail[:], op0=ALU.max, op1=ALU.add
-        )
-
-        ident_bf16 = setup.tile([P, P], BF16, name="ident_bf16")
-        make_identity(nc, ident_bf16[:])
-        gain_rows = gains.rearrange("b h (t n) j -> (b h t) (n j)", n=P)
-        for first_row in (0, HEADS * TILES - P):
-            new = 0 if first_row == 0 else P - first_row
-            by_row = setup.tile([P, P * SCALES], BF16, name="by_row%d" % first_row)
-            nc.sync.dma_start(out=by_row[:], in_=gain_rows[first_row : first_row + P, :])
-            for j0 in range(0, SCALES, GAIN_RUN):
-                count = min(GAIN_RUN, SCALES - j0)
-                by_token = psum.tile([P, GAIN_RUN, P], BF16, name="by_token")
-                for j in range(j0, j0 + count):
-                    nc.tensor.transpose(
-                        out=by_token[:, j0 + count - 1 - j, :],
-                        in_=by_row[:, j : P * SCALES : SCALES],
-                        identity=ident_bf16[:],
-                    )
-                s0 = SCALES - j0 - count
-                nc.scalar.copy(
-                    out=gains_raw[:, first_row + new : first_row + P, s0 : s0 + count],
-                    in_=by_token[:, 0:count, new:P].rearrange("p j r -> p r j"),
-                )
-
-
 def tile_dwarfattention_pa_kernel(
     tc, x, W_qkv_words, W_qkv_scales, b_qkv, gains, pos_bias, identity_bypass, out
 ):
@@ -168,29 +110,19 @@ def tile_dwarfattention_pa_kernel(
             nc.gpsimd.memset(kb[:], 0.0)
         w_planes = keep.tile([P, PASSES, 3 * WIDTH], U8, name="w_planes", align_bytes=64)
         nc.vector.memset(w_planes[:].bitcast(I32), 0)
-        for quadrant in range(4):
-            nc.sync.dma_start(
-                out=w_planes[32 * quadrant : 32 * quadrant + 4, :, :].bitcast(I32),
-                in_=W_qkv_scales[:, 4 * quadrant : 4 * quadrant + 4, :].bitcast(I32).rearrange("g r n -> r g n"),
-            )
         w_codes = keep.tile([P, PASSES, 2 * 3 * WIDTH], U8, name="w_codes", align_bytes=64)
-        for at in (K_AT, Q_AT, V_AT):
-            for g in range(PASSES):
-                nc.sync.dma_start(
-                    out=w_codes[:, g, 2 * at : 2 * (at + WIDTH)].bitcast(I32),
-                    in_=W_qkv_words[g, :, 2 * at : 2 * (at + WIDTH)].bitcast(I32),
-                )
-        load_tables(
-            tc, ident, b_qkv, pos_bias, identity_bypass, gains, bias_qk, bias_v, tap_bias, bypass, gains_raw
-        )
+        inputs = (W_qkv_words, W_qkv_scales, b_qkv, pos_bias, identity_bypass, gains)
         with tc.manual_schedule(engines={mybir.EngineType.PE}):
             stream(
-                tc, ident, x_rows, out_rows, w_codes, w_planes, bias_qk, bias_v, gains_raw, tap_bias, bypass, k_all, key_blocks
+                tc, ident, x_rows, out_rows, inputs, w_codes, w_planes, bias_qk, bias_v, gains_raw, tap_bias, bypass, k_all, key_blocks
             )
 
 
-def stream(tc, ident, x_rows, out_rows, w_codes, w_planes, bias_qk, bias_v, gains_raw, tap_bias, bypass, k_all, key_blocks):
+def stream(
+    tc, ident, x_rows, out_rows, inputs, w_codes, w_planes, bias_qk, bias_v, gains_raw, tap_bias, bypass, k_all, key_blocks
+):
     nc = tc.nc
+    w_words, w_scales, b_qkv, pos_bias, identity_bypass, gains = inputs
     with (
         tc.tile_pool(name="work", bufs=2) as work,
         tc.tile_pool(name="taps", bufs=1) as taps,
@@ -202,6 +134,80 @@ def stream(tc, ident, x_rows, out_rows, w_codes, w_planes, bias_qk, bias_v, gain
 
         def bank(name, shape):
             return psum.tile(shape, F32, name=name, tag="bank", bufs=4)
+
+        def load_weight():
+            for quadrant in range(4):
+                nc.sync.dma_start(
+                    out=w_planes[32 * quadrant : 32 * quadrant + 4, :, :].bitcast(I32),
+                    in_=w_scales[:, 4 * quadrant : 4 * quadrant + 4, :].bitcast(I32).rearrange("g r n -> r g n"),
+                )
+            for at in (Q_AT, K_AT, V_AT):
+                for g in range(PASSES):
+                    nc.sync.dma_start(
+                        out=w_codes[:, g, 2 * at : 2 * (at + WIDTH)].bitcast(I32),
+                        in_=w_words[g, :, 2 * at : 2 * (at + WIDTH)].bitcast(I32),
+                    )
+
+        def setup_tile(name, shape, dtype):
+            return work.tile(shape, dtype, name=name, tag="shifted", bufs=SHIFTED_BUFS)
+
+        def load_biases():
+            bias_rows = setup_tile("bias_rows", [P, P], BF16)
+            nc.vector.memset(bias_rows[:], 0.0)
+            nc.sync.dma_start(
+                out=bias_rows[0 : 2 * CHUNKS, :], in_=b_qkv[Q_AT : Q_AT + 2 * WIDTH].rearrange("(c p) -> c p", p=P)
+            )
+            bias_rows_f32 = setup_tile("bias_rows_f32", [P, P], F32)
+            nc.vector.tensor_copy(out=bias_rows_f32[:], in_=bias_rows[:])
+            bias_ps = bank("bias_ps", [P, P])
+            nc.tensor.transpose(out=bias_ps[:], in_=bias_rows_f32[:], identity=ident[:])
+            nc.vector.tensor_copy(out=bias_qk[:], in_=bias_ps[:, 0 : 2 * CHUNKS])
+
+        def load_tables():
+            nc.sync.dma_start(out=bias_v[:], in_=b_qkv[V_AT : V_AT + WIDTH].partition_broadcast(P))
+
+            pos_raw = setup_tile("pos_raw", [P, SCALES * TAUS * HEADS], BF16)
+            nc.sync.dma_start(out=pos_raw[:], in_=pos_bias.rearrange("r h -> (r h)").partition_broadcast(P))
+            pos_view = pos_raw[:].rearrange("p (j t h) -> p j t h", t=TAUS, h=HEADS)
+            nc.gpsimd.memset(tap_bias[:, LOCAL, :], 0.0)
+            for first, count, s0, tau in ENTRY_RUNS:
+                for e in range(count):
+                    nc.gpsimd.tensor_copy(out=tap_bias[:, first + e, :], in_=pos_view[:, SCALES - 1 - s0 - e, tau, :])
+
+            bypass_raw = taps.tile([P, HEADS], BF16, name="bypass_raw")
+            nc.sync.dma_start(out=bypass_raw[:], in_=identity_bypass.partition_broadcast(P))
+            bypass_f32 = taps.tile([P, HEADS], F32, name="bypass_f32")
+            nc.vector.tensor_copy(out=bypass_f32[:], in_=bypass_raw[:])
+            tail = taps.tile([P, HEADS], F32, name="tail")
+            nc.scalar.activation(out=tail[:], in_=bypass_f32[:], func=ACT.Abs)
+            nc.scalar.activation(out=tail[:], in_=tail[:], func=ACT.Exp, scale=-1.0)
+            nc.vector.tensor_scalar_add(out=tail[:], in0=tail[:], scalar1=1.0)
+            nc.scalar.activation(out=tail[:], in_=tail[:], func=ACT.Ln)
+            nc.vector.scalar_tensor_tensor(
+                out=bypass[:], in0=bypass_f32[:], scalar=0.0, in1=tail[:], op0=ALU.max, op1=ALU.add
+            )
+
+            ident_bf16 = setup_tile("ident_bf16", [P, P], BF16)
+            nc.vector.tensor_copy(out=ident_bf16[:], in_=ident[:])
+            gain_rows = gains.rearrange("b h (t n) j -> (b h t) (n j)", n=P)
+            for first_row in (0, HEADS * TILES - P):
+                new = 0 if first_row == 0 else P - first_row
+                by_row = setup_tile("by_row", [P, P * SCALES], BF16)
+                nc.sync.dma_start(out=by_row[:], in_=gain_rows[first_row : first_row + P, :])
+                for j0 in range(0, SCALES, GAIN_RUN):
+                    count = min(GAIN_RUN, SCALES - j0)
+                    by_scale = psum.tile([P, GAIN_RUN, P], BF16, name="by_scale", tag="bank", bufs=4)
+                    for j in range(j0, j0 + count):
+                        nc.tensor.transpose(
+                            out=by_scale[:, j0 + count - 1 - j, :],
+                            in_=by_row[:, j : P * SCALES : SCALES],
+                            identity=ident_bf16[:],
+                        )
+                    s0 = SCALES - j0 - count
+                    nc.scalar.copy(
+                        out=gains_raw[:, first_row + new : first_row + P, s0 : s0 + count],
+                        in_=by_scale[:, 0:count, new:P].rearrange("p j r -> p r j"),
+                    )
 
         def load_x(t):
             x_sb_of[t] = work.tile([P, D_IN], BF16, name="x_sb", bufs=1)
@@ -499,7 +505,7 @@ def stream(tc, ident, x_rows, out_rows, w_codes, w_planes, bias_qk, bias_v, gain
             else:
                 first = t * P - offset
                 missing = max(0, -first)
-                shifted = work.tile([P, WIDTH], F32, name="shifted", bufs=5)
+                shifted = work.tile([P, WIDTH], F32, name="shifted", bufs=SHIFTED_BUFS)
                 if missing:
                     nc.gpsimd.memset(shifted[0:missing, :], 0.0)
                 split = P - (P - missing) % DMA_ENGINES
@@ -644,12 +650,17 @@ def stream(tc, ident, x_rows, out_rows, w_codes, w_planes, bias_qk, bias_v, gain
             project_v(t)
 
         load_x(0)
+        load_weight()
+        load_biases()
         for part in range(2):
             quarter = slice(part * ROW // 4, (part + 1) * ROW // 4)
             nc.sync.dma_start(
                 out=scratch_rows(0)[:, quarter].rearrange("r (c n) -> r c n", n=PAD), in_=k_all[0:KEYS, :, 0:PAD]
             )
         quantise_x(0)
+        while next_tile(projection, "runs") == 0:
+            issue_run()
+        load_tables()
         prepare_output(0)
         owed = {"runs": 0.0, "dots": 0.0}
         products = [(t, n) for t in range(TILES) for n in range(len(slots_of(t)))]

import concourse.mybir as mybir
from concourse.masks import make_identity

F32 = mybir.dt.float32
BF16 = mybir.dt.bfloat16
I32 = mybir.dt.int32
U32 = mybir.dt.uint32
U8 = mybir.dt.uint8
FP8X4 = mybir.dt.float8_e4m3fn_x4
FP4X4 = mybir.dt.float4_e2m1fn_x4
ALU = mybir.AluOpType
ACT = mybir.ActivationFunctionType
AXIS = mybir.AxisListType

P = 128
TOKENS = 1536
D_IN = 1024
HEADS = 16
HEAD_DIM = 64
WIDTH = HEADS * HEAD_DIM
Q_AT = 0
K_AT = WIDTH
V_AT = 2 * WIDTH
SCALES = 11
TAUS = 4
D4 = [0.4829629131445341, 0.8365163037378079, 0.2241438680420134, -0.1294095225512604]

PACK = 4
K_PASS = P * PACK
PASSES = D_IN // K_PASS
BANK = 512
TILES = TOKENS // P
CHUNKS = WIDTH // P
PER_BANK = BANK // P
HALVES = CHUNKS // PER_BANK
HEADS_PER_BANK = HEADS // HALVES
PAD = P // 2

KEYS = HEAD_DIM
BLOCKS = TOKENS // KEYS
NEAR_MAX = KEYS
ROW = 2 * KEYS * HEADS
UNIT = P * WIDTH

OFFSETS = sorted(set(tau << j for j in range(SCALES) for tau in range(TAUS) if (tau << j) < TOKENS), reverse=True)
SLOTS = len(OFFSETS)
HERE_SLOT = SLOTS - 1
assert OFFSETS[HERE_SLOT] == 0
assert all(OFFSETS[2 * i] == 1 << (10 - i) for i in range(10))
assert all(OFFSETS[2 * i + 1] == 3 << (8 - i) for i in range(9)) and OFFSETS[19] == 1
FAR_SLOTS = len([o for o in OFFSETS if o > NEAR_MAX])
NEAR_RUNS = [(8, 2, 16), (10, 2, 8), (12, 2, 4), (14, 2, 2), (16, 5, 1)]

LATE_TILE = 8
MAX_VECTOR_SLOTS = 10
EARLY_VECTOR_SLOTS = 3
SHIFTED_BUFS = 5
SCALED_BUFS = 5
SUM_LAG = 2
TURN_LAG = 2
RUNS_PER_PRODUCT = 0.75
DOTS_PER_PRODUCT = 0.5
LEAD = 4
GAIN_RUN = 6
DMA_ENGINES = 16

ENTRY_RUNS = [(0, 11, 0, 0), (12, 10, 0, 1), (22, 10, 1, 2), (32, 9, 2, 3), (41, 1, 10, 1)]
LOCAL = 11
HERE = 12
EVEN = 10
ODD_FIRST = HERE + 2 * EVEN
ENTRIES = ODD_FIRST + EVEN
LAST = ENTRIES - 1

FLOPS = 2 * TOKENS * D_IN * 3 * WIDTH + 4 * TOKENS * WIDTH * ENTRIES


def slots_of(t):
    return [i for i in range(SLOTS) if OFFSETS[i] <= t * P + P - 1]


def unit_of(block):
    return 9 + block % 3 if block < BLOCKS - 3 else (10 if block < BLOCKS - 1 else 11)


def vector_slots(t):
    return EARLY_VECTOR_SLOTS if t < LATE_TILE else MAX_VECTOR_SLOTS


def tile_dwarfattention_pa_kernel(
    tc, x, W_qkv_words, W_qkv_scales, b_qkv, gains, pos_bias, identity_bypass, out
):
    nc = tc.nc
    out_rows = out.flatten_outer_dims()
    x_rows = x.flatten_outer_dims()
    with (
        tc.tile_pool(name="keep", bufs=1) as keep,
    ):
        ident = keep.tile([P, P], F32, name="ident")
        make_identity(nc, ident[:])
        tap_bias = keep.tile([P, ENTRIES, HEADS], F32, name="tap_bias")
        bypass = keep.tile([P, HEADS], F32, name="bypass")
        bias_qk = keep.tile([P, 2 * CHUNKS], F32, name="bias_qk")
        bias_v = keep.tile([P, WIDTH], BF16, name="bias_v")
        gains_raw = keep.tile([P, HEADS * TILES, SCALES], BF16, name="gains_raw")
        k_all = keep.tile([P, CHUNKS, PAD + TOKENS], F32, name="k_all")
        nc.gpsimd.memset(k_all[:, :, 0:PAD], 0.0)
        key_blocks = [keep.tile([P, CHUNKS, 2, KEYS], F32, name="key_block%d" % i) for i in range(2)]
        for kb in key_blocks:
            nc.gpsimd.memset(kb[:], 0.0)
        w_planes = keep.tile([P, PASSES, 3 * WIDTH], U8, name="w_planes", align_bytes=64)
        nc.vector.memset(w_planes[:].bitcast(I32), 0)
        w_codes = keep.tile([P, PASSES, 2 * 3 * WIDTH], U8, name="w_codes", align_bytes=64)
        inputs = (W_qkv_words, W_qkv_scales, b_qkv, pos_bias, identity_bypass, gains)
        with tc.manual_schedule(engines={mybir.EngineType.PE}):
            stream(
                tc, ident, x_rows, out_rows, inputs, w_codes, w_planes, bias_qk, bias_v, gains_raw, tap_bias, bypass, k_all, key_blocks
            )


def stream(
    tc, ident, x_rows, out_rows, inputs, w_codes, w_planes, bias_qk, bias_v, gains_raw, tap_bias, bypass, k_all, key_blocks
):
    nc = tc.nc
    w_words, w_scales, b_qkv, pos_bias, identity_bypass, gains = inputs
    with (
        tc.tile_pool(name="work", bufs=2) as work,
        tc.tile_pool(name="taps", bufs=1) as taps,
        tc.psum_pool(name="ps", bufs=1) as psum,
    ):
        x_sb_of, codes_of, q_of, near_of, dots_of = {}, {}, {}, {}, {}
        gain_of, score_of, weight_of, weight_ps_of, term_of, inv_z_of = {}, {}, {}, {}, {}, {}
        v_of, sum_of, rows_of = {}, {}, {}

        def bank(name, shape):
            return psum.tile(shape, F32, name=name, tag="bank", bufs=4)

        def load_weight():
            for quadrant in range(4):
                nc.sync.dma_start(
                    out=w_planes[32 * quadrant : 32 * quadrant + 4, :, :].bitcast(I32),
                    in_=w_scales[:, 4 * quadrant : 4 * quadrant + 4, :].bitcast(I32).rearrange("g r n -> r g n"),
                )
            for at in (Q_AT, K_AT, V_AT):
                for g in range(PASSES):
                    nc.sync.dma_start(
                        out=w_codes[:, g, 2 * at : 2 * (at + WIDTH)].bitcast(I32),
                        in_=w_words[g, :, 2 * at : 2 * (at + WIDTH)].bitcast(I32),
                    )

        def setup_tile(name, shape, dtype):
            return work.tile(shape, dtype, name=name, tag="shifted", bufs=SHIFTED_BUFS)

        def load_biases():
            bias_rows = setup_tile("bias_rows", [P, P], BF16)
            nc.vector.memset(bias_rows[:], 0.0)
            nc.sync.dma_start(
                out=bias_rows[0 : 2 * CHUNKS, :], in_=b_qkv[Q_AT : Q_AT + 2 * WIDTH].rearrange("(c p) -> c p", p=P)
            )
            bias_rows_f32 = setup_tile("bias_rows_f32", [P, P], F32)
            nc.vector.tensor_copy(out=bias_rows_f32[:], in_=bias_rows[:])
            bias_ps = bank("bias_ps", [P, P])
            nc.tensor.transpose(out=bias_ps[:], in_=bias_rows_f32[:], identity=ident[:])
            nc.vector.tensor_copy(out=bias_qk[:], in_=bias_ps[:, 0 : 2 * CHUNKS])

        def load_tables():
            nc.sync.dma_start(out=bias_v[:], in_=b_qkv[V_AT : V_AT + WIDTH].partition_broadcast(P))

            pos_raw = setup_tile("pos_raw", [P, SCALES * TAUS * HEADS], BF16)
            nc.sync.dma_start(out=pos_raw[:], in_=pos_bias.rearrange("r h -> (r h)").partition_broadcast(P))
            pos_view = pos_raw[:].rearrange("p (j t h) -> p j t h", t=TAUS, h=HEADS)
            nc.gpsimd.memset(tap_bias[:, LOCAL, :], 0.0)
            for first, count, s0, tau in ENTRY_RUNS:
                for e in range(count):
                    nc.gpsimd.tensor_copy(out=tap_bias[:, first + e, :], in_=pos_view[:, SCALES - 1 - s0 - e, tau, :])

            bypass_raw = taps.tile([P, HEADS], BF16, name="bypass_raw")
            nc.sync.dma_start(out=bypass_raw[:], in_=identity_bypass.partition_broadcast(P))
            bypass_f32 = taps.tile([P, HEADS], F32, name="bypass_f32")
            nc.vector.tensor_copy(out=bypass_f32[:], in_=bypass_raw[:])
            tail = taps.tile([P, HEADS], F32, name="tail")
            nc.scalar.activation(out=tail[:], in_=bypass_f32[:], func=ACT.Abs)
            nc.scalar.activation(out=tail[:], in_=tail[:], func=ACT.Exp, scale=-1.0)
            nc.vector.tensor_scalar_add(out=tail[:], in0=tail[:], scalar1=1.0)
            nc.scalar.activation(out=tail[:], in_=tail[:], func=ACT.Ln)
            nc.vector.scalar_tensor_tensor(
                out=bypass[:], in0=bypass_f32[:], scalar=0.0, in1=tail[:], op0=ALU.max, op1=ALU.add
            )

            ident_bf16 = setup_tile("ident_bf16", [P, P], BF16)
            nc.vector.tensor_copy(out=ident_bf16[:], in_=ident[:])
            gain_rows = gains.rearrange("b h (t n) j -> (b h t) (n j)", n=P)
            for first_row in (0, HEADS * TILES - P):
                new = 0 if first_row == 0 else P - first_row
                by_row = setup_tile("by_row", [P, P * SCALES], BF16)
                nc.sync.dma_start(out=by_row[:], in_=gain_rows[first_row : first_row + P, :])
                for j0 in range(0, SCALES, GAIN_RUN):
                    count = min(GAIN_RUN, SCALES - j0)
                    by_scale = psum.tile([P, GAIN_RUN, P], BF16, name="by_scale", tag="bank", bufs=4)
                    for j in range(j0, j0 + count):
                        nc.tensor.transpose(
                            out=by_scale[:, j0 + count - 1 - j, :],
                            in_=by_row[:, j : P * SCALES : SCALES],
                            identity=ident_bf16[:],
                        )
                    s0 = SCALES - j0 - count
                    nc.scalar.copy(
                        out=gains_raw[:, first_row + new : first_row + P, s0 : s0 + count],
                        in_=by_scale[:, 0:count, new:P].rearrange("p j r -> p r j"),
                    )

        def load_x(t):
            x_sb_of[t] = work.tile([P, D_IN], BF16, name="x_sb", bufs=1)
            nc.sync.dma_start(out=x_sb_of[t][:], in_=x_rows[t * P : (t + 1) * P, :])

        def quantise_x(t):
            turned = bank("turned", [P, PASSES, 2, P])
            words = x_sb_of[t][:].bitcast(F32)
            per_pass = K_PASS // 2
            for g in range(PASSES):
                for u in range(2):
                    nc.tensor.transpose(
                        out=turned[:, g, u, :], in_=words[:, per_pass * g + u : per_pass * (g + 1) : 2], identity=ident[:]
                    )
            grouped = work.tile([P, PASSES, P, PACK], BF16, name="grouped", align_bytes=64, bufs=1)
            nc.scalar.copy(
                out=grouped[:]
                .rearrange("p g r t -> p (g r t)")
                .bitcast(F32)
                .rearrange("p (g r u) -> p g r u", g=PASSES, u=2),
                in_=turned[:].rearrange("p g u r -> p g r u"),
            )
            codes = work.tile([P, PASSES, P], U32, name="x_codes", align_bytes=64, bufs=LEAD)
            planes = work.tile([P, PASSES, P], U8, name="x_planes", align_bytes=64, bufs=LEAD)
            nc.vector.quantize_mx(
                out=codes[:].rearrange("p g r -> p (g r)").bitcast(FP8X4),
                scales=planes[:].rearrange("p g r -> p (g r)"),
                in_=grouped[:].rearrange("p g r t -> p (g r t)"),
            )
            codes_of[t] = (codes, planes)

        def project_features(t, at, half, home, bias_column):
            codes, planes = codes_of[t]
            product = bank("product", [P, PER_BANK, P])
            for i in range(PER_BANK):
                column = at + (half * PER_BANK + i) * P
                for g in range(PASSES):
                    nc.tensor.matmul_mx(
                        out=product[:, i, :],
                        lhsT=w_codes[:, g, 2 * column : 2 * (column + P)].bitcast(FP4X4),
                        lhsT_scale=w_planes[:, g, column : column + P],
                        rhs=codes[:, g, :].bitcast(FP8X4),
                        rhs_scale=planes[:, g, :],
                        start=(g == 0),
                        stop=(g == PASSES - 1),
                    )
            first = bias_column + half * PER_BANK
            bias = bias_qk[:, first : first + PER_BANK].unsqueeze(2)
            nc.vector.tensor_tensor(
                out=home, in0=product[:], in1=bias.to_broadcast([P, PER_BANK, P]), op=ALU.add
            )
            if at == K_AT:
                mask_keys(2 * t, half, product, bias)
                mask_keys(2 * t + 1, half, product, bias)

        def project_k(t, half):
            chunks = slice(half * PER_BANK, (half + 1) * PER_BANK)
            project_features(t, K_AT, half, k_all[:, chunks, PAD + t * P : PAD + (t + 1) * P], CHUNKS)

        def open_q(t):
            q_of[t] = work.tile([P, CHUNKS, KEYS + P], F32, name="q_tile")
            if t > 0:
                nc.scalar.copy(out=q_of[t][:, :, 0:KEYS], in_=q_of[t - 1][:, :, P : P + KEYS])
            if t == TILES:
                nc.gpsimd.memset(q_of[t][:, :, KEYS:P], 0.0)

        def project_q(t, half):
            chunks = slice(half * PER_BANK, (half + 1) * PER_BANK)
            project_features(t, Q_AT, half, q_of[t][:, chunks, KEYS : KEYS + P], 0)

        def mask_keys(block, half, product, bias):
            chunks = slice(half * PER_BANK, (half + 1) * PER_BANK)
            tokens = slice(block % 2 * KEYS, (block % 2 + 1) * KEYS)
            for odd in range(2):
                rows = slice(odd * HEAD_DIM, (odd + 1) * HEAD_DIM)
                nc.vector.tensor_tensor(
                    out=key_blocks[block % 2][rows, chunks, odd, :],
                    in0=product[rows, :, tokens],
                    in1=bias[rows].to_broadcast([HEAD_DIM, PER_BANK, KEYS]),
                    op=ALU.add,
                )

        def project_v(t):
            codes, planes = codes_of[t]
            v_tok = work.tile([P, WIDTH], F32, name="v_tok", bufs=10)
            for half in range(HALVES):
                column = V_AT + half * BANK
                product = bank("product_v", [P, BANK])
                for g in range(PASSES):
                    nc.tensor.matmul_mx(
                        out=product[:],
                        lhsT=codes[:, g, :].bitcast(FP8X4),
                        lhsT_scale=planes[:, g, :],
                        rhs=w_codes[:, g, 2 * column : 2 * (column + BANK)].bitcast(FP4X4),
                        rhs_scale=w_planes[:, g, column : column + BANK],
                        start=(g == 0),
                        stop=(g == PASSES - 1),
                    )
                features = slice(half * BANK, (half + 1) * BANK)
                nc.vector.tensor_tensor(out=v_tok[:, features], in0=product[:], in1=bias_v[:, features], op=ALU.add)
            v_of[t] = v_tok
            nc.sync.dma_start(out=out_rows[t * P : (t + 1) * P, :], in_=v_tok[:])

        def scratch(block):
            first = unit_of(block) * P
            return out_rows[first : first + P, :]

        def scratch_rows(block):
            return scratch(block).rearrange("(n two) f -> n (two f)", two=2)

        staged_of = {}

        def multiply_block(block, half):
            t, at = ((block + 1) // 2, 0) if block % 2 == 1 else (block // 2, KEYS)
            if half == 0:
                staged_of[block] = work.tile([P, KEYS, HEADS], F32, name="staged")
            dots = bank("block_dots", [P, PER_BANK, 2, KEYS])
            for i in range(PER_BANK):
                c = half * PER_BANK + i
                nc.tensor.matmul(
                    out=dots[:, i, :, :].rearrange("p e m -> p (e m)"),
                    lhsT=q_of[t][:, c, at : at + P],
                    rhs=key_blocks[block % 2][:, c, :, :].rearrange("p e m -> p (e m)"),
                    start=True,
                    stop=True,
                )
            heads = slice(half * HEADS_PER_BANK, (half + 1) * HEADS_PER_BANK)
            nc.vector.tensor_copy(
                out=staged_of[block][:, :, heads], in_=dots[:].rearrange("p c e m -> p m (c e)")
            )

        def write_block(block):
            staged = staged_of[block][:].rearrange("p m h -> p (m h)")
            nc.sync.dma_start(out=scratch_rows(block)[:, ROW // 2 : ROW], in_=staged[0:KEYS, :])

        def write_next(block):
            staged = staged_of[block][:].rearrange("p m h -> p (m h)")
            nc.sync.dma_start(out=scratch_rows(block + 1)[:, 0 : ROW // 2], in_=staged[KEYS:P, :])

        def read_block(block):
            t, odd = divmod(block, 2)
            if odd == 0:
                near_of[t] = work.tile([P, NEAR_MAX + 1, HEADS], F32, name="near", bufs=1)
            near = near_of[t][:].rearrange("p o h -> p (o h)")
            step = ROW + HEADS
            wanted = (NEAR_MAX + 1) * HEADS
            flat = scratch(block).rearrange("n f -> (n f)")
            for first, count in ((0, 48), (48, 15)):
                nc.sync.dma_start(
                    out=near[odd * KEYS + first : odd * KEYS + first + count, :],
                    in_=flat[first * step : (first + count) * step].rearrange("(r w) -> r w", w=step)[:, 0:wanted],
                )
            nc.sync.dma_start(
                out=near[odd * KEYS + KEYS - 1 : odd * KEYS + KEYS, :],
                in_=flat[(KEYS - 1) * step : (KEYS - 1) * step + wanted].unsqueeze(0),
            )

        gathered = set()

        def gather_near(t):
            if t in gathered:
                return
            gathered.add(t)
            open_dots(t)
            for first, count, step in NEAR_RUNS:
                at = NEAR_MAX - OFFSETS[first]
                nc.scalar.copy(
                    out=dots_of[t][:, first : first + count, :],
                    in_=near_of[t][:, at : at + (count - 1) * step + 1 : step, :],
                )

        def open_dots(t):
            if t in dots_of:
                return
            dots_of[t] = taps.tile([P, SLOTS, HEADS], F32, name="dots", bufs=LEAD)
            unused = slots_of(t)[0]
            if unused > 0:
                nc.gpsimd.memset(dots_of[t][:, 0:unused, :], 0.0)

        prod_of = {}

        def far_dot(t, slot):
            open_dots(t)
            first = PAD + t * P - OFFSETS[slot]
            missing = max(0, -first)
            prod = work.tile([P, CHUNKS, P], F32, name="prod", bufs=3)
            if missing:
                nc.gpsimd.memset(prod[:, :, 0:missing], 0.0)
            nc.gpsimd.tensor_tensor(
                out=prod[:, :, missing:P],
                in0=q_of[t][:, :, KEYS + missing : KEYS + P],
                in1=k_all[:, :, first + missing : first + P],
                op=ALU.mult,
            )
            prod_of[t, slot] = prod

        def fold_dot(t, slot):
            prod = prod_of[t, slot]
            for half in range(HALVES):
                by_token = bank("by_token", [P, PER_BANK, P])
                for i in range(PER_BANK):
                    nc.tensor.transpose(out=by_token[:, i, :], in_=prod[:, half * PER_BANK + i, :], identity=ident[:])
                nc.vector.tensor_reduce(
                    out=dots_of[t][:, slot, half * HEADS_PER_BANK : (half + 1) * HEADS_PER_BANK],
                    in_=by_token[:].rearrange("p c (e d) -> p (c e) d", d=HEAD_DIM),
                    axis=AXIS.X,
                    op=ALU.add,
                )

        def scale_gains(t):
            by_scale = gains_raw[:].rearrange("p (h t) s -> p t s h", t=TILES)[:, t]
            gain = taps.tile([P, ENTRIES, HEADS], F32, name="gain")
            for first, count, s0, tau in ENTRY_RUNS:
                nc.scalar.mul(out=gain[:, first : first + count, :], in_=by_scale[:, s0 : s0 + count, :], mul=abs(D4[tau]))
            nc.scalar.copy(out=gain[:, LOCAL, :], in_=bypass[:])
            gain_of[t] = gain

        def score_entries(t):
            dots = dots_of[t]
            u = taps.tile([P, ENTRIES, HEADS], F32, name="u")
            nc.gpsimd.tensor_tensor(
                out=u[:, 0:HERE, :],
                in0=dots[:, HERE_SLOT : HERE_SLOT + 1, :].to_broadcast([P, HERE, HEADS]),
                in1=tap_bias[:, 0:HERE, :],
                op=ALU.add,
            )
            nc.gpsimd.tensor_tensor(
                out=u[:, HERE:ODD_FIRST, :].rearrange("p (c e) h -> p c e h", c=2),
                in0=dots[:, 0 : 2 * EVEN : 2, :].unsqueeze(1).to_broadcast([P, 2, EVEN, HEADS]),
                in1=tap_bias[:, HERE:ODD_FIRST, :].rearrange("p (c e) h -> p c e h", c=2),
                op=ALU.add,
            )
            nc.gpsimd.tensor_tensor(
                out=u[:, ODD_FIRST:ENTRIES, :],
                in0=dots[:, 1 : 2 * EVEN : 2, :],
                in1=tap_bias[:, ODD_FIRST:ENTRIES, :],
                op=ALU.add,
            )
            decay = taps.tile([P, ENTRIES, HEADS], F32, name="decay")
            nc.scalar.activation(out=decay[:], in_=u[:], func=ACT.Relu, scale=-1.0)
            nc.scalar.activation(out=decay[:], in_=decay[:], func=ACT.Exp, scale=-1.0)
            score_of[t] = (u, decay)

        def weigh_entries(t):
            u, decay = score_of[t]
            nc.vector.scalar_tensor_tensor(out=decay[:], in0=u[:], scalar=0.0, in1=decay[:], op0=ALU.max, op1=ALU.add)
            term = decay
            nc.vector.tensor_tensor(out=term[:], in0=decay[:], in1=gain_of[t][:], op=ALU.mult)
            weight = taps.tile([P, SLOTS, HEADS], F32, name="weight", bufs=2)
            nc.vector.tensor_reduce(
                out=weight[:, HERE_SLOT, :], in_=term[:, 0:HERE, :].rearrange("p e h -> p h e"), axis=AXIS.X, op=ALU.add
            )
            nc.vector.tensor_reduce(
                out=weight[:, 0 : 2 * EVEN : 2, :],
                in_=term[:, HERE:ODD_FIRST, :].rearrange("p (c e) h -> p e h c", c=2),
                axis=AXIS.X,
                op=ALU.add,
            )
            z = taps.tile([P, HEADS], F32, name="z")
            nc.vector.tensor_reduce(out=z[:], in_=term[:].rearrange("p e h -> p h e"), axis=AXIS.X, op=ALU.add)
            nc.scalar.mul(out=weight[:, 1 : 2 * EVEN - 1 : 2, :], in_=term[:, ODD_FIRST:LAST, :], mul=-1.0)
            nc.scalar.copy(out=weight[:, 2 * EVEN - 1, :], in_=term[:, LAST, :])
            z_safe = taps.tile([P, HEADS], F32, name="z_safe")
            nc.scalar.activation(out=z_safe[:], in_=z[:], func=ACT.Identity, bias=1e-6)
            inv_z = taps.tile([P, HEADS], F32, name="inv_z", bufs=2)
            nc.vector.reciprocal(out=inv_z[:], in_=z_safe[:])
            inv_z_of[t] = inv_z
            weight_of[t] = weight

        def show_weights(t):
            count = vector_slots(t)
            weight_ps = psum.tile([P, MAX_VECTOR_SLOTS, HEADS], F32, name="weight_ps")
            nc.tensor.matmul(
                out=weight_ps[:, 0:count, :].rearrange("p s h -> p (s h)"),
                lhsT=ident[:],
                rhs=weight_of[t][:, SLOTS - count : SLOTS, :].rearrange("p s h -> p (s h)"),
                start=True,
                stop=True,
            )
            weight_ps_of[t] = weight_ps

        def order_of(t):
            used = slots_of(t)
            theirs = [s for s in used if s < SLOTS - vector_slots(t)]
            own = [s for s in used if s >= SLOTS - vector_slots(t)]
            merged = [((n + 0.5) / len(part), s) for part in (theirs, own) for n, s in enumerate(part)]
            return [s for at, s in sorted(merged)]

        scaled_of = {}

        def multiply_w_v(t, slot):
            offset = OFFSETS[slot]
            if offset % P == 0:
                shifted = v_of[t - offset // P]
            else:
                first = t * P - offset
                missing = max(0, -first)
                shifted = work.tile([P, WIDTH], F32, name="shifted", bufs=SHIFTED_BUFS)
                if missing:
                    nc.gpsimd.memset(shifted[0:missing, :], 0.0)
                split = P - (P - missing) % DMA_ENGINES
                for low, high in ((missing, split), (split, P)):
                    if low < high:
                        nc.sync.dma_start(out=shifted[low:high, :], in_=out_rows[first + low : first + high, :])
            scaled = work.tile([P, WIDTH], F32, name="scaled", bufs=SCALED_BUFS)
            if slot >= SLOTS - vector_slots(t):
                nc.vector.tensor_tensor(
                    out=scaled[:].rearrange("p (h d) -> p h d", h=HEADS),
                    in0=shifted[:].rearrange("p (h d) -> p h d", h=HEADS),
                    in1=weight_ps_of[t][:, slot - (SLOTS - vector_slots(t)), :].unsqueeze(2).to_broadcast([P, HEADS, HEAD_DIM]),
                    op=ALU.mult,
                )
            else:
                for h in range(HEADS):
                    features = slice(h * HEAD_DIM, (h + 1) * HEAD_DIM)
                    nc.scalar.activation(
                        out=scaled[:, features],
                        in_=shifted[:, features],
                        func=ACT.Copy,
                        scale=weight_of[t][:, slot, h : h + 1],
                    )
            scaled_of[t, slot] = scaled

        def add_product(t, slot, is_first, is_last):
            if is_first:
                sum_of[t] = [psum.tile([P, PER_BANK, P], F32, name="sum_ps", tag="sum", bufs=3) for b in range(HALVES)]
            scaled = scaled_of[t, slot]
            for c in range(CHUNKS):
                nc.tensor.matmul(
                    out=sum_of[t][c // PER_BANK][:, c % PER_BANK, :],
                    lhsT=scaled[:, c * P : (c + 1) * P],
                    rhs=ident[:],
                    is_transpose=True,
                    start=(is_first and c % PER_BANK == 0),
                    stop=(is_last and c % PER_BANK == PER_BANK - 1),
                )

        sum_sb_of = {}

        def copy_sums(t):
            sum_flat = work.tile([P, WIDTH], F32, name="sum_sb", tag="scaled", bufs=SCALED_BUFS)
            sum_sb = sum_flat[:].rearrange("p (c n) -> p c n", c=CHUNKS)
            nc.scalar.copy(out=sum_sb[:, 0:PER_BANK, :], in_=sum_of[t][0][:])
            nc.vector.tensor_copy(out=sum_sb[:, PER_BANK:CHUNKS, :], in_=sum_of[t][1][:])
            sum_sb_of[t] = sum_sb

        def turn_sums(t):
            sum_sb = sum_sb_of[t]
            rows = work.tile([P, HEADS, HEAD_DIM], F32, name="rows", bufs=3)
            for b in range(HALVES):
                rows_ps = bank("rows_ps", [P, PER_BANK, P])
                for i in range(PER_BANK):
                    nc.tensor.transpose(out=rows_ps[:, i, :], in_=sum_sb[:, b * PER_BANK + i, :], identity=ident[:])
                heads = slice(b * HEADS_PER_BANK, (b + 1) * HEADS_PER_BANK)
                nc.vector.tensor_tensor(
                    out=rows[:, heads, :],
                    in0=rows_ps[:].rearrange("p c (e d) -> p (c e) d", d=HEAD_DIM),
                    in1=inv_z_of[t][:, heads].unsqueeze(2).to_broadcast([P, HEADS_PER_BANK, HEAD_DIM]),
                    op=ALU.mult,
                )
            rows_of[t] = rows

        def store(t):
            nc.sync.dma_start(
                out=out_rows[t * P : (t + 1) * P, :], in_=rows_of[t][:].rearrange("p h d -> p (h d)")
            )

        def dot_tasks(t):
            tasks = [lambda s=s: far_dot(t, s) for s in slots_of(t) if s < FAR_SLOTS]
            return tasks

        def projection_tasks(t):
            runs = [[lambda: open_q(t)]]
            if t + 1 < TILES:
                runs[0].append(lambda: load_x(t + 1))

            def project(f):
                for half in range(HALVES):
                    runs.append([lambda half=half: f(t, half)])

            def multiply(block):
                for half in range(HALVES):
                    runs.append([lambda half=half: multiply_block(block, half)])
                runs[-1].append(lambda: write_block(block))
                if block % 2 == 1:
                    runs[-1].append(lambda: read_block(block - 1))
                    runs[-1].append(lambda: read_block(block))
                if block + 1 < BLOCKS:
                    runs[-1].append(lambda: write_next(block))

            if t < TILES:
                project(project_q)
            if t > 0:
                multiply(2 * t - 1)
            if t < TILES:
                project(project_k)
                multiply(2 * t)
            if t + 1 < TILES:
                runs[-1].append(lambda: quantise_x(t + 1))
            if t >= 2:
                runs[2].append(lambda: gather_near(t - 2))
            runs[1] = runs[0] + runs[1]
            return [lambda run=run: [task() for task in run] for run in runs[1:]]

        projection = [(t, task) for t in range(TILES + 1) for task in projection_tasks(t)]
        far_dots = [(t, slot) for t in range(TILES) for slot in slots_of(t) if slot < FAR_SLOTS]
        issued = {"runs": 0, "dots": 0, "folds": 0}

        def next_tile(tasks, name):
            return tasks[issued[name]][0] if issued[name] < len(tasks) else TILES + 1

        def issue_run():
            if issued["runs"] < len(projection):
                issued["runs"] += 1
                projection[issued["runs"] - 1][1]()

        def issue_fold():
            issued["folds"] += 1
            fold_dot(*far_dots[issued["folds"] - 1])

        def issue_dot():
            if next_tile(far_dots, "dots") < min(next_tile(projection, "runs"), TILES):
                issued["dots"] += 1
                far_dot(*far_dots[issued["dots"] - 1])
            if issued["folds"] < issued["dots"] - 1:
                issue_fold()

        def prepare_output(t):
            needed = t + 1 if t < unit_of(BLOCKS - 2) else TILES
            while next_tile(projection, "runs") <= needed:
                issue_run()
            while next_tile(far_dots, "dots") <= t:
                issue_dot()
            while next_tile(far_dots, "folds") <= t:
                issue_fold()
            gather_near(t)
            scale_gains(t)
            score_entries(t)
            weigh_entries(t)
            project_v(t)

        load_x(0)
        load_weight()
        load_biases()
        for part in range(2):
            quarter = slice(part * ROW // 4, (part + 1) * ROW // 4)
            nc.sync.dma_start(
                out=scratch_rows(0)[:, quarter].rearrange("r (c n) -> r c n", n=PAD), in_=k_all[0:KEYS, :, 0:PAD]
            )
        quantise_x(0)
        while next_tile(projection, "runs") == 0:
            issue_run()
        load_tables()
        prepare_output(0)
        owed = {"runs": 0.0, "dots": 0.0}
        products = [(t, n) for t in range(TILES) for n in range(len(slots_of(t)))]
        for beat in range(len(products) + SUM_LAG + TURN_LAG):
            if beat < len(products):
                t, n = products[beat]
                order = order_of(t)
                if n == 0:
                    show_weights(t)
                multiply_w_v(t, order[n])
                if n == 2 * len(order) // 3 and t + 1 < TILES:
                    prepare_output(t + 1)
                owed["runs"] += RUNS_PER_PRODUCT
                owed["dots"] += DOTS_PER_PRODUCT
            if 0 <= beat - SUM_LAG < len(products):
                t, n = products[beat - SUM_LAG]
                order = order_of(t)
                add_product(t, order[n], n == 0, n == len(order) - 1)
                if n == len(order) - 1:
                    copy_sums(t)
            if 0 <= beat - SUM_LAG - TURN_LAG < len(products):
                t, n = products[beat - SUM_LAG - TURN_LAG]
                if n == len(slots_of(t)) - 1:
                    turn_sums(t)
                    if t >= 2:
                        store(t - 2)
            if owed["runs"] >= 1.0:
                owed["runs"] -= 1.0
                if next_tile(projection, "runs") < products[min(beat, len(products) - 1)][0] + LEAD - 1:
                    issue_run()
            if owed["dots"] >= 1.0:
                owed["dots"] -= 1.0
                issue_dot()
        store(TILES - 2)
        store(TILES - 1)
